import numpy as np
import ml_dtypes


def mxq(x, axis, fmt="e4m3"):
    dtype, down = {"e4m3": (ml_dtypes.float8_e4m3fn, 7), "e5m2": (ml_dtypes.float8_e5m2, 14)}[fmt]
    v = np.moveaxis(np.asarray(x, np.float32).astype(ml_dtypes.bfloat16).astype(np.float64), axis, -1)
    blocks = v.reshape(v.shape[:-1] + (-1, 32))
    amax = np.abs(blocks).max(-1, keepdims=True)
    byte = np.maximum(np.where(amax > 0, np.frexp(amax)[1] - 1 + 127, 0) - down, 1)
    scale = np.exp2(byte - 127.0)
    codes = (blocks / scale).astype(np.float32).astype(dtype).astype(np.float64)
    return np.moveaxis((codes * scale).reshape(v.shape), -1, axis)


WIDE = False


def mx_kscale(k):
    if not WIDE:
        return np.ones(k)
    levels = np.array([10, -10, 5, -5, 0])
    a = np.random.permutation(np.resize(levels, k // 512 * 4)).reshape(k // 512, 4)
    idx = np.arange(k)
    return np.exp2(a[idx // 512, idx % 128 // 32])


BF16 = ml_dtypes.bfloat16


def bf(x):
    return np.asarray(x, np.float32).astype(BF16)


def f64(x):
    return np.asarray(x).astype(np.float64)


B, C, H, W, KS, NCAPS, CCH = 4, 512, 32, 32, 3, 16, 16
STRIDE = 1
PAD = KS // 2
NIT = 3
NC = NCAPS * CCH


def gather_positions(y, k, stride, pad):
    yp = np.pad(y, ((0, 0), (0, 0), (0, 0), (pad, pad), (pad, pad), (0, 0)))
    hh, ww = yp.shape[3], yp.shape[4]
    oh = (hh - k) // stride + 1
    ow = (ww - k) // stride + 1
    tiles = [yp[i, j, :, i:i + stride * (oh - 1) + 1:stride, j:j + stride * (ow - 1) + 1:stride, :]
             for i in range(k) for j in range(k)]
    return np.stack(tiles, 3)


def setup_inputs():
    s = mx_kscale(C)
    g = np.exp2(np.linspace(-1.5, 1.5, KS * KS)).reshape(KS, KS, 1, 1)
    return {"input": bf(np.random.standard_normal((B, C, H, W)) * s[None, :, None, None]),
            "weight": bf(np.random.standard_normal((1, 1, 1, KS, KS, C, NC)) * g / np.sqrt(C) / s[:, None]),
            "bias": bf(np.random.standard_normal((1, 1, 1, KS, KS, 1, NC)) * 0.2)}


def reference(input, weight, bias):
    x = f64(input)
    nb, c, h, wd = x.shape
    n = weight.shape[-1]
    xq = mxq(x.transpose(0, 2, 3, 1).reshape(nb * h * wd, c), 1, "e4m3")
    wq = mxq(f64(weight).reshape(KS * KS, c, n), 1, "e4m3")
    b = f64(bias).reshape(KS * KS, n)
    prod = xq @ wq
    priors = gather_positions(prod.reshape(KS, KS, nb, h, wd, n), KS, STRIDE, PAD) + b
    oh, ow = priors.shape[1], priors.shape[2]
    priors = priors.reshape(nb, oh, ow, KS * KS, NCAPS, CCH)
    outputs = priors.mean(3, keepdims=True)
    for _ in range(NIT):
        d = outputs - priors
        cw = 1.0 / np.sqrt(np.sum(d * d, axis=-1, keepdims=True) + 1e-4)
        cw = cw / np.sum(cw, axis=3, keepdims=True)
        outputs = np.sum(priors * cw, axis=3, keepdims=True)
    out = outputs.reshape(nb, oh, ow, NCAPS * CCH)
    return np.transpose(out, (0, 3, 1, 2))

@@ -1,0 +1,288 @@
+from contextlib import ExitStack
+
+import concourse.mybir as mybir
+from concourse.masks import make_identity
+
+F32 = mybir.dt.float32
+BF16 = mybir.dt.bfloat16
+U32 = mybir.dt.uint32
+U8 = mybir.dt.uint8
+I32 = mybir.dt.int32
+FP8X4 = mybir.dt.float8_e4m3fn_x4
+ALU = mybir.AluOpType
+ACT = mybir.ActivationFunctionType
+AXIS_X = mybir.AxisListType.X
+
+P = 128
+PACK = 4
+IMAGES = 4
+ROWS = 32
+COLS = 32
+PIXELS = ROWS * COLS
+KS = 3
+TAPS = KS * KS
+FEATURES = 256
+CAPS = 16
+CAP_CH = 16
+HALVES = FEATURES // P
+HALF_CAPS = CAPS // HALVES
+ROUTING_ITERATIONS = 3
+EPS = 1e-4
+CHUNK = 512
+CHUNK_ROWS = CHUNK // COLS
+CHUNKS_PER_IMAGE = PIXELS // CHUNK
+N_CHUNKS = IMAGES * CHUNKS_PER_IMAGE
+BLOCK_ROWS = P // COLS
+BLOCKS_PER_CHUNK = CHUNK // P
+QUAD = 4
+
+FLOPS = 2 * IMAGES * PIXELS * 512 * TAPS * FEATURES
+
+
+def tile_capsulelayer_t_kernel(tc, image, weight, bias, out):
+    nc = tc.nc
+    with ExitStack() as ctx:
+        consts = ctx.enter_context(tc.tile_pool(name="consts", bufs=1))
+        stage = ctx.enter_context(tc.tile_pool(name="stage", bufs=2))
+        chunk_pool = ctx.enter_context(tc.tile_pool(name="chunk", bufs=2))
+        route_pool = ctx.enter_context(tc.tile_pool(name="route", bufs=2))
+        small = ctx.enter_context(tc.tile_pool(name="small", bufs=3))
+        transit = ctx.enter_context(tc.psum_pool(name="transit", bufs=3))
+        pri_pool = ctx.enter_context(tc.psum_pool(name="pri", bufs=1))
+
+        ident = consts.tile([P, P], F32)
+        make_identity(nc, ident[:])
+
+        x_grouped = [consts.tile([P, ROWS, COLS, PACK], BF16, name="x_grouped%d" % j, align_bytes=64) for j in range(KS)]
+        x_codes = [consts.tile([P, COLS + PIXELS + COLS], U32, name="x_codes%d" % j, align_bytes=64) for j in range(KS)]
+        x_centre = [consts.tile([P, PIXELS], U8, name="x_centre%d" % j, align_bytes=64) for j in range(KS)]
+        x_offset = [consts.tile([P, COLS + PIXELS + COLS], U8, name="x_offset%d" % j, align_bytes=64) for j in range(KS)]
+        for j in range(KS):
+            nc.vector.memset(x_codes[j][:, 0:COLS].bitcast(I32), 0)
+            nc.vector.memset(x_codes[j][:, COLS + PIXELS :].bitcast(I32), 0)
+            nc.vector.memset(x_centre[j][:].bitcast(I32), 0)
+            nc.vector.memset(x_offset[j][:].bitcast(I32), 0)
+        nc.vector.memset(x_grouped[0][:, :, 0:4, :], 0.0)
+        nc.vector.memset(x_grouped[2][:, :, COLS - 4 : COLS, :], 0.0)
+
+        def load_image(b):
+            x_raw = stage.tile([P, PACK, ROWS, COLS], BF16)
+            nc.sync.dma_start(out=x_raw[:], in_=image[b].rearrange("(p r) h w -> p r h w", r=PACK))
+            return x_raw
+
+        def regroup_image(x_raw, j, on_vector):
+            shift = j - 1
+            lo = max(0, -shift)
+            hi = COLS - max(0, shift)
+            dst = x_grouped[j][:, :, lo:hi, :]
+            src = x_raw[:, :, :, lo + shift : hi + shift].rearrange("p r h w -> p h w r")
+            if on_vector:
+                nc.vector.tensor_copy(out=dst, in_=src)
+            else:
+                nc.scalar.copy(out=dst, in_=src)
+
+        def quantise_image(j):
+            nc.vector.quantize_mx(
+                out=x_codes[j][:, COLS : COLS + PIXELS].bitcast(FP8X4),
+                scales=x_centre[j][:],
+                in_=x_grouped[j][:].rearrange("p h w r -> p (h w r)"),
+            )
+            nc.vector.tensor_copy(
+                out=x_offset[j][:, COLS : COLS + PIXELS].bitcast(I32), in_=x_centre[j][:].bitcast(I32)
+            )
+
+        def x_window(first_row, t, width):
+            i, j = divmod(t, KS)
+            start = COLS * (first_row + i)
+            codes = x_codes[j][:, start : start + width].bitcast(FP8X4)
+            if i == 1:
+                scales = x_centre[j][:, start - COLS : start - COLS + width]
+            else:
+                scales = x_offset[j][:, start : start + width]
+            return codes, scales
+
+        x_raw_first = load_image(0)
+        w_rows = weight.rearrange("a b c i j (p r) n -> p (a b c i j) r n", r=PACK)
+        w_codes = consts.tile([P, TAPS, FEATURES], U32, align_bytes=64)
+        w_scales = consts.tile([P, TAPS, FEATURES], U8, align_bytes=64)
+        w_raws = []
+        for i in range(KS):
+            w_raw = stage.tile([P, KS, PACK, FEATURES], BF16, bufs=KS)
+            nc.sync.dma_start(out=w_raw[:], in_=w_rows[:, KS * i : KS * (i + 1), :, :])
+            w_raws.append(w_raw)
+
+        bias_cols_bf = consts.tile([P, TAPS * HALVES], BF16)
+        with nc.allow_non_contiguous_dma(reason="2304 bias values, one to a partition, once"):
+            nc.sync.dma_start(
+                out=bias_cols_bf[:], in_=bias.rearrange("a b c i j o (g f) -> f (a b c i j o g)", g=HALVES)
+            )
+        bias_cols = consts.tile([P, TAPS * HALVES], F32)
+        nc.vector.tensor_copy(out=bias_cols[:], in_=bias_cols_bf[:])
+        mean_cols = consts.tile([P, HALVES], F32)
+        nc.vector.tensor_reduce(
+            out=mean_cols[:], in_=bias_cols[:].rearrange("p (t g) -> p g t", g=HALVES), axis=AXIS_X, op=ALU.add
+        )
+        nc.vector.tensor_scalar_mul(out=mean_cols[:], in0=mean_cols[:], scalar1=1.0 / TAPS)
+        mean_ps = transit.tile([P, HALVES, P], F32, tag="transit")
+        for g in range(HALVES):
+            nc.tensor.transpose(mean_ps[:, g, :], mean_cols[:, g : g + 1].to_broadcast([P, P]), ident[:])
+        mean_bias = consts.tile([P, FEATURES], F32)
+        nc.vector.tensor_copy(out=mean_bias[:].rearrange("p (g f) -> p g f", g=HALVES), in_=mean_ps[:])
+
+        for j in range(KS):
+            regroup_image(x_raw_first, j, True)
+        for t in range(TAPS):
+            w_grouped = stage.tile([P, FEATURES, PACK], BF16, align_bytes=64, bufs=3)
+            nc.scalar.copy(out=w_grouped[:], in_=w_raws[t // KS][:, t % KS, :, :].rearrange("p r n -> p n r"))
+            nc.vector.quantize_mx(
+                out=w_codes[:, t, :].bitcast(FP8X4),
+                scales=w_scales[:, t, :],
+                in_=w_grouped[:].rearrange("p n r -> p (n r)"),
+            )
+        for j in range(KS):
+            quantise_image(j)
+
+        chunk_tiles = {}
+
+        def produce(c, part):
+            first_row = CHUNK_ROWS * (c % CHUNKS_PER_IMAGE)
+            if part == 0:
+                pri_a = chunk_pool.tile([P, HALVES, TAPS, CHUNK], F32)
+                o_first = chunk_pool.tile([P, BLOCKS_PER_CHUNK, FEATURES], F32)
+                chunk_tiles[c] = (pri_a, o_first)
+            pri_a, o_first = chunk_tiles[c]
+            for k in range(part, HALVES * TAPS, BLOCKS_PER_CHUNK):
+                t, half = divmod(k, HALVES)
+                feats = slice(half * P, (half + 1) * P)
+                codes, scales = x_window(first_row, t, CHUNK)
+                acc = transit.tile([P, CHUNK], F32, tag="transit")
+                nc.tensor.matmul_mx(
+                    out=acc[:],
+                    lhsT=w_codes[:, t, feats].bitcast(FP8X4),
+                    lhsT_scale=w_scales[:, t, feats],
+                    rhs=codes,
+                    rhs_scale=scales,
+                    start=True,
+                    stop=True,
+                )
+                nc.scalar.activation(
+                    out=pri_a[:, half, t, :], in_=acc[:], func=ACT.Identity, bias=bias_cols[:, k : k + 1]
+                )
+            mean_acc = transit.tile([P, FEATURES], F32, tag="transit")
+            for t in range(TAPS):
+                codes, scales = x_window(first_row + BLOCK_ROWS * part, t, P)
+                nc.tensor.matmul_mx(
+                    out=mean_acc[:],
+                    lhsT=codes,
+                    lhsT_scale=scales,
+                    rhs=w_codes[:, t, :].bitcast(FP8X4),
+                    rhs_scale=w_scales[:, t, :],
+                    start=(t == 0),
+                    stop=(t == TAPS - 1),
+                )
+            nc.vector.scalar_tensor_tensor(
+                out=o_first[:, part, :], in0=mean_acc[:], scalar=1.0 / TAPS, in1=mean_bias[:], op0=ALU.mult, op1=ALU.add
+            )
+
+        def route(c, blk, out_sb):
+            pri_a, o_first = chunk_tiles[c]
+            pixels = slice(blk * P, (blk + 1) * P)
+            quads = [
+                [pri_pool.tile([P, QUAD, P], F32, name="pri_h%d_q%d" % (h, q), tag="pri_h%d_q%d" % (h, q)) for q in range(2)]
+                for h in range(HALVES)
+            ]
+            last = pri_pool.tile([P, HALVES, P], F32, name="pri_last", tag="pri_last")
+            pieces = []
+            for h in range(HALVES):
+                for t in range(TAPS):
+                    dst = quads[h][t // QUAD][:, t % QUAD, :] if t < 2 * QUAD else last[:, h, :]
+                    nc.tensor.transpose(dst, pri_a[:, h, t, pixels], ident[:])
+                pieces.append(
+                    [
+                        (quads[h][0][:], 0, QUAD),
+                        (quads[h][1][:], QUAD, QUAD),
+                        (last[:, h : h + 1, :], 2 * QUAD, 1),
+                    ]
+                )
+
+            work = route_pool.tile([P, TAPS, FEATURES], F32)
+            o = o_first[:, blk, :]
+            for it in range(ROUTING_ITERATIONS):
+                dist = small.tile([P, TAPS, CAPS], F32)
+                cw = small.tile([P, TAPS, CAPS], F32)
+                for h in range(HALVES):
+                    feats = slice(h * P, (h + 1) * P)
+                    for pri, tap0, n in pieces[h]:
+                        taps = slice(tap0, tap0 + n)
+                        nc.vector.tensor_tensor(
+                            out=work[:, taps, feats],
+                            in0=pri,
+                            in1=o[:, feats].unsqueeze(1).to_broadcast([P, n, P]),
+                            op=ALU.subtract,
+                        )
+                        nc.scalar.activation(out=work[:, taps, feats], in_=work[:, taps, feats], func=ACT.Square)
+                for h in range(HALVES):
+                    feats = slice(h * P, (h + 1) * P)
+                    caps = slice(h * HALF_CAPS, (h + 1) * HALF_CAPS)
+                    nc.vector.tensor_reduce(
+                        out=dist[:, :, caps],
+                        in_=work[:, :, feats].rearrange("p t (c k) -> p t c k", k=CAP_CH),
+                        axis=AXIS_X,
+                        op=ALU.add,
+                    )
+                    nc.scalar.activation(out=cw[:, :, caps], in_=dist[:, :, caps], func=ACT.Abs_reciprocal_sqrt, bias=EPS)
+                for h in range(HALVES):
+                    feats = slice(h * P, (h + 1) * P)
+                    caps = slice(h * HALF_CAPS, (h + 1) * HALF_CAPS)
+                    for pri, tap0, n in pieces[h]:
+                        taps = slice(tap0, tap0 + n)
+                        nc.vector.tensor_tensor(
+                            out=work[:, taps, feats].rearrange("p t (c k) -> p t c k", k=CAP_CH),
+                            in0=pri.rearrange("p t (c k) -> p t c k", k=CAP_CH),
+                            in1=cw[:, taps, caps].unsqueeze(3).to_broadcast([P, n, HALF_CAPS, CAP_CH]),
+                            op=ALU.mult,
+                        )
+                cw_sum = small.tile([P, CAPS], F32)
+                nc.vector.tensor_reduce(out=cw_sum[:], in_=cw[:].rearrange("p t c -> p c t"), axis=AXIS_X, op=ALU.add)
+                cw_norm = small.tile([P, CAPS], F32)
+                nc.vector.reciprocal(out=cw_norm[:], in_=cw_sum[:])
+                nc.vector.tensor_tensor(out=work[:, 0:4, :], in0=work[:, 0:4, :], in1=work[:, 4:8, :], op=ALU.add)
+                nc.vector.tensor_tensor(out=work[:, 0:2, :], in0=work[:, 0:2, :], in1=work[:, 2:4, :], op=ALU.add)
+                nc.vector.tensor_tensor(out=work[:, 0, :], in0=work[:, 0, :], in1=work[:, 1, :], op=ALU.add)
+                nc.vector.tensor_tensor(out=work[:, 0, :], in0=work[:, 0, :], in1=work[:, 8, :], op=ALU.add)
+                o_next = small.tile([P, FEATURES], F32)
+                nc.vector.tensor_tensor(
+                    out=o_next[:].rearrange("p (c k) -> p c k", k=CAP_CH),
+                    in0=work[:, 0, :].rearrange("p (c k) -> p c k", k=CAP_CH),
+                    in1=cw_norm[:].unsqueeze(2).to_broadcast([P, CAPS, CAP_CH]),
+                    op=ALU.mult,
+                )
+                o = o_next[:]
+
+            out_ps = transit.tile([P, HALVES, P], F32, tag="transit")
+            for h in range(HALVES):
+                nc.tensor.transpose(out_ps[:, h, :], o[:, h * P : (h + 1) * P], ident[:])
+            nc.scalar.copy(out=out_sb[:, :, pixels], in_=out_ps[:])
+
+        for part in range(BLOCKS_PER_CHUNK):
+            produce(0, part)
+        x_raw_next = None
+        for c in range(N_CHUNKS):
+            b, ph = divmod(c, CHUNKS_PER_IMAGE)
+            out_sb = chunk_pool.tile([P, HALVES, CHUNK], F32)
+            for blk in range(BLOCKS_PER_CHUNK):
+                if ph == 0 and b + 1 < IMAGES:
+                    if blk == 0:
+                        x_raw_next = load_image(b + 1)
+                    if blk < KS:
+                        regroup_image(x_raw_next, blk, False)
+                if c + 1 < N_CHUNKS:
+                    if ph == CHUNKS_PER_IMAGE - 1 and blk == 0:
+                        for j in range(KS):
+                            quantise_image(j)
+                    produce(c + 1, blk)
+                route(c, blk, out_sb)
+            nc.sync.dma_start(
+                out=out[b].rearrange("(g f) h w -> f g (h w)", g=HALVES)[:, :, ph * CHUNK : (ph + 1) * CHUNK],
+                in_=out_sb[:],
+            )

@@ -22,19 +22,25 @@ PIXELS = ROWS * COLS
 KS = 3
 TAPS = KS * KS
 FEATURES = 256
-CAPS = 16
 CAP_CH = 16
 HALVES = FEATURES // P
-HALF_CAPS = CAPS // HALVES
-ROUTING_ITERATIONS = 3
+HALF_CAPS = P // CAP_CH
+ITERATIONS = 3
 EPS = 1e-4
-CHUNK = 512
-CHUNK_ROWS = CHUNK // COLS
-CHUNKS_PER_IMAGE = PIXELS // CHUNK
-N_CHUNKS = IMAGES * CHUNKS_PER_IMAGE
 BLOCK_ROWS = P // COLS
-BLOCKS_PER_CHUNK = CHUNK // P
+BLOCKS_PER_IMAGE = PIXELS // P
+N_BLOCKS = IMAGES * BLOCKS_PER_IMAGE
 QUAD = 4
+N_CHAINS = N_BLOCKS * HALVES
+LIVE = 3
+N_ITEMS = -(-N_CHAINS // LIVE) * LIVE * ITERATIONS
+PASSES = TAPS * HALVES
+PASSES_PER_TICK = 3
+TICKS_PER_BLOCK = PASSES // PASSES_PER_TICK
+TICKS_PER_IMAGE = TICKS_PER_BLOCK * BLOCKS_PER_IMAGE
+AHEAD = 2 * TICKS_PER_BLOCK
+REGROUP_ROWS = 4
+SLICES = KS * ROWS // REGROUP_ROWS
 
 FLOPS = 2 * IMAGES * PIXELS * 512 * TAPS * FEATURES
 
@@ -42,12 +48,13 @@ FLOPS = 2 * IMAGES * PIXELS * 512 * TAPS * FEATURES
 def tile_capsulelayer_t_kernel(tc, image, weight, bias, out):
     nc = tc.nc
     with ExitStack() as ctx:
+        ctx.enter_context(tc.manual_schedule())
         consts = ctx.enter_context(tc.tile_pool(name="consts", bufs=1))
         stage = ctx.enter_context(tc.tile_pool(name="stage", bufs=2))
-        chunk_pool = ctx.enter_context(tc.tile_pool(name="chunk", bufs=2))
-        route_pool = ctx.enter_context(tc.tile_pool(name="route", bufs=2))
-        small = ctx.enter_context(tc.tile_pool(name="small", bufs=3))
-        transit = ctx.enter_context(tc.psum_pool(name="transit", bufs=3))
+        block_pool = ctx.enter_context(tc.tile_pool(name="block", bufs=3))
+        chain_pool = ctx.enter_context(tc.tile_pool(name="chain", bufs=LIVE + 1))
+        item_pool = ctx.enter_context(tc.tile_pool(name="item", bufs=LIVE + 1))
+        transit = ctx.enter_context(tc.psum_pool(name="transit", bufs=1))
         pri_pool = ctx.enter_context(tc.psum_pool(name="pri", bufs=1))
 
         ident = consts.tile([P, P], F32)
@@ -70,38 +77,37 @@ def tile_capsulelayer_t_kernel(tc, image, weight, bias, out):
             nc.sync.dma_start(out=x_raw[:], in_=image[b].rearrange("(p r) h w -> p r h w", r=PACK))
             return x_raw
 
-        def regroup_image(x_raw, j, on_vector):
+        def regroup_views(x_raw, j, row0, n_rows):
             shift = j - 1
             lo = max(0, -shift)
             hi = COLS - max(0, shift)
-            dst = x_grouped[j][:, :, lo:hi, :]
-            src = x_raw[:, :, :, lo + shift : hi + shift].rearrange("p r h w -> p h w r")
-            if on_vector:
-                nc.vector.tensor_copy(out=dst, in_=src)
-            else:
-                nc.scalar.copy(out=dst, in_=src)
+            dst = x_grouped[j][:, row0 : row0 + n_rows, lo:hi, :]
+            src = x_raw[:, :, row0 : row0 + n_rows, lo + shift : hi + shift].rearrange("p r h w -> p h w r")
+            return dst, src
 
-        def quantise_image(j):
-            nc.vector.quantize_mx(
-                out=x_codes[j][:, COLS : COLS + PIXELS].bitcast(FP8X4),
-                scales=x_centre[j][:],
-                in_=x_grouped[j][:].rearrange("p h w r -> p (h w r)"),
-            )
-            nc.vector.tensor_copy(
-                out=x_offset[j][:, COLS : COLS + PIXELS].bitcast(I32), in_=x_centre[j][:].bitcast(I32)
-            )
+        def quantise_image():
+            for j in range(KS):
+                nc.vector.quantize_mx(
+                    out=x_codes[j][:, COLS : COLS + PIXELS].bitcast(FP8X4),
+                    scales=x_centre[j][:],
+                    in_=x_grouped[j][:].rearrange("p h w r -> p (h w r)"),
+                )
+            for j in range(KS):
+                nc.vector.tensor_copy(
+                    out=x_offset[j][:, COLS : COLS + PIXELS].bitcast(I32), in_=x_centre[j][:].bitcast(I32)
+                )
 
-        def x_window(first_row, t, width):
+        def x_window(first_row, t):
             i, j = divmod(t, KS)
             start = COLS * (first_row + i)
-            codes = x_codes[j][:, start : start + width].bitcast(FP8X4)
+            codes = x_codes[j][:, start : start + P].bitcast(FP8X4)
             if i == 1:
-                scales = x_centre[j][:, start - COLS : start - COLS + width]
+                scales = x_centre[j][:, start - COLS : start - COLS + P]
             else:
-                scales = x_offset[j][:, start : start + width]
+                scales = x_offset[j][:, start : start + P]
             return codes, scales
 
-        x_raw_first = load_image(0)
+        x_raw = load_image(0)
         w_rows = weight.rearrange("a b c i j (p r) n -> p (a b c i j) r n", r=PACK)
         w_codes = consts.tile([P, TAPS, FEATURES], U32, align_bytes=64)
         w_scales = consts.tile([P, TAPS, FEATURES], U8, align_bytes=64)
@@ -110,54 +116,54 @@ def tile_capsulelayer_t_kernel(tc, image, weight, bias, out):
             w_raw = stage.tile([P, KS, PACK, FEATURES], BF16, bufs=KS)
             nc.sync.dma_start(out=w_raw[:], in_=w_rows[:, KS * i : KS * (i + 1), :, :])
             w_raws.append(w_raw)
-
-        bias_cols_bf = consts.tile([P, TAPS * HALVES], BF16)
+        bias_bf = consts.tile([P, PASSES], BF16)
         with nc.allow_non_contiguous_dma(reason="2304 bias values, one to a partition, once"):
-            nc.sync.dma_start(
-                out=bias_cols_bf[:], in_=bias.rearrange("a b c i j o (g f) -> f (a b c i j o g)", g=HALVES)
-            )
-        bias_cols = consts.tile([P, TAPS * HALVES], F32)
-        nc.vector.tensor_copy(out=bias_cols[:], in_=bias_cols_bf[:])
-        mean_cols = consts.tile([P, HALVES], F32)
-        nc.vector.tensor_reduce(
-            out=mean_cols[:], in_=bias_cols[:].rearrange("p (t g) -> p g t", g=HALVES), axis=AXIS_X, op=ALU.add
-        )
-        nc.vector.tensor_scalar_mul(out=mean_cols[:], in0=mean_cols[:], scalar1=1.0 / TAPS)
-        mean_ps = transit.tile([P, HALVES, P], F32, tag="transit")
-        for g in range(HALVES):
-            nc.tensor.transpose(mean_ps[:, g, :], mean_cols[:, g : g + 1].to_broadcast([P, P]), ident[:])
-        mean_bias = consts.tile([P, FEATURES], F32)
-        nc.vector.tensor_copy(out=mean_bias[:].rearrange("p (g f) -> p g f", g=HALVES), in_=mean_ps[:])
+            nc.sync.dma_start(out=bias_bf[:], in_=bias.rearrange("a b c i j o (g f) -> f (a b c i j o g)", g=HALVES))
 
         for j in range(KS):
-            regroup_image(x_raw_first, j, True)
+            dst, src = regroup_views(x_raw, j, 0, ROWS)
+            nc.vector.tensor_copy(out=dst, in_=src)
+        w_groupeds = []
         for t in range(TAPS):
-            w_grouped = stage.tile([P, FEATURES, PACK], BF16, align_bytes=64, bufs=3)
+            w_grouped = stage.tile([P, FEATURES, PACK], BF16, align_bytes=64, bufs=TAPS)
             nc.scalar.copy(out=w_grouped[:], in_=w_raws[t // KS][:, t % KS, :, :].rearrange("p r n -> p n r"))
+            w_groupeds.append(w_grouped)
+        quantise_image()
+        for t in range(TAPS):
             nc.vector.quantize_mx(
                 out=w_codes[:, t, :].bitcast(FP8X4),
                 scales=w_scales[:, t, :],
-                in_=w_grouped[:].rearrange("p n r -> p (n r)"),
+                in_=w_groupeds[t][:].rearrange("p n r -> p (n r)"),
             )
-        for j in range(KS):
-            quantise_image(j)
 
-        chunk_tiles = {}
+        bias_cols = consts.tile([P, TAPS, HALVES], F32)
+        nc.vector.tensor_copy(out=bias_cols[:].rearrange("p t g -> p (t g)"), in_=bias_bf[:])
+        bias_mean = consts.tile([P, HALVES], F32)
+        nc.vector.tensor_reduce(out=bias_mean[:], in_=bias_cols[:].rearrange("p t g -> p g t"), axis=AXIS_X, op=ALU.add)
+        nc.vector.tensor_scalar_mul(out=bias_mean[:], in0=bias_mean[:], scalar1=1.0 / TAPS)
+        bias_rel = consts.tile([P, TAPS, HALVES], F32)
+        nc.vector.tensor_tensor(
+            out=bias_rel[:], in0=bias_cols[:], in1=bias_mean[:].unsqueeze(1).to_broadcast([P, TAPS, HALVES]), op=ALU.subtract
+        )
 
-        def produce(c, part):
-            first_row = CHUNK_ROWS * (c % CHUNKS_PER_IMAGE)
+        blocks = {}
+        banks = {}
+
+        def issue(tick):
+            block, part = divmod(tick, TICKS_PER_BLOCK)
+            first_row = BLOCK_ROWS * (block % BLOCKS_PER_IMAGE)
             if part == 0:
-                pri_a = chunk_pool.tile([P, HALVES, TAPS, CHUNK], F32)
-                o_first = chunk_pool.tile([P, BLOCKS_PER_CHUNK, FEATURES], F32)
-                chunk_tiles[c] = (pri_a, o_first)
-            pri_a, o_first = chunk_tiles[c]
-            for k in range(part, HALVES * TAPS, BLOCKS_PER_CHUNK):
-                t, half = divmod(k, HALVES)
+                pri_a = block_pool.tile([P, PASSES, P], F32)
+                o_first = block_pool.tile([P, FEATURES], F32)
+                blocks[block] = (pri_a, o_first)
+            bank = transit.tile([P, PASSES_PER_TICK + 1, P], F32, tag="transit")
+            banks[tick] = bank
+            for s in range(PASSES_PER_TICK):
+                t, half = divmod(PASSES_PER_TICK * part + s, HALVES)
                 feats = slice(half * P, (half + 1) * P)
-                codes, scales = x_window(first_row, t, CHUNK)
-                acc = transit.tile([P, CHUNK], F32, tag="transit")
+                codes, scales = x_window(first_row, t)
                 nc.tensor.matmul_mx(
-                    out=acc[:],
+                    out=bank[:, s, :],
                     lhsT=w_codes[:, t, feats].bitcast(FP8X4),
                     lhsT_scale=w_scales[:, t, feats],
                     rhs=codes,
@@ -165,124 +171,193 @@ def tile_capsulelayer_t_kernel(tc, image, weight, bias, out):
                     start=True,
                     stop=True,
                 )
-                nc.scalar.activation(
-                    out=pri_a[:, half, t, :], in_=acc[:], func=ACT.Identity, bias=bias_cols[:, k : k + 1]
-                )
-            mean_acc = transit.tile([P, FEATURES], F32, tag="transit")
-            for t in range(TAPS):
-                codes, scales = x_window(first_row + BLOCK_ROWS * part, t, P)
-                nc.tensor.matmul_mx(
-                    out=mean_acc[:],
-                    lhsT=codes,
-                    lhsT_scale=scales,
-                    rhs=w_codes[:, t, :].bitcast(FP8X4),
-                    rhs_scale=w_scales[:, t, :],
-                    start=(t == 0),
-                    stop=(t == TAPS - 1),
-                )
-            nc.vector.scalar_tensor_tensor(
-                out=o_first[:, part, :], in0=mean_acc[:], scalar=1.0 / TAPS, in1=mean_bias[:], op0=ALU.mult, op1=ALU.add
-            )
-
-        def route(c, blk, out_sb):
-            pri_a, o_first = chunk_tiles[c]
-            pixels = slice(blk * P, (blk + 1) * P)
-            quads = [
-                [pri_pool.tile([P, QUAD, P], F32, name="pri_h%d_q%d" % (h, q), tag="pri_h%d_q%d" % (h, q)) for q in range(2)]
-                for h in range(HALVES)
-            ]
-            last = pri_pool.tile([P, HALVES, P], F32, name="pri_last", tag="pri_last")
-            pieces = []
-            for h in range(HALVES):
+            if part < HALVES:
+                feats = slice(part * P, (part + 1) * P)
                 for t in range(TAPS):
-                    dst = quads[h][t // QUAD][:, t % QUAD, :] if t < 2 * QUAD else last[:, h, :]
-                    nc.tensor.transpose(dst, pri_a[:, h, t, pixels], ident[:])
-                pieces.append(
-                    [
-                        (quads[h][0][:], 0, QUAD),
-                        (quads[h][1][:], QUAD, QUAD),
-                        (last[:, h : h + 1, :], 2 * QUAD, 1),
-                    ]
-                )
-
-            work = route_pool.tile([P, TAPS, FEATURES], F32)
-            o = o_first[:, blk, :]
-            for it in range(ROUTING_ITERATIONS):
-                dist = small.tile([P, TAPS, CAPS], F32)
-                cw = small.tile([P, TAPS, CAPS], F32)
-                for h in range(HALVES):
-                    feats = slice(h * P, (h + 1) * P)
-                    for pri, tap0, n in pieces[h]:
-                        taps = slice(tap0, tap0 + n)
-                        nc.vector.tensor_tensor(
-                            out=work[:, taps, feats],
-                            in0=pri,
-                            in1=o[:, feats].unsqueeze(1).to_broadcast([P, n, P]),
-                            op=ALU.subtract,
-                        )
-                        nc.scalar.activation(out=work[:, taps, feats], in_=work[:, taps, feats], func=ACT.Square)
-                for h in range(HALVES):
-                    feats = slice(h * P, (h + 1) * P)
-                    caps = slice(h * HALF_CAPS, (h + 1) * HALF_CAPS)
-                    nc.vector.tensor_reduce(
-                        out=dist[:, :, caps],
-                        in_=work[:, :, feats].rearrange("p t (c k) -> p t c k", k=CAP_CH),
-                        axis=AXIS_X,
-                        op=ALU.add,
+                    codes, scales = x_window(first_row, t)
+                    nc.tensor.matmul_mx(
+                        out=bank[:, PASSES_PER_TICK, :],
+                        lhsT=codes,
+                        lhsT_scale=scales,
+                        rhs=w_codes[:, t, feats].bitcast(FP8X4),
+                        rhs_scale=w_scales[:, t, feats],
+                        start=(t == 0),
+                        stop=(t == TAPS - 1),
                     )
-                    nc.scalar.activation(out=cw[:, :, caps], in_=dist[:, :, caps], func=ACT.Abs_reciprocal_sqrt, bias=EPS)
-                for h in range(HALVES):
-                    feats = slice(h * P, (h + 1) * P)
-                    caps = slice(h * HALF_CAPS, (h + 1) * HALF_CAPS)
-                    for pri, tap0, n in pieces[h]:
-                        taps = slice(tap0, tap0 + n)
-                        nc.vector.tensor_tensor(
-                            out=work[:, taps, feats].rearrange("p t (c k) -> p t c k", k=CAP_CH),
-                            in0=pri.rearrange("p t (c k) -> p t c k", k=CAP_CH),
-                            in1=cw[:, taps, caps].unsqueeze(3).to_broadcast([P, n, HALF_CAPS, CAP_CH]),
-                            op=ALU.mult,
-                        )
-                cw_sum = small.tile([P, CAPS], F32)
-                nc.vector.tensor_reduce(out=cw_sum[:], in_=cw[:].rearrange("p t c -> p c t"), axis=AXIS_X, op=ALU.add)
-                cw_norm = small.tile([P, CAPS], F32)
-                nc.vector.reciprocal(out=cw_norm[:], in_=cw_sum[:])
-                nc.vector.tensor_tensor(out=work[:, 0:4, :], in0=work[:, 0:4, :], in1=work[:, 4:8, :], op=ALU.add)
-                nc.vector.tensor_tensor(out=work[:, 0:2, :], in0=work[:, 0:2, :], in1=work[:, 2:4, :], op=ALU.add)
-                nc.vector.tensor_tensor(out=work[:, 0, :], in0=work[:, 0, :], in1=work[:, 1, :], op=ALU.add)
-                nc.vector.tensor_tensor(out=work[:, 0, :], in0=work[:, 0, :], in1=work[:, 8, :], op=ALU.add)
-                o_next = small.tile([P, FEATURES], F32)
-                nc.vector.tensor_tensor(
-                    out=o_next[:].rearrange("p (c k) -> p c k", k=CAP_CH),
-                    in0=work[:, 0, :].rearrange("p (c k) -> p c k", k=CAP_CH),
-                    in1=cw_norm[:].unsqueeze(2).to_broadcast([P, CAPS, CAP_CH]),
-                    op=ALU.mult,
+
+        def collect(tick):
+            block, part = divmod(tick, TICKS_PER_BLOCK)
+            pri_a, o_first = blocks[block]
+            bank = banks[tick]
+            for s in range(PASSES_PER_TICK):
+                k = PASSES_PER_TICK * part + s
+                t, half = divmod(k, HALVES)
+                nc.scalar.activation(
+                    out=pri_a[:, k, :], in_=bank[:, s, :], func=ACT.Identity, bias=bias_rel[:, t, half : half + 1]
                 )
-                o = o_next[:]
+            if part < HALVES:
+                nc.scalar.mul(out=o_first[:, part * P : (part + 1) * P], in_=bank[:, PASSES_PER_TICK, :], mul=1.0 / TAPS)
 
-            out_ps = transit.tile([P, HALVES, P], F32, tag="transit")
-            for h in range(HALVES):
-                nc.tensor.transpose(out_ps[:, h, :], o[:, h * P : (h + 1) * P], ident[:])
-            nc.scalar.copy(out=out_sb[:, :, pixels], in_=out_ps[:])
+        tap8 = pri_pool.tile([P, LIVE, P], F32, name="tap8", tag="tap8")
+        chains = {}
 
-        for part in range(BLOCKS_PER_CHUNK):
-            produce(0, part)
-        x_raw_next = None
-        for c in range(N_CHUNKS):
-            b, ph = divmod(c, CHUNKS_PER_IMAGE)
-            out_sb = chunk_pool.tile([P, HALVES, CHUNK], F32)
-            for blk in range(BLOCKS_PER_CHUNK):
-                if ph == 0 and b + 1 < IMAGES:
-                    if blk == 0:
-                        x_raw_next = load_image(b + 1)
-                    if blk < KS:
-                        regroup_image(x_raw_next, blk, False)
-                if c + 1 < N_CHUNKS:
-                    if ph == CHUNKS_PER_IMAGE - 1 and blk == 0:
-                        for j in range(KS):
-                            quantise_image(j)
-                    produce(c + 1, blk)
-                route(c, blk, out_sb)
-            nc.sync.dma_start(
-                out=out[b].rearrange("(g f) h w -> f g (h w)", g=HALVES)[:, :, ph * CHUNK : (ph + 1) * CHUNK],
-                in_=out_sb[:],
+        def item(n):
+            group, rest = divmod(n, LIVE * ITERATIONS)
+            it, member = divmod(rest, LIVE)
+            chain = LIVE * group + member
+            if n < 0 or chain >= N_CHAINS:
+                return None
+            return chain, it
+
+        def load_chain(chain):
+            block, half = divmod(chain, HALVES)
+            pri_a, o_first = blocks[block]
+            slot = chain % LIVE
+            quad0 = pri_pool.tile([P, QUAD, P], F32, name="quad0_%d" % slot, tag="quad0_%d" % slot)
+            quad1 = pri_pool.tile([P, QUAD, P], F32, name="quad1_%d" % slot, tag="quad1_%d" % slot)
+            pieces = [(quad0[:], 0, QUAD), (quad1[:], QUAD, QUAD), (tap8[:, slot : slot + 1, :], 2 * QUAD, 1)]
+            for pri, tap0, n_taps in pieces:
+                for u in range(n_taps):
+                    nc.tensor.transpose(pri[:, u, :], pri_a[:, HALVES * (tap0 + u) + half, :], ident[:])
+            work = chain_pool.tile([P, TAPS, P], F32)
+            chains[chain] = {"pieces": pieces, "work": work, "o": o_first[:, half * P : (half + 1) * P]}
+
+        def new_item(ch):
+            dist = item_pool.tile([P, TAPS, HALF_CAPS], F32)
+            cw = item_pool.tile([P, TAPS, HALF_CAPS], F32)
+            ch["dist"] = dist
+            ch["cw"] = cw
+
+        def subtract_and_square(ch, piece):
+            pri, tap0, n_taps = ch["pieces"][piece]
+            diff = ch["work"][:, tap0 : tap0 + n_taps, :]
+            nc.vector.tensor_tensor(
+                out=diff, in0=pri, in1=ch["o"].unsqueeze(1).to_broadcast([P, n_taps, P]), op=ALU.subtract
             )
+            nc.scalar.activation(out=diff, in_=diff, func=ACT.Square)
+
+        def sum_channels(ch, piece):
+            pri, tap0, n_taps = ch["pieces"][piece]
+            nc.vector.tensor_reduce(
+                out=ch["dist"][:, tap0 : tap0 + n_taps, :],
+                in_=ch["work"][:, tap0 : tap0 + n_taps, :].rearrange("p t (c k) -> p t c k", k=CAP_CH),
+                axis=AXIS_X,
+                op=ALU.add,
+            )
+
+        def inverse_root(ch, tap0, n_taps):
+            taps = slice(tap0, tap0 + n_taps)
+            nc.scalar.activation(out=ch["cw"][:, taps, :], in_=ch["dist"][:, taps, :], func=ACT.Abs_reciprocal_sqrt, bias=EPS)
+
+        def multiply(ch, piece):
+            pri, tap0, n_taps = ch["pieces"][piece]
+            nc.vector.tensor_tensor(
+                out=ch["work"][:, tap0 : tap0 + n_taps, :].rearrange("p t (c k) -> p t c k", k=CAP_CH),
+                in0=pri.rearrange("p t (c k) -> p t c k", k=CAP_CH),
+                in1=ch["cw"][:, tap0 : tap0 + n_taps, :].unsqueeze(3).to_broadcast([P, n_taps, HALF_CAPS, CAP_CH]),
+                op=ALU.mult,
+            )
+
+        def sum_weights(ch):
+            cw_sum = item_pool.tile([P, HALF_CAPS], F32)
+            nc.vector.tensor_reduce(out=cw_sum[:], in_=ch["cw"][:].rearrange("p t c -> p c t"), axis=AXIS_X, op=ALU.add)
+            ch["cw_sum"] = cw_sum
+
+        def invert_sum(ch):
+            cw_inv = item_pool.tile([P, HALF_CAPS], F32)
+            nc.vector.reciprocal(out=cw_inv[:], in_=ch["cw_sum"][:])
+            ch["cw_inv"] = cw_inv
+
+        def sum_taps(ch):
+            work = ch["work"]
+            nc.gpsimd.tensor_tensor(out=work[:, 0:4, :], in0=work[:, 0:4, :], in1=work[:, 4:8, :], op=ALU.add)
+            nc.gpsimd.tensor_tensor(out=work[:, 0:2, :], in0=work[:, 0:2, :], in1=work[:, 2:4, :], op=ALU.add)
+            nc.gpsimd.tensor_tensor(out=work[:, 0, :], in0=work[:, 0, :], in1=work[:, 1, :], op=ALU.add)
+            nc.gpsimd.tensor_tensor(out=work[:, 0, :], in0=work[:, 0, :], in1=work[:, 8, :], op=ALU.add)
+            o_next = item_pool.tile([P, P], F32)
+            nc.gpsimd.tensor_tensor(
+                out=o_next[:].rearrange("p (c k) -> p c k", k=CAP_CH),
+                in0=work[:, 0, :].rearrange("p (c k) -> p c k", k=CAP_CH),
+                in1=ch["cw_inv"][:].unsqueeze(2).to_broadcast([P, HALF_CAPS, CAP_CH]),
+                op=ALU.mult,
+            )
+            ch["o"] = o_next[:]
+
+        def prepare_input(tick):
+            b, pos = divmod(tick, TICKS_PER_IMAGE)
+            first = TICKS_PER_IMAGE - SLICES
+            if b + 1 >= IMAGES or pos < first - 1:
+                return
+            if pos == first - 1:
+                raws[b + 1] = load_image(b + 1)
+                return
+            j, part = divmod(pos - first, ROWS // REGROUP_ROWS)
+            dst, src = regroup_views(raws[b + 1], j, REGROUP_ROWS * part, REGROUP_ROWS)
+            nc.scalar.copy(out=dst, in_=src)
+
+        raws = {}
+        N_TICKS = N_BLOCKS * TICKS_PER_BLOCK
+
+        issue(0)
+        for tick in range(AHEAD):
+            collect(tick)
+            issue(tick + 1)
+        load_chain(0)
+
+        for n in range(N_ITEMS + 3):
+            measure = item(n)
+            weigh = item(n - 1)
+            total = item(n - 2)
+            leave = item(n - 3)
+            coming = item(n + 1)
+            m_ch = chains[measure[0]] if measure else None
+            w_ch = chains[weigh[0]] if weigh else None
+
+            tick = n + AHEAD
+            if tick < N_TICKS:
+                collect(tick)
+                prepare_input(tick)
+            if coming and coming[1] == 0:
+                load_chain(coming[0])
+            out_ps = None
+            if leave and leave[1] == ITERATIONS - 1:
+                out_ps = transit.tile([P, P], F32, tag="transit")
+                nc.tensor.transpose(out_ps[:], chains[leave[0]]["o"], ident[:])
+
+            if m_ch:
+                new_item(m_ch)
+            for piece in range(2):
+                if w_ch:
+                    multiply(w_ch, piece)
+                if m_ch:
+                    subtract_and_square(m_ch, piece)
+            if w_ch:
+                sum_weights(w_ch)
+                multiply(w_ch, 2)
+            if m_ch:
+                subtract_and_square(m_ch, 2)
+            if out_ps is not None:
+                block, half = divmod(leave[0], HALVES)
+                b, blk = divmod(block, BLOCKS_PER_IMAGE)
+                out_sb = item_pool.tile([P, P], F32)
+                nc.scalar.activation(out=out_sb[:], in_=out_ps[:], func=ACT.Identity, bias=bias_mean[:, half : half + 1])
+                nc.sync.dma_start(
+                    out=out[b].rearrange("f h w -> f (h w)")[half * P : (half + 1) * P, blk * P : (blk + 1) * P],
+                    in_=out_sb[:],
+                )
+            if m_ch:
+                sum_channels(m_ch, 0)
+                inverse_root(m_ch, 0, QUAD)
+            if w_ch:
+                invert_sum(w_ch)
+            if m_ch:
+                sum_channels(m_ch, 1)
+                sum_channels(m_ch, 2)
+                inverse_root(m_ch, QUAD, TAPS - QUAD)
+            if total:
+                sum_taps(chains[total[0]])
+
+            if tick + 1 < N_TICKS:
+                if (tick + 1) % TICKS_PER_IMAGE == 0:
+                    quantise_image()
+                issue(tick + 1)

@@ -41,6 +41,7 @@ TICKS_PER_IMAGE = TICKS_PER_BLOCK * BLOCKS_PER_IMAGE
 AHEAD = 2 * TICKS_PER_BLOCK
 REGROUP_ROWS = 4
 SLICES = KS * ROWS // REGROUP_ROWS
+EARLY_BANKS = 4
 
 FLOPS = 2 * IMAGES * PIXELS * 512 * TAPS * FEATURES
 
@@ -55,7 +56,6 @@ def tile_capsulelayer_t_kernel(tc, image, weight, bias, out):
         chain_pool = ctx.enter_context(tc.tile_pool(name="chain", bufs=LIVE + 1))
         item_pool = ctx.enter_context(tc.tile_pool(name="item", bufs=LIVE + 1))
         transit = ctx.enter_context(tc.psum_pool(name="transit", bufs=1))
-        pri_pool = ctx.enter_context(tc.psum_pool(name="pri", bufs=1))
 
         ident = consts.tile([P, P], F32)
         make_identity(nc, ident[:])
@@ -149,14 +149,14 @@ def tile_capsulelayer_t_kernel(tc, image, weight, bias, out):
         blocks = {}
         banks = {}
 
-        def issue(tick):
+        def issue(tick, pool):
             block, part = divmod(tick, TICKS_PER_BLOCK)
             first_row = BLOCK_ROWS * (block % BLOCKS_PER_IMAGE)
             if part == 0:
                 pri_a = block_pool.tile([P, PASSES, P], F32)
                 o_first = block_pool.tile([P, FEATURES], F32)
                 blocks[block] = (pri_a, o_first)
-            bank = transit.tile([P, PASSES_PER_TICK + 1, P], F32, tag="transit")
+            bank = pool.tile([P, PASSES_PER_TICK + 1, P], F32, tag="bank")
             banks[tick] = bank
             for s in range(PASSES_PER_TICK):
                 t, half = divmod(PASSES_PER_TICK * part + s, HALVES)
@@ -198,6 +198,15 @@ def tile_capsulelayer_t_kernel(tc, image, weight, bias, out):
             if part < HALVES:
                 nc.scalar.mul(out=o_first[:, part * P : (part + 1) * P], in_=bank[:, PASSES_PER_TICK, :], mul=1.0 / TAPS)
 
+        with tc.psum_pool(name="early", bufs=EARLY_BANKS) as early:
+            for tick in range(AHEAD + EARLY_BANKS):
+                if tick >= EARLY_BANKS:
+                    collect(tick - EARLY_BANKS)
+                if tick < AHEAD:
+                    issue(tick, early)
+        issue(AHEAD, transit)
+
+        pri_pool = ctx.enter_context(tc.psum_pool(name="pri", bufs=1))
         tap8 = pri_pool.tile([P, LIVE, P], F32, name="tap8", tag="tap8")
         chains = {}
 
@@ -236,8 +245,7 @@ def tile_capsulelayer_t_kernel(tc, image, weight, bias, out):
             )
             nc.scalar.activation(out=diff, in_=diff, func=ACT.Square)
 
-        def sum_channels(ch, piece):
-            pri, tap0, n_taps = ch["pieces"][piece]
+        def sum_channels(ch, tap0, n_taps):
             nc.vector.tensor_reduce(
                 out=ch["dist"][:, tap0 : tap0 + n_taps, :],
                 in_=ch["work"][:, tap0 : tap0 + n_taps, :].rearrange("p t (c k) -> p t c k", k=CAP_CH),
@@ -265,7 +273,8 @@ def tile_capsulelayer_t_kernel(tc, image, weight, bias, out):
 
         def invert_sum(ch):
             cw_inv = item_pool.tile([P, HALF_CAPS], F32)
-            nc.vector.reciprocal(out=cw_inv[:], in_=ch["cw_sum"][:])
+            nc.scalar.activation(out=cw_inv[:], in_=ch["cw_sum"][:], func=ACT.Abs_reciprocal_sqrt)
+            nc.scalar.activation(out=cw_inv[:], in_=cw_inv[:], func=ACT.Square)
             ch["cw_inv"] = cw_inv
 
         def sum_taps(ch):
@@ -298,10 +307,6 @@ def tile_capsulelayer_t_kernel(tc, image, weight, bias, out):
         raws = {}
         N_TICKS = N_BLOCKS * TICKS_PER_BLOCK
 
-        issue(0)
-        for tick in range(AHEAD):
-            collect(tick)
-            issue(tick + 1)
         load_chain(0)
 
         for n in range(N_ITEMS + 3):
@@ -321,7 +326,7 @@ def tile_capsulelayer_t_kernel(tc, image, weight, bias, out):
                 load_chain(coming[0])
             out_ps = None
             if leave and leave[1] == ITERATIONS - 1:
-                out_ps = transit.tile([P, P], F32, tag="transit")
+                out_ps = transit.tile([P, P], F32, tag="bank")
                 nc.tensor.transpose(out_ps[:], chains[leave[0]]["o"], ident[:])
 
             if m_ch:
@@ -345,14 +350,12 @@ def tile_capsulelayer_t_kernel(tc, image, weight, bias, out):
                     out=out[b].rearrange("f h w -> f (h w)")[half * P : (half + 1) * P, blk * P : (blk + 1) * P],
                     in_=out_sb[:],
                 )
-            if m_ch:
-                sum_channels(m_ch, 0)
-                inverse_root(m_ch, 0, QUAD)
             if w_ch:
                 invert_sum(w_ch)
             if m_ch:
-                sum_channels(m_ch, 1)
-                sum_channels(m_ch, 2)
+                sum_channels(m_ch, 0, QUAD)
+                inverse_root(m_ch, 0, QUAD)
+                sum_channels(m_ch, QUAD, TAPS - QUAD)
                 inverse_root(m_ch, QUAD, TAPS - QUAD)
             if total:
                 sum_taps(chains[total[0]])
@@ -360,4 +363,4 @@ def tile_capsulelayer_t_kernel(tc, image, weight, bias, out):
             if tick + 1 < N_TICKS:
                 if (tick + 1) % TICKS_PER_IMAGE == 0:
                     quantise_image()
-                issue(tick + 1)
+                issue(tick + 1, transit)

@@ -31,14 +31,15 @@ BLOCK_ROWS = P // COLS
 BLOCKS_PER_IMAGE = PIXELS // P
 N_BLOCKS = IMAGES * BLOCKS_PER_IMAGE
 QUAD = 4
-N_CHAINS = N_BLOCKS * HALVES
 LIVE = 3
-N_ITEMS = -(-N_CHAINS // LIVE) * LIVE * ITERATIONS
+GROUP_ITEMS = ITERATIONS * LIVE * HALVES
+N_ITEMS = -(-N_BLOCKS // LIVE) * GROUP_ITEMS
+SLOTS = 3
 PASSES = TAPS * HALVES
 PASSES_PER_TICK = 3
 TICKS_PER_BLOCK = PASSES // PASSES_PER_TICK
 TICKS_PER_IMAGE = TICKS_PER_BLOCK * BLOCKS_PER_IMAGE
-AHEAD = 2 * TICKS_PER_BLOCK
+AHEAD = LIVE * TICKS_PER_BLOCK
 REGROUP_ROWS = 4
 SLICES = KS * ROWS // REGROUP_ROWS
 EARLY_BANKS = 4
@@ -52,8 +53,8 @@ def tile_capsulelayer_t_kernel(tc, image, weight, bias, out):
         ctx.enter_context(tc.manual_schedule())
         consts = ctx.enter_context(tc.tile_pool(name="consts", bufs=1))
         stage = ctx.enter_context(tc.tile_pool(name="stage", bufs=2))
-        block_pool = ctx.enter_context(tc.tile_pool(name="block", bufs=3))
-        chain_pool = ctx.enter_context(tc.tile_pool(name="chain", bufs=LIVE + 1))
+        block_pool = ctx.enter_context(tc.tile_pool(name="block", bufs=2 * LIVE))
+        work_pool = ctx.enter_context(tc.tile_pool(name="work", bufs=LIVE + 1))
         item_pool = ctx.enter_context(tc.tile_pool(name="item", bufs=LIVE + 1))
         transit = ctx.enter_context(tc.psum_pool(name="transit", bufs=1))
 
@@ -207,90 +208,106 @@ def tile_capsulelayer_t_kernel(tc, image, weight, bias, out):
         issue(AHEAD, transit)
 
         pri_pool = ctx.enter_context(tc.psum_pool(name="pri", bufs=1))
-        tap8 = pri_pool.tile([P, LIVE, P], F32, name="tap8", tag="tap8")
-        chains = {}
+        tap8 = pri_pool.tile([P, SLOTS, P], F32, name="tap8", tag="tap8")
+        uses = {}
+        routes = {}
 
         def item(n):
-            group, rest = divmod(n, LIVE * ITERATIONS)
-            it, member = divmod(rest, LIVE)
-            chain = LIVE * group + member
-            if n < 0 or chain >= N_CHAINS:
+            group, rest = divmod(n, GROUP_ITEMS)
+            it, rest = divmod(rest, LIVE * HALVES)
+            member, half = divmod(rest, HALVES)
+            block = LIVE * group + member
+            if n < 0 or block >= N_BLOCKS:
                 return None
-            return chain, it
+            return block, it, half
 
-        def load_chain(chain):
-            block, half = divmod(chain, HALVES)
-            pri_a, o_first = blocks[block]
-            slot = chain % LIVE
+        def load_priors(use):
+            who = item(use // 2 - use % 2)
+            if who is None:
+                return
+            block, it, half = who
+            pri_a = blocks[block][0]
+            slot = use % SLOTS
             quad0 = pri_pool.tile([P, QUAD, P], F32, name="quad0_%d" % slot, tag="quad0_%d" % slot)
             quad1 = pri_pool.tile([P, QUAD, P], F32, name="quad1_%d" % slot, tag="quad1_%d" % slot)
-            pieces = [(quad0[:], 0, QUAD), (quad1[:], QUAD, QUAD), (tap8[:, slot : slot + 1, :], 2 * QUAD, 1)]
+            pieces = [(tap8[:, slot : slot + 1, :], 2 * QUAD, 1), (quad0[:], 0, QUAD), (quad1[:], QUAD, QUAD)]
             for pri, tap0, n_taps in pieces:
                 for u in range(n_taps):
                     nc.tensor.transpose(pri[:, u, :], pri_a[:, HALVES * (tap0 + u) + half, :], ident[:])
-            work = chain_pool.tile([P, TAPS, P], F32)
-            chains[chain] = {"pieces": pieces, "work": work, "o": o_first[:, half * P : (half + 1) * P]}
+            uses[use] = [pieces[1], pieces[2], pieces[0]]
 
-        def new_item(ch):
-            dist = item_pool.tile([P, TAPS, HALF_CAPS], F32)
-            cw = item_pool.tile([P, TAPS, HALF_CAPS], F32)
-            ch["dist"] = dist
-            ch["cw"] = cw
+        def start_iteration(block, it):
+            if it == 0:
+                work = work_pool.tile([P, TAPS, FEATURES], F32)
+                routes[block] = {"work": work, "o": blocks[block][1][:]}
+            dist = item_pool.tile([P, TAPS, HALVES * HALF_CAPS], F32)
+            cw = item_pool.tile([P, TAPS, HALVES * HALF_CAPS], F32)
+            routes[block]["dist"] = dist
+            routes[block]["cw"] = cw
 
-        def subtract_and_square(ch, piece):
-            pri, tap0, n_taps = ch["pieces"][piece]
-            diff = ch["work"][:, tap0 : tap0 + n_taps, :]
-            nc.vector.tensor_tensor(
-                out=diff, in0=pri, in1=ch["o"].unsqueeze(1).to_broadcast([P, n_taps, P]), op=ALU.subtract
-            )
+        def subtract(rt, half, pieces):
+            feats = slice(half * P, (half + 1) * P)
+            for pri, tap0, n_taps in pieces:
+                nc.vector.tensor_tensor(
+                    out=rt["work"][:, tap0 : tap0 + n_taps, feats],
+                    in0=pri,
+                    in1=rt["o"][:, feats].unsqueeze(1).to_broadcast([P, n_taps, P]),
+                    op=ALU.subtract,
+                )
+
+        def square(rt, half, tap0, n_taps):
+            diff = rt["work"][:, tap0 : tap0 + n_taps, half * P : (half + 1) * P]
             nc.scalar.activation(out=diff, in_=diff, func=ACT.Square)
 
-        def sum_channels(ch, tap0, n_taps):
+        def sum_channels(rt, half, tap0, n_taps):
             nc.vector.tensor_reduce(
-                out=ch["dist"][:, tap0 : tap0 + n_taps, :],
-                in_=ch["work"][:, tap0 : tap0 + n_taps, :].rearrange("p t (c k) -> p t c k", k=CAP_CH),
+                out=rt["dist"][:, tap0 : tap0 + n_taps, half * HALF_CAPS : (half + 1) * HALF_CAPS],
+                in_=rt["work"][:, tap0 : tap0 + n_taps, half * P : (half + 1) * P].rearrange("p t (c k) -> p t c k", k=CAP_CH),
                 axis=AXIS_X,
                 op=ALU.add,
             )
 
-        def inverse_root(ch, tap0, n_taps):
+        def inverse_root(rt, half, tap0, n_taps):
             taps = slice(tap0, tap0 + n_taps)
-            nc.scalar.activation(out=ch["cw"][:, taps, :], in_=ch["dist"][:, taps, :], func=ACT.Abs_reciprocal_sqrt, bias=EPS)
+            caps = slice(half * HALF_CAPS, (half + 1) * HALF_CAPS)
+            nc.scalar.activation(out=rt["cw"][:, taps, caps], in_=rt["dist"][:, taps, caps], func=ACT.Abs_reciprocal_sqrt, bias=EPS)
 
-        def multiply(ch, piece):
-            pri, tap0, n_taps = ch["pieces"][piece]
-            nc.vector.tensor_tensor(
-                out=ch["work"][:, tap0 : tap0 + n_taps, :].rearrange("p t (c k) -> p t c k", k=CAP_CH),
-                in0=pri.rearrange("p t (c k) -> p t c k", k=CAP_CH),
-                in1=ch["cw"][:, tap0 : tap0 + n_taps, :].unsqueeze(3).to_broadcast([P, n_taps, HALF_CAPS, CAP_CH]),
-                op=ALU.mult,
-            )
+        def multiply(rt, half, pieces):
+            for pri, tap0, n_taps in pieces:
+                nc.vector.tensor_tensor(
+                    out=rt["work"][:, tap0 : tap0 + n_taps, half * P : (half + 1) * P].rearrange("p t (c k) -> p t c k", k=CAP_CH),
+                    in0=pri.rearrange("p t (c k) -> p t c k", k=CAP_CH),
+                    in1=rt["cw"][:, tap0 : tap0 + n_taps, half * HALF_CAPS : (half + 1) * HALF_CAPS]
+                    .unsqueeze(3)
+                    .to_broadcast([P, n_taps, HALF_CAPS, CAP_CH]),
+                    op=ALU.mult,
+                )
 
-        def sum_weights(ch):
-            cw_sum = item_pool.tile([P, HALF_CAPS], F32)
-            nc.vector.tensor_reduce(out=cw_sum[:], in_=ch["cw"][:].rearrange("p t c -> p c t"), axis=AXIS_X, op=ALU.add)
-            ch["cw_sum"] = cw_sum
+        def sum_weights(rt):
+            cw_sum = item_pool.tile([P, HALVES * HALF_CAPS], F32)
+            nc.vector.tensor_reduce(out=cw_sum[:], in_=rt["cw"][:].rearrange("p t c -> p c t"), axis=AXIS_X, op=ALU.add)
+            rt["cw_sum"] = cw_sum
 
-        def invert_sum(ch):
-            cw_inv = item_pool.tile([P, HALF_CAPS], F32)
-            nc.scalar.activation(out=cw_inv[:], in_=ch["cw_sum"][:], func=ACT.Abs_reciprocal_sqrt)
+        def invert_sum(rt):
+            cw_inv = item_pool.tile([P, HALVES * HALF_CAPS], F32)
+            nc.scalar.activation(out=cw_inv[:], in_=rt["cw_sum"][:], func=ACT.Abs_reciprocal_sqrt)
             nc.scalar.activation(out=cw_inv[:], in_=cw_inv[:], func=ACT.Square)
-            ch["cw_inv"] = cw_inv
+            rt["cw_inv"] = cw_inv
 
-        def sum_taps(ch):
-            work = ch["work"]
+        def sum_taps(rt):
+            work = rt["work"]
             nc.gpsimd.tensor_tensor(out=work[:, 0:4, :], in0=work[:, 0:4, :], in1=work[:, 4:8, :], op=ALU.add)
             nc.gpsimd.tensor_tensor(out=work[:, 0:2, :], in0=work[:, 0:2, :], in1=work[:, 2:4, :], op=ALU.add)
             nc.gpsimd.tensor_tensor(out=work[:, 0, :], in0=work[:, 0, :], in1=work[:, 1, :], op=ALU.add)
             nc.gpsimd.tensor_tensor(out=work[:, 0, :], in0=work[:, 0, :], in1=work[:, 8, :], op=ALU.add)
-            o_next = item_pool.tile([P, P], F32)
+            o_next = item_pool.tile([P, FEATURES], F32)
             nc.gpsimd.tensor_tensor(
                 out=o_next[:].rearrange("p (c k) -> p c k", k=CAP_CH),
                 in0=work[:, 0, :].rearrange("p (c k) -> p c k", k=CAP_CH),
-                in1=ch["cw_inv"][:].unsqueeze(2).to_broadcast([P, HALF_CAPS, CAP_CH]),
+                in1=rt["cw_inv"][:].unsqueeze(2).to_broadcast([P, HALVES * HALF_CAPS, CAP_CH]),
                 op=ALU.mult,
             )
-            ch["o"] = o_next[:]
+            rt["o"] = o_next[:]
 
         def prepare_input(tick):
             b, pos = divmod(tick, TICKS_PER_IMAGE)
@@ -306,59 +323,60 @@ def tile_capsulelayer_t_kernel(tc, image, weight, bias, out):
 
         raws = {}
         N_TICKS = N_BLOCKS * TICKS_PER_BLOCK
+        LEAVE_AFTER = 4
 
-        load_chain(0)
+        for use in range(SLOTS):
+            load_priors(use)
 
-        for n in range(N_ITEMS + 3):
+        for n in range(N_ITEMS + LEAVE_AFTER + 1):
             measure = item(n)
             weigh = item(n - 1)
-            total = item(n - 2)
-            leave = item(n - 3)
-            coming = item(n + 1)
-            m_ch = chains[measure[0]] if measure else None
-            w_ch = chains[weigh[0]] if weigh else None
-
+            left = item(n - LEAVE_AFTER)
             tick = n + AHEAD
+
+            if measure:
+                block, it, half = measure
+                if half == 0:
+                    start_iteration(block, it)
+                subtract(routes[block], half, uses[2 * n])
+                square(routes[block], half, 0, QUAD)
+                square(routes[block], half, QUAD, TAPS - QUAD)
+            load_priors(2 * n + SLOTS)
+            if weigh:
+                multiply(routes[weigh[0]], weigh[2], uses[2 * n + 1])
+            block_done = weigh and weigh[2] == HALVES - 1
+            if block_done:
+                sum_weights(routes[weigh[0]])
             if tick < N_TICKS:
                 collect(tick)
-                prepare_input(tick)
-            if coming and coming[1] == 0:
-                load_chain(coming[0])
             out_ps = None
-            if leave and leave[1] == ITERATIONS - 1:
-                out_ps = transit.tile([P, P], F32, tag="bank")
-                nc.tensor.transpose(out_ps[:], chains[leave[0]]["o"], ident[:])
-
-            if m_ch:
-                new_item(m_ch)
-            for piece in range(2):
-                if w_ch:
-                    multiply(w_ch, piece)
-                if m_ch:
-                    subtract_and_square(m_ch, piece)
-            if w_ch:
-                sum_weights(w_ch)
-                multiply(w_ch, 2)
-            if m_ch:
-                subtract_and_square(m_ch, 2)
+            if left and left[1] == ITERATIONS - 1 and left[2] == HALVES - 1:
+                out_ps = transit.tile([P, HALVES, P], F32, tag="bank")
+                for g in range(HALVES):
+                    nc.tensor.transpose(out_ps[:, g, :], routes[left[0]]["o"][:, g * P : (g + 1) * P], ident[:])
+            load_priors(2 * n + 1 + SLOTS)
+            if measure:
+                sum_channels(routes[block], half, 0, QUAD)
+                inverse_root(routes[block], half, 0, QUAD)
+            if block_done:
+                invert_sum(routes[weigh[0]])
             if out_ps is not None:
-                block, half = divmod(leave[0], HALVES)
-                b, blk = divmod(block, BLOCKS_PER_IMAGE)
-                out_sb = item_pool.tile([P, P], F32)
-                nc.scalar.activation(out=out_sb[:], in_=out_ps[:], func=ACT.Identity, bias=bias_mean[:, half : half + 1])
+                b, blk = divmod(left[0], BLOCKS_PER_IMAGE)
+                out_sb = item_pool.tile([P, HALVES, P], F32)
+                for g in range(HALVES):
+                    nc.scalar.activation(
+                        out=out_sb[:, g, :], in_=out_ps[:, g, :], func=ACT.Identity, bias=bias_mean[:, g : g + 1]
+                    )
                 nc.sync.dma_start(
-                    out=out[b].rearrange("f h w -> f (h w)")[half * P : (half + 1) * P, blk * P : (blk + 1) * P],
-                    in_=out_sb[:],
+                    out=out[b].rearrange("(g f) h w -> f g (h w)", g=HALVES)[:, :, blk * P : (blk + 1) * P], in_=out_sb[:]
                 )
-            if w_ch:
-                invert_sum(w_ch)
-            if m_ch:
-                sum_channels(m_ch, 0, QUAD)
-                inverse_root(m_ch, 0, QUAD)
-                sum_channels(m_ch, QUAD, TAPS - QUAD)
-                inverse_root(m_ch, QUAD, TAPS - QUAD)
-            if total:
-                sum_taps(chains[total[0]])
+            if tick < N_TICKS:
+                prepare_input(tick)
+            if measure:
+                sum_channels(routes[block], half, QUAD, TAPS - QUAD)
+                inverse_root(routes[block], half, QUAD, TAPS - QUAD)
+            if block_done:
+                sum_taps(routes[weigh[0]])
 
             if tick + 1 < N_TICKS:
                 if (tick + 1) % TICKS_PER_IMAGE == 0:

@@ -209,7 +209,7 @@ def tile_capsulelayer_t_kernel(tc, image, weight, bias, out):
 
         pri_pool = ctx.enter_context(tc.psum_pool(name="pri", bufs=1))
         tap8 = pri_pool.tile([P, SLOTS, P], F32, name="tap8", tag="tap8")
-        uses = {}
+        loaded = {}
         routes = {}
 
         def item(n):
@@ -221,20 +221,20 @@ def tile_capsulelayer_t_kernel(tc, image, weight, bias, out):
                 return None
             return block, it, half
 
-        def load_priors(use):
-            who = item(use // 2 - use % 2)
+        def load_priors(n):
+            who = item(n)
             if who is None:
                 return
             block, it, half = who
             pri_a = blocks[block][0]
-            slot = use % SLOTS
+            slot = n % SLOTS
             quad0 = pri_pool.tile([P, QUAD, P], F32, name="quad0_%d" % slot, tag="quad0_%d" % slot)
             quad1 = pri_pool.tile([P, QUAD, P], F32, name="quad1_%d" % slot, tag="quad1_%d" % slot)
             pieces = [(tap8[:, slot : slot + 1, :], 2 * QUAD, 1), (quad0[:], 0, QUAD), (quad1[:], QUAD, QUAD)]
             for pri, tap0, n_taps in pieces:
                 for u in range(n_taps):
                     nc.tensor.transpose(pri[:, u, :], pri_a[:, HALVES * (tap0 + u) + half, :], ident[:])
-            uses[use] = [pieces[1], pieces[2], pieces[0]]
+            loaded[n] = [pieces[1], pieces[2], pieces[0]]
 
         def start_iteration(block, it):
             if it == 0:
@@ -325,8 +325,8 @@ def tile_capsulelayer_t_kernel(tc, image, weight, bias, out):
         N_TICKS = N_BLOCKS * TICKS_PER_BLOCK
         LEAVE_AFTER = 4
 
-        for use in range(SLOTS):
-            load_priors(use)
+        load_priors(0)
+        load_priors(1)
 
         for n in range(N_ITEMS + LEAVE_AFTER + 1):
             measure = item(n)
@@ -338,12 +338,11 @@ def tile_capsulelayer_t_kernel(tc, image, weight, bias, out):
                 block, it, half = measure
                 if half == 0:
                     start_iteration(block, it)
-                subtract(routes[block], half, uses[2 * n])
+                subtract(routes[block], half, loaded[n])
                 square(routes[block], half, 0, QUAD)
                 square(routes[block], half, QUAD, TAPS - QUAD)
-            load_priors(2 * n + SLOTS)
             if weigh:
-                multiply(routes[weigh[0]], weigh[2], uses[2 * n + 1])
+                multiply(routes[weigh[0]], weigh[2], loaded[n - 1])
             block_done = weigh and weigh[2] == HALVES - 1
             if block_done:
                 sum_weights(routes[weigh[0]])
@@ -354,10 +353,7 @@ def tile_capsulelayer_t_kernel(tc, image, weight, bias, out):
                 out_ps = transit.tile([P, HALVES, P], F32, tag="bank")
                 for g in range(HALVES):
                     nc.tensor.transpose(out_ps[:, g, :], routes[left[0]]["o"][:, g * P : (g + 1) * P], ident[:])
-            load_priors(2 * n + 1 + SLOTS)
-            if measure:
-                sum_channels(routes[block], half, 0, QUAD)
-                inverse_root(routes[block], half, 0, QUAD)
+            load_priors(n + SLOTS - 1)
             if block_done:
                 invert_sum(routes[weigh[0]])
             if out_ps is not None:
@@ -373,8 +369,9 @@ def tile_capsulelayer_t_kernel(tc, image, weight, bias, out):
             if tick < N_TICKS:
                 prepare_input(tick)
             if measure:
+                sum_channels(routes[block], half, 0, QUAD)
                 sum_channels(routes[block], half, QUAD, TAPS - QUAD)
-                inverse_root(routes[block], half, QUAD, TAPS - QUAD)
+                inverse_root(routes[block], half, 0, TAPS)
             if block_done:
                 sum_taps(routes[weigh[0]])
 

@@ -242,8 +242,10 @@ def tile_capsulelayer_t_kernel(tc, image, weight, bias, out):
                 routes[block] = {"work": work, "o": blocks[block][1][:]}
             dist = item_pool.tile([P, TAPS, HALVES * HALF_CAPS], F32)
             cw = item_pool.tile([P, TAPS, HALVES * HALF_CAPS], F32)
+            cw_sum = item_pool.tile([P, HALVES * HALF_CAPS], F32)
             routes[block]["dist"] = dist
             routes[block]["cw"] = cw
+            routes[block]["cw_sum"] = cw_sum
 
         def subtract(rt, half, pieces):
             feats = slice(half * P, (half + 1) * P)
@@ -267,10 +269,15 @@ def tile_capsulelayer_t_kernel(tc, image, weight, bias, out):
                 op=ALU.add,
             )
 
-        def inverse_root(rt, half, tap0, n_taps):
-            taps = slice(tap0, tap0 + n_taps)
-            caps = slice(half * HALF_CAPS, (half + 1) * HALF_CAPS)
-            nc.scalar.activation(out=rt["cw"][:, taps, caps], in_=rt["dist"][:, taps, caps], func=ACT.Abs_reciprocal_sqrt, bias=EPS)
+        def inverse_root(rt, half):
+            for cap in range(half * HALF_CAPS, (half + 1) * HALF_CAPS):
+                nc.scalar.activation(
+                    out=rt["cw"][:, :, cap],
+                    in_=rt["dist"][:, :, cap],
+                    func=ACT.Abs_reciprocal_sqrt,
+                    bias=EPS,
+                    accum_out=rt["cw_sum"][:, cap : cap + 1],
+                )
 
         def multiply(rt, half, pieces):
             for pri, tap0, n_taps in pieces:
@@ -282,11 +289,6 @@ def tile_capsulelayer_t_kernel(tc, image, weight, bias, out):
                     .to_broadcast([P, n_taps, HALF_CAPS, CAP_CH]),
                     op=ALU.mult,
                 )
-
-        def sum_weights(rt):
-            cw_sum = item_pool.tile([P, HALVES * HALF_CAPS], F32)
-            nc.vector.tensor_reduce(out=cw_sum[:], in_=rt["cw"][:].rearrange("p t c -> p c t"), axis=AXIS_X, op=ALU.add)
-            rt["cw_sum"] = cw_sum
 
         def invert_sum(rt):
             cw_inv = item_pool.tile([P, HALVES * HALF_CAPS], F32)
@@ -344,8 +346,6 @@ def tile_capsulelayer_t_kernel(tc, image, weight, bias, out):
             if weigh:
                 multiply(routes[weigh[0]], weigh[2], loaded[n - 1])
             block_done = weigh and weigh[2] == HALVES - 1
-            if block_done:
-                sum_weights(routes[weigh[0]])
             if tick < N_TICKS:
                 collect(tick)
             out_ps = None
@@ -371,7 +371,7 @@ def tile_capsulelayer_t_kernel(tc, image, weight, bias, out):
             if measure:
                 sum_channels(routes[block], half, 0, QUAD)
                 sum_channels(routes[block], half, QUAD, TAPS - QUAD)
-                inverse_root(routes[block], half, 0, TAPS)
+                inverse_root(routes[block], half)
             if block_done:
                 sum_taps(routes[weigh[0]])
 

@@ -94,7 +94,7 @@ def tile_capsulelayer_t_kernel(tc, image, weight, bias, out):
                     in_=x_grouped[j][:].rearrange("p h w r -> p (h w r)"),
                 )
             for j in range(KS):
-                nc.vector.tensor_copy(
+                nc.gpsimd.tensor_copy(
                     out=x_offset[j][:, COLS : COLS + PIXELS].bitcast(I32), in_=x_centre[j][:].bitcast(I32)
                 )
 
@@ -186,23 +186,30 @@ def tile_capsulelayer_t_kernel(tc, image, weight, bias, out):
                         stop=(t == TAPS - 1),
                     )
 
-        def collect(tick):
+        def collect(tick, by_vector=False):
             block, part = divmod(tick, TICKS_PER_BLOCK)
             pri_a, o_first = blocks[block]
             bank = banks[tick]
             for s in range(PASSES_PER_TICK):
                 k = PASSES_PER_TICK * part + s
                 t, half = divmod(k, HALVES)
-                nc.scalar.activation(
-                    out=pri_a[:, k, :], in_=bank[:, s, :], func=ACT.Identity, bias=bias_rel[:, t, half : half + 1]
-                )
+                if by_vector:
+                    nc.vector.tensor_scalar_add(out=pri_a[:, k, :], in0=bank[:, s, :], scalar1=bias_rel[:, t, half : half + 1])
+                else:
+                    nc.scalar.activation(
+                        out=pri_a[:, k, :], in_=bank[:, s, :], func=ACT.Identity, bias=bias_rel[:, t, half : half + 1]
+                    )
             if part < HALVES:
-                nc.scalar.mul(out=o_first[:, part * P : (part + 1) * P], in_=bank[:, PASSES_PER_TICK, :], mul=1.0 / TAPS)
+                mean = o_first[:, part * P : (part + 1) * P]
+                if by_vector:
+                    nc.vector.tensor_scalar_mul(out=mean, in0=bank[:, PASSES_PER_TICK, :], scalar1=1.0 / TAPS)
+                else:
+                    nc.scalar.mul(out=mean, in_=bank[:, PASSES_PER_TICK, :], mul=1.0 / TAPS)
 
         with tc.psum_pool(name="early", bufs=EARLY_BANKS) as early:
             for tick in range(AHEAD + EARLY_BANKS):
                 if tick >= EARLY_BANKS:
-                    collect(tick - EARLY_BANKS)
+                    collect(tick - EARLY_BANKS, by_vector=(tick % 2 == 1))
                 if tick < AHEAD:
                     issue(tick, early)
         issue(AHEAD, transit)
@@ -311,6 +318,18 @@ def tile_capsulelayer_t_kernel(tc, image, weight, bias, out):
             )
             rt["o"] = o_next[:]
 
+        def sum_taps_at_the_end(rt):
+            summed = item_pool.tile([P, FEATURES], F32)
+            nc.vector.tensor_reduce(out=summed[:], in_=rt["work"][:].rearrange("p t f -> p f t"), axis=AXIS_X, op=ALU.add)
+            o_last = item_pool.tile([P, FEATURES], F32)
+            nc.vector.tensor_tensor(
+                out=o_last[:].rearrange("p (c k) -> p c k", k=CAP_CH),
+                in0=summed[:].rearrange("p (c k) -> p c k", k=CAP_CH),
+                in1=rt["cw_inv"][:].unsqueeze(2).to_broadcast([P, HALVES * HALF_CAPS, CAP_CH]),
+                op=ALU.mult,
+            )
+            rt["o"] = o_last[:]
+
         def prepare_input(tick):
             b, pos = divmod(tick, TICKS_PER_IMAGE)
             first = TICKS_PER_IMAGE - SLICES
@@ -373,7 +392,10 @@ def tile_capsulelayer_t_kernel(tc, image, weight, bias, out):
                 sum_channels(routes[block], half, QUAD, TAPS - QUAD)
                 inverse_root(routes[block], half)
             if block_done:
-                sum_taps(routes[weigh[0]])
+                if weigh[0] == N_BLOCKS - 1 and weigh[1] == ITERATIONS - 1:
+                    sum_taps_at_the_end(routes[weigh[0]])
+                else:
+                    sum_taps(routes[weigh[0]])
 
             if tick + 1 < N_TICKS:
                 if (tick + 1) % TICKS_PER_IMAGE == 0:

@@ -94,7 +94,7 @@ def tile_capsulelayer_t_kernel(tc, image, weight, bias, out):
                     in_=x_grouped[j][:].rearrange("p h w r -> p (h w r)"),
                 )
             for j in range(KS):
-                nc.gpsimd.tensor_copy(
+                nc.vector.tensor_copy(
                     out=x_offset[j][:, COLS : COLS + PIXELS].bitcast(I32), in_=x_centre[j][:].bitcast(I32)
                 )
 

@@ -215,7 +215,8 @@ def tile_capsulelayer_t_kernel(tc, image, weight, bias, out):
         issue(AHEAD, transit)
 
         pri_pool = ctx.enter_context(tc.psum_pool(name="pri", bufs=1))
-        tap8 = pri_pool.tile([P, SLOTS, P], F32, name="tap8", tag="tap8")
+        tap8 = pri_pool.tile([P, 2, HALVES, P], F32, name="tap8", tag="tap8")
+        last_tap = {}
         loaded = {}
         routes = {}
 
@@ -237,11 +238,16 @@ def tile_capsulelayer_t_kernel(tc, image, weight, bias, out):
             slot = n % SLOTS
             quad0 = pri_pool.tile([P, QUAD, P], F32, name="quad0_%d" % slot, tag="quad0_%d" % slot)
             quad1 = pri_pool.tile([P, QUAD, P], F32, name="quad1_%d" % slot, tag="quad1_%d" % slot)
-            pieces = [(tap8[:, slot : slot + 1, :], 2 * QUAD, 1), (quad0[:], 0, QUAD), (quad1[:], QUAD, QUAD)]
+            if half == HALVES - 1:
+                place = (n // HALVES) % 2
+                for g in range(HALVES):
+                    nc.tensor.transpose(tap8[:, place, g, :], pri_a[:, HALVES * 2 * QUAD + g, :], ident[:])
+                last_tap[n - 1] = tap8[:, place, :, :]
+            pieces = [(quad0[:], 0, QUAD), (quad1[:], QUAD, QUAD)]
             for pri, tap0, n_taps in pieces:
                 for u in range(n_taps):
                     nc.tensor.transpose(pri[:, u, :], pri_a[:, HALVES * (tap0 + u) + half, :], ident[:])
-            loaded[n] = [pieces[1], pieces[2], pieces[0]]
+            loaded[n] = pieces
 
         def start_iteration(block, it):
             if it == 0:
@@ -263,6 +269,19 @@ def tile_capsulelayer_t_kernel(tc, image, weight, bias, out):
                     in1=rt["o"][:, feats].unsqueeze(1).to_broadcast([P, n_taps, P]),
                     op=ALU.subtract,
                 )
+
+        def subtract_last(rt, pri):
+            nc.vector.tensor_tensor(
+                out=rt["work"][:, TAPS - 1, :], in0=pri.rearrange("p g f -> p (g f)"), in1=rt["o"], op=ALU.subtract
+            )
+
+        def multiply_last(rt, pri):
+            nc.vector.tensor_tensor(
+                out=rt["work"][:, TAPS - 1, :].rearrange("p (c k) -> p c k", k=CAP_CH),
+                in0=pri.rearrange("p g (c k) -> p (g c) k", k=CAP_CH),
+                in1=rt["cw"][:, TAPS - 1, :].unsqueeze(2).to_broadcast([P, HALVES * HALF_CAPS, CAP_CH]),
+                op=ALU.mult,
+            )
 
         def square(rt, half, tap0, n_taps):
             diff = rt["work"][:, tap0 : tap0 + n_taps, half * P : (half + 1) * P]
@@ -344,7 +363,7 @@ def tile_capsulelayer_t_kernel(tc, image, weight, bias, out):
 
         raws = {}
         N_TICKS = N_BLOCKS * TICKS_PER_BLOCK
-        LEAVE_AFTER = 4
+        LEAVE_AFTER = 5
 
         load_priors(0)
         load_priors(1)
@@ -352,6 +371,7 @@ def tile_capsulelayer_t_kernel(tc, image, weight, bias, out):
         for n in range(N_ITEMS + LEAVE_AFTER + 1):
             measure = item(n)
             weigh = item(n - 1)
+            ends = item(n - 2)
             left = item(n - LEAVE_AFTER)
             tick = n + AHEAD
 
@@ -360,11 +380,15 @@ def tile_capsulelayer_t_kernel(tc, image, weight, bias, out):
                 if half == 0:
                     start_iteration(block, it)
                 subtract(routes[block], half, loaded[n])
+                if half == 0:
+                    subtract_last(routes[block], last_tap[n])
                 square(routes[block], half, 0, QUAD)
                 square(routes[block], half, QUAD, TAPS - QUAD)
+            block_done = ends and ends[2] == HALVES - 1
+            if block_done:
+                multiply_last(routes[ends[0]], last_tap[n - 1 - HALVES])
             if weigh:
                 multiply(routes[weigh[0]], weigh[2], loaded[n - 1])
-            block_done = weigh and weigh[2] == HALVES - 1
             if tick < N_TICKS:
                 collect(tick)
             out_ps = None
@@ -373,7 +397,7 @@ def tile_capsulelayer_t_kernel(tc, image, weight, bias, out):
                 for g in range(HALVES):
                     nc.tensor.transpose(out_ps[:, g, :], routes[left[0]]["o"][:, g * P : (g + 1) * P], ident[:])
             load_priors(n + SLOTS - 1)
-            if block_done:
+            if weigh and weigh[2] == HALVES - 1:
                 invert_sum(routes[weigh[0]])
             if out_ps is not None:
                 b, blk = divmod(left[0], BLOCKS_PER_IMAGE)
@@ -392,10 +416,10 @@ def tile_capsulelayer_t_kernel(tc, image, weight, bias, out):
                 sum_channels(routes[block], half, QUAD, TAPS - QUAD)
                 inverse_root(routes[block], half)
             if block_done:
-                if weigh[0] == N_BLOCKS - 1 and weigh[1] == ITERATIONS - 1:
-                    sum_taps_at_the_end(routes[weigh[0]])
+                if ends[0] == N_BLOCKS - 1 and ends[1] == ITERATIONS - 1:
+                    sum_taps_at_the_end(routes[ends[0]])
                 else:
-                    sum_taps(routes[weigh[0]])
+                    sum_taps(routes[ends[0]])
 
             if tick + 1 < N_TICKS:
                 if (tick + 1) % TICKS_PER_IMAGE == 0:

@@ -252,7 +252,8 @@ def tile_capsulelayer_t_kernel(tc, image, weight, bias, out):
         def start_iteration(block, it):
             if it == 0:
                 work = work_pool.tile([P, TAPS, FEATURES], F32)
-                routes[block] = {"work": work, "o": blocks[block][1][:]}
+                pri_last = work_pool.tile([P, FEATURES], F32)
+                routes[block] = {"work": work, "o": blocks[block][1][:], "pri_last": pri_last}
             dist = item_pool.tile([P, TAPS, HALVES * HALF_CAPS], F32)
             cw = item_pool.tile([P, TAPS, HALVES * HALF_CAPS], F32)
             cw_sum = item_pool.tile([P, HALVES * HALF_CAPS], F32)
@@ -275,11 +276,16 @@ def tile_capsulelayer_t_kernel(tc, image, weight, bias, out):
                 out=rt["work"][:, TAPS - 1, :], in0=pri.rearrange("p g f -> p (g f)"), in1=rt["o"], op=ALU.subtract
             )
 
-        def multiply_last(rt, pri):
+        def keep_last(rt, pri):
+            nc.scalar.copy(out=rt["pri_last"][:].rearrange("p (g f) -> p g f", g=HALVES), in_=pri)
+
+        def multiply_last(rt, pri, half):
             nc.vector.tensor_tensor(
-                out=rt["work"][:, TAPS - 1, :].rearrange("p (c k) -> p c k", k=CAP_CH),
-                in0=pri.rearrange("p g (c k) -> p (g c) k", k=CAP_CH),
-                in1=rt["cw"][:, TAPS - 1, :].unsqueeze(2).to_broadcast([P, HALVES * HALF_CAPS, CAP_CH]),
+                out=rt["work"][:, TAPS - 1, half * P : (half + 1) * P].rearrange("p (c k) -> p c k", k=CAP_CH),
+                in0=pri[:, half, :].rearrange("p (c k) -> p c k", k=CAP_CH),
+                in1=rt["cw"][:, TAPS - 1, half * HALF_CAPS : (half + 1) * HALF_CAPS]
+                .unsqueeze(2)
+                .to_broadcast([P, HALF_CAPS, CAP_CH]),
                 op=ALU.mult,
             )
 
@@ -322,7 +328,7 @@ def tile_capsulelayer_t_kernel(tc, image, weight, bias, out):
             nc.scalar.activation(out=cw_inv[:], in_=cw_inv[:], func=ACT.Square)
             rt["cw_inv"] = cw_inv
 
-        def sum_taps(rt):
+        def sum_taps(rt, goes_on):
             work = rt["work"]
             nc.gpsimd.tensor_tensor(out=work[:, 0:4, :], in0=work[:, 0:4, :], in1=work[:, 4:8, :], op=ALU.add)
             nc.gpsimd.tensor_tensor(out=work[:, 0:2, :], in0=work[:, 0:2, :], in1=work[:, 2:4, :], op=ALU.add)
@@ -336,6 +342,8 @@ def tile_capsulelayer_t_kernel(tc, image, weight, bias, out):
                 op=ALU.mult,
             )
             rt["o"] = o_next[:]
+            if goes_on:
+                nc.gpsimd.tensor_tensor(out=work[:, TAPS - 1, :], in0=rt["pri_last"][:], in1=o_next[:], op=ALU.subtract)
 
         def sum_taps_at_the_end(rt):
             summed = item_pool.tile([P, FEATURES], F32)
@@ -380,17 +388,19 @@ def tile_capsulelayer_t_kernel(tc, image, weight, bias, out):
                 if half == 0:
                     start_iteration(block, it)
                 subtract(routes[block], half, loaded[n])
-                if half == 0:
+                if half == 0 and it == 0:
                     subtract_last(routes[block], last_tap[n])
                 square(routes[block], half, 0, QUAD)
                 square(routes[block], half, QUAD, TAPS - QUAD)
             block_done = ends and ends[2] == HALVES - 1
-            if block_done:
-                multiply_last(routes[ends[0]], last_tap[n - 1 - HALVES])
+            if ends:
+                multiply_last(routes[ends[0]], last_tap[n - 2 - ends[2]], ends[2])
             if weigh:
                 multiply(routes[weigh[0]], weigh[2], loaded[n - 1])
             if tick < N_TICKS:
                 collect(tick)
+            if measure and half == 0 and it == 0:
+                keep_last(routes[block], last_tap[n])
             out_ps = None
             if left and left[1] == ITERATIONS - 1 and left[2] == HALVES - 1:
                 out_ps = transit.tile([P, HALVES, P], F32, tag="bank")
@@ -419,7 +429,7 @@ def tile_capsulelayer_t_kernel(tc, image, weight, bias, out):
                 if ends[0] == N_BLOCKS - 1 and ends[1] == ITERATIONS - 1:
                     sum_taps_at_the_end(routes[ends[0]])
                 else:
-                    sum_taps(routes[ends[0]])
+                    sum_taps(routes[ends[0]], goes_on=ends[1] < ITERATIONS - 1)
 
             if tick + 1 < N_TICKS:
                 if (tick + 1) % TICKS_PER_IMAGE == 0:

@@ -21,28 +21,29 @@ COLS = 32
 PIXELS = ROWS * COLS
 KS = 3
 TAPS = KS * KS
+REF = TAPS - 1
 FEATURES = 256
 CAP_CH = 16
+CAPS = FEATURES // CAP_CH
 HALVES = FEATURES // P
-HALF_CAPS = P // CAP_CH
 ITERATIONS = 3
 EPS = 1e-4
-BLOCK_ROWS = P // COLS
-BLOCKS_PER_IMAGE = PIXELS // P
-N_BLOCKS = IMAGES * BLOCKS_PER_IMAGE
-QUAD = 4
-LIVE = 3
-GROUP_ITEMS = ITERATIONS * LIVE * HALVES
-N_ITEMS = -(-N_BLOCKS // LIVE) * GROUP_ITEMS
-SLOTS = 3
-PASSES = TAPS * HALVES
-PASSES_PER_TICK = 3
-TICKS_PER_BLOCK = PASSES // PASSES_PER_TICK
-TICKS_PER_IMAGE = TICKS_PER_BLOCK * BLOCKS_PER_IMAGE
-AHEAD = LIVE * TICKS_PER_BLOCK
+LIVE = 4
+GROUP_PIXELS = LIVE * P
+GROUP_ROWS = GROUP_PIXELS // COLS
+GROUPS_PER_IMAGE = PIXELS // GROUP_PIXELS
+N_GROUPS = IMAGES * GROUPS_PER_IMAGE
+GROUP_ITEMS = LIVE * ITERATIONS
+N_ITEMS = N_GROUPS * GROUP_ITEMS
+NEG_REF = TAPS
+PAIRS = REF // 2
+EARLY_DEPTH = {"made": 4, "turned": 2, "sum": 2}
+DEPTH = {"made": 2, "turned": 2, "sum": 1}
+SLOTS_PER_STEP = 3
+INPUT_WORKS = 4
+G_TAPS = 6
 REGROUP_ROWS = 4
-SLICES = KS * ROWS // REGROUP_ROWS
-EARLY_BANKS = 4
+SLICES = ROWS // REGROUP_ROWS
 
 FLOPS = 2 * IMAGES * PIXELS * 512 * TAPS * FEATURES
 
@@ -52,386 +53,425 @@ def tile_capsulelayer_t_kernel(tc, image, weight, bias, out):
     with ExitStack() as ctx:
         ctx.enter_context(tc.manual_schedule())
         consts = ctx.enter_context(tc.tile_pool(name="consts", bufs=1))
-        stage = ctx.enter_context(tc.tile_pool(name="stage", bufs=2))
-        block_pool = ctx.enter_context(tc.tile_pool(name="block", bufs=2 * LIVE))
-        work_pool = ctx.enter_context(tc.tile_pool(name="work", bufs=LIVE + 1))
-        item_pool = ctx.enter_context(tc.tile_pool(name="item", bufs=LIVE + 1))
-        transit = ctx.enter_context(tc.psum_pool(name="transit", bufs=1))
+        images = ctx.enter_context(tc.tile_pool(name="images", bufs=2))
 
         ident = consts.tile([P, P], F32)
         make_identity(nc, ident[:])
 
-        x_grouped = [consts.tile([P, ROWS, COLS, PACK], BF16, name="x_grouped%d" % j, align_bytes=64) for j in range(KS)]
-        x_codes = [consts.tile([P, COLS + PIXELS + COLS], U32, name="x_codes%d" % j, align_bytes=64) for j in range(KS)]
-        x_centre = [consts.tile([P, PIXELS], U8, name="x_centre%d" % j, align_bytes=64) for j in range(KS)]
-        x_offset = [consts.tile([P, COLS + PIXELS + COLS], U8, name="x_offset%d" % j, align_bytes=64) for j in range(KS)]
-        for j in range(KS):
-            nc.vector.memset(x_codes[j][:, 0:COLS].bitcast(I32), 0)
-            nc.vector.memset(x_codes[j][:, COLS + PIXELS :].bitcast(I32), 0)
-            nc.vector.memset(x_centre[j][:].bitcast(I32), 0)
-            nc.vector.memset(x_offset[j][:].bitcast(I32), 0)
-        nc.vector.memset(x_grouped[0][:, :, 0:4, :], 0.0)
-        nc.vector.memset(x_grouped[2][:, :, COLS - 4 : COLS, :], 0.0)
+        x_grouped = consts.tile([P, ROWS, COLS, PACK], BF16, align_bytes=64)
+        x_sets = []
+        for s in range(2):
+            codes = [consts.tile([P, COLS + PIXELS + COLS], U32, name="x_codes%d_%d" % (s, j), align_bytes=64) for j in range(KS)]
+            centre = [consts.tile([P, PIXELS], U8, name="x_centre%d_%d" % (s, j), align_bytes=64) for j in range(KS)]
+            offset = [consts.tile([P, COLS + PIXELS + COLS], U8, name="x_offset%d_%d" % (s, j), align_bytes=64) for j in range(KS)]
+            for j in range(KS):
+                nc.gpsimd.memset(codes[j][:].bitcast(F32), 0.0)
+                nc.gpsimd.memset(centre[j][:].bitcast(F32), 0.0)
+                nc.gpsimd.memset(offset[j][:].bitcast(F32), 0.0)
+            x_sets.append((codes, centre, offset))
 
         def load_image(b):
-            x_raw = stage.tile([P, PACK, ROWS, COLS], BF16)
+            x_raw = images.tile([P, PACK, ROWS, COLS], BF16)
             nc.sync.dma_start(out=x_raw[:], in_=image[b].rearrange("(p r) h w -> p r h w", r=PACK))
             return x_raw
 
-        def regroup_views(x_raw, j, row0, n_rows):
-            shift = j - 1
-            lo = max(0, -shift)
-            hi = COLS - max(0, shift)
-            dst = x_grouped[j][:, row0 : row0 + n_rows, lo:hi, :]
-            src = x_raw[:, :, row0 : row0 + n_rows, lo + shift : hi + shift].rearrange("p r h w -> p h w r")
+        def regroup_views(x_raw, row0, n_rows):
+            dst = x_grouped[:, row0 : row0 + n_rows, :, :]
+            src = x_raw[:, :, row0 : row0 + n_rows, :].rearrange("p r h w -> p h w r")
             return dst, src
 
-        def quantise_image():
-            for j in range(KS):
+        def columns(ap, lo, hi):
+            return ap.rearrange("p (h w) -> p h w", w=COLS)[:, :, lo:hi]
+
+        def input_work(b, number):
+            codes, centre, offset = x_sets[b % 2]
+            words = [codes[j][:, COLS : COLS + PIXELS].bitcast(I32) for j in range(KS)]
+            if number == 0:
                 nc.vector.quantize_mx(
-                    out=x_codes[j][:, COLS : COLS + PIXELS].bitcast(FP8X4),
-                    scales=x_centre[j][:],
-                    in_=x_grouped[j][:].rearrange("p h w r -> p (h w r)"),
+                    out=codes[1][:, COLS : COLS + PIXELS].bitcast(FP8X4),
+                    scales=centre[1][:],
+                    in_=x_grouped[:].rearrange("p h w r -> p (h w r)"),
                 )
-            for j in range(KS):
-                nc.vector.tensor_copy(
-                    out=x_offset[j][:, COLS : COLS + PIXELS].bitcast(I32), in_=x_centre[j][:].bitcast(I32)
-                )
-
-        def x_window(first_row, t):
-            i, j = divmod(t, KS)
-            start = COLS * (first_row + i)
-            codes = x_codes[j][:, start : start + P].bitcast(FP8X4)
-            if i == 1:
-                scales = x_centre[j][:, start - COLS : start - COLS + P]
+            elif number == 1:
+                nc.vector.tensor_copy(out=columns(words[0], 1, COLS), in_=columns(words[1], 0, COLS - 1))
+                nc.vector.tensor_copy(out=columns(words[2], 0, COLS - 1), in_=columns(words[1], 1, COLS))
+            elif number == 2:
+                nc.vector.tensor_copy(out=columns(centre[0][:], 1, COLS), in_=columns(centre[1][:], 0, COLS - 1))
+                nc.vector.tensor_copy(out=columns(centre[2][:], 0, COLS - 1), in_=columns(centre[1][:], 1, COLS))
             else:
-                scales = x_offset[j][:, start : start + P]
-            return codes, scales
+                for j in range(KS):
+                    nc.vector.tensor_copy(
+                        out=offset[j][:, COLS : COLS + PIXELS].bitcast(I32), in_=centre[j][:].bitcast(I32)
+                    )
 
-        x_raw = load_image(0)
+        def x_window(group, t):
+            i, j = divmod(t, KS)
+            b, part = divmod(group, GROUPS_PER_IMAGE)
+            codes, centre, offset = x_sets[b % 2]
+            start = COLS * (GROUP_ROWS * part + i)
+            words = codes[j][:, start : start + GROUP_PIXELS].bitcast(FP8X4)
+            if i == 1:
+                scales = centre[j][:, start - COLS : start - COLS + GROUP_PIXELS]
+            else:
+                scales = offset[j][:, start : start + GROUP_PIXELS]
+            return words, scales
+
+        raws = {0: load_image(0)}
+        w_codes = consts.tile([P, TAPS + 1, FEATURES], U32, align_bytes=64)
+        w_scales = consts.tile([P, TAPS + 1, FEATURES], U8, align_bytes=64)
+        bias_bf = consts.tile([P, TAPS * HALVES], BF16)
         w_rows = weight.rearrange("a b c i j (p r) n -> p (a b c i j) r n", r=PACK)
-        w_codes = consts.tile([P, TAPS, FEATURES], U32, align_bytes=64)
-        w_scales = consts.tile([P, TAPS, FEATURES], U8, align_bytes=64)
-        w_raws = []
-        for i in range(KS):
-            w_raw = stage.tile([P, KS, PACK, FEATURES], BF16, bufs=KS)
-            nc.sync.dma_start(out=w_raw[:], in_=w_rows[:, KS * i : KS * (i + 1), :, :])
-            w_raws.append(w_raw)
-        bias_bf = consts.tile([P, PASSES], BF16)
-        with nc.allow_non_contiguous_dma(reason="2304 bias values, one to a partition, once"):
-            nc.sync.dma_start(out=bias_bf[:], in_=bias.rearrange("a b c i j o (g f) -> f (a b c i j o g)", g=HALVES))
-
-        for j in range(KS):
-            dst, src = regroup_views(x_raw, j, 0, ROWS)
+        with tc.tile_pool(name="head", bufs=1) as head:
+            w_raws = []
+            for i in range(KS):
+                w_raw = head.tile([P, KS, PACK, FEATURES], BF16, bufs=KS)
+                nc.sync.dma_start(out=w_raw[:], in_=w_rows[:, KS * i : KS * (i + 1), :, :])
+                w_raws.append(w_raw)
+            with nc.allow_non_contiguous_dma(reason="2304 bias values, one to a partition, once"):
+                nc.sync.dma_start(out=bias_bf[:], in_=bias.rearrange("a b c i j o (g f) -> f (a b c i j o g)", g=HALVES))
+            dst, src = regroup_views(raws[0], 0, ROWS)
             nc.vector.tensor_copy(out=dst, in_=src)
-        w_groupeds = []
-        for t in range(TAPS):
-            w_grouped = stage.tile([P, FEATURES, PACK], BF16, align_bytes=64, bufs=TAPS)
-            nc.scalar.copy(out=w_grouped[:], in_=w_raws[t // KS][:, t % KS, :, :].rearrange("p r n -> p n r"))
-            w_groupeds.append(w_grouped)
-        quantise_image()
-        for t in range(TAPS):
+            w_groupeds = []
+            for t in range(TAPS):
+                w_grouped = head.tile([P, FEATURES, PACK], BF16, align_bytes=64, bufs=TAPS)
+                w_groupeds.append(w_grouped)
+
+            def regroup_weights(t, copy):
+                copy(out=w_groupeds[t][:], in_=w_raws[t // KS][:, t % KS, :, :].rearrange("p r n -> p n r"))
+
+            def quantise_weights(t):
+                nc.vector.quantize_mx(
+                    out=w_codes[:, t, :].bitcast(FP8X4),
+                    scales=w_scales[:, t, :],
+                    in_=w_groupeds[t][:].rearrange("p n r -> p (n r)"),
+                )
+
+            for t in (0, 1, 3, 5, 7):
+                regroup_weights(t, nc.scalar.copy)
+            for number in range(INPUT_WORKS):
+                input_work(0, number)
+            for t in (REF, 2, 4, 6):
+                regroup_weights(t, nc.vector.tensor_copy)
+            for t in range(TAPS):
+                quantise_weights(t)
+            w_negated = head.tile([P, FEATURES, PACK], BF16, align_bytes=64)
+            nc.vector.tensor_scalar_mul(out=w_negated[:], in0=w_groupeds[REF][:], scalar1=-1.0)
             nc.vector.quantize_mx(
-                out=w_codes[:, t, :].bitcast(FP8X4),
-                scales=w_scales[:, t, :],
-                in_=w_groupeds[t][:].rearrange("p n r -> p (n r)"),
+                out=w_codes[:, NEG_REF, :].bitcast(FP8X4),
+                scales=w_scales[:, NEG_REF, :],
+                in_=w_negated[:].rearrange("p n r -> p (n r)"),
             )
+        raws[1] = load_image(1)
 
         bias_cols = consts.tile([P, TAPS, HALVES], F32)
         nc.vector.tensor_copy(out=bias_cols[:].rearrange("p t g -> p (t g)"), in_=bias_bf[:])
-        bias_mean = consts.tile([P, HALVES], F32)
-        nc.vector.tensor_reduce(out=bias_mean[:], in_=bias_cols[:].rearrange("p t g -> p g t"), axis=AXIS_X, op=ALU.add)
-        nc.vector.tensor_scalar_mul(out=bias_mean[:], in0=bias_mean[:], scalar1=1.0 / TAPS)
-        bias_rel = consts.tile([P, TAPS, HALVES], F32)
+        bias_rel = consts.tile([P, REF, HALVES], F32)
         nc.vector.tensor_tensor(
-            out=bias_rel[:], in0=bias_cols[:], in1=bias_mean[:].unsqueeze(1).to_broadcast([P, TAPS, HALVES]), op=ALU.subtract
+            out=bias_rel[:],
+            in0=bias_cols[:, 0:REF, :],
+            in1=bias_cols[:, REF : REF + 1, :].to_broadcast([P, REF, HALVES]),
+            op=ALU.subtract,
         )
+        bias_start = consts.tile([P, HALVES], F32)
+        nc.vector.tensor_reduce(out=bias_start[:], in_=bias_rel[:].rearrange("p t g -> p g t"), axis=AXIS_X, op=ALU.add)
+        nc.vector.tensor_scalar_mul(out=bias_start[:], in0=bias_start[:], scalar1=1.0 / TAPS)
 
-        blocks = {}
+        group_pool = ctx.enter_context(tc.tile_pool(name="group", bufs=2))
+        block_pool = ctx.enter_context(tc.tile_pool(name="block", bufs=2 * LIVE))
+        work_pool = ctx.enter_context(tc.tile_pool(name="work", bufs=2))
+        item_pool = ctx.enter_context(tc.tile_pool(name="item", bufs=4))
+        groups = {}
         banks = {}
 
-        def issue(tick, pool):
-            block, part = divmod(tick, TICKS_PER_BLOCK)
-            first_row = BLOCK_ROWS * (block % BLOCKS_PER_IMAGE)
-            if part == 0:
-                pri_a = block_pool.tile([P, PASSES, P], F32)
-                o_first = block_pool.tile([P, FEATURES], F32)
-                blocks[block] = (pri_a, o_first)
-            bank = pool.tile([P, PASSES_PER_TICK + 1, P], F32, tag="bank")
-            banks[tick] = bank
-            for s in range(PASSES_PER_TICK):
-                t, half = divmod(PASSES_PER_TICK * part + s, HALVES)
-                feats = slice(half * P, (half + 1) * P)
-                codes, scales = x_window(first_row, t)
-                nc.tensor.matmul_mx(
-                    out=bank[:, s, :],
-                    lhsT=w_codes[:, t, feats].bitcast(FP8X4),
-                    lhsT_scale=w_scales[:, t, feats],
-                    rhs=codes,
-                    rhs_scale=scales,
-                    start=True,
-                    stop=True,
-                )
-            if part < HALVES:
-                feats = slice(part * P, (part + 1) * P)
-                for t in range(TAPS):
-                    codes, scales = x_window(first_row, t)
-                    nc.tensor.matmul_mx(
-                        out=bank[:, PASSES_PER_TICK, :],
-                        lhsT=codes,
-                        lhsT_scale=scales,
-                        rhs=w_codes[:, t, feats].bitcast(FP8X4),
-                        rhs_scale=w_scales[:, t, feats],
-                        start=(t == 0),
-                        stop=(t == TAPS - 1),
-                    )
+        def begin_group(group):
+            ref_T = group_pool.tile([P, HALVES, GROUP_PIXELS], F32)
+            start_T = group_pool.tile([P, HALVES, GROUP_PIXELS], F32)
+            groups[group] = {"ref_T": ref_T, "start_T": start_T, "u_pix": [], "taps_T": {}}
 
-        def collect(tick, by_vector=False):
-            block, part = divmod(tick, TICKS_PER_BLOCK)
-            pri_a, o_first = blocks[block]
-            bank = banks[tick]
-            for s in range(PASSES_PER_TICK):
-                k = PASSES_PER_TICK * part + s
-                t, half = divmod(k, HALVES)
-                if by_vector:
-                    nc.vector.tensor_scalar_add(out=pri_a[:, k, :], in0=bank[:, s, :], scalar1=bias_rel[:, t, half : half + 1])
+        def product(group, bank, t_x, w_place, half, start, stop):
+            feats = slice(half * P, (half + 1) * P)
+            words, scales = x_window(group, t_x)
+            nc.tensor.matmul_mx(
+                out=bank,
+                lhsT=w_codes[:, w_place, feats].bitcast(FP8X4),
+                lhsT_scale=w_scales[:, w_place, feats],
+                rhs=words,
+                rhs_scale=scales,
+                start=start,
+                stop=stop,
+            )
+
+        def empty(dst, src, bias_col, by_vector):
+            if by_vector:
+                nc.vector.tensor_scalar_add(out=dst, in0=src, scalar1=bias_col)
+            else:
+                nc.scalar.activation(out=dst, in_=src, func=ACT.Identity, bias=bias_col)
+
+        TAP_UNITS = [("tap", t, h) for t in range(REF) for h in range(HALVES)]
+        REF_UNITS = [("ref", 0, h) for h in range(HALVES)]
+        MEAN_UNITS = [("mean", t, h) for h in range(HALVES) for t in range(REF)]
+        TURN_UNITS = [("turn", pair, j) for j in range(LIVE) for pair in range(PAIRS)]
+
+        def issue(pool, depth, group, kind, a, k):
+            g = groups[group]
+            if kind == "mean":
+                if a == 0:
+                    sum_bank = pool.tile([P, GROUP_PIXELS], F32, tag="sum", bufs=depth["sum"])
+                    banks[group, kind, k] = sum_bank
+                bank = banks[group, kind, k]
+                product(group, bank[:], a, a, k, a == 0, False)
+                product(group, bank[:], REF, NEG_REF, k, False, a == REF - 1)
+                return
+            if kind == "turn":
+                bank = pool.tile([P, 2, FEATURES], F32, tag="turned", bufs=depth["turned"])
+                for tt in range(2):
+                    for h in range(HALVES):
+                        nc.tensor.transpose(
+                            bank[:, tt, h * P : (h + 1) * P], g["taps_T"][a][:, 2 * tt + h, k * P : (k + 1) * P], ident[:]
+                        )
+            else:
+                bank = pool.tile([P, GROUP_PIXELS], F32, tag="made", bufs=depth["made"])
+                if kind == "ref":
+                    product(group, bank[:], REF, REF, k, True, True)
                 else:
+                    product(group, bank[:], a, a, k, True, False)
+                    product(group, bank[:], REF, NEG_REF, k, False, True)
+            banks[group, kind, a, k] = bank
+
+        def collect(group, kind, a, k, by_vector=False):
+            g = groups[group]
+            if kind == "mean":
+                if a == REF - 1:
                     nc.scalar.activation(
-                        out=pri_a[:, k, :], in_=bank[:, s, :], func=ACT.Identity, bias=bias_rel[:, t, half : half + 1]
+                        out=g["start_T"][:, k, :],
+                        in_=banks[group, kind, k][:],
+                        func=ACT.Identity,
+                        bias=bias_start[:, k : k + 1],
+                        scale=1.0 / TAPS,
                     )
-            if part < HALVES:
-                mean = o_first[:, part * P : (part + 1) * P]
+                return
+            bank = banks[group, kind, a, k]
+            if kind == "ref":
+                empty(g["ref_T"][:, k, :], bank[:], bias_cols[:, REF, k : k + 1], by_vector)
+            elif kind == "tap":
+                pair, tt = divmod(a, 2)
+                if tt == 0 and k == 0:
+                    taps_T = group_pool.tile([P, 2 * HALVES, GROUP_PIXELS], F32, bufs=PAIRS)
+                    g["taps_T"][pair] = taps_T
+                empty(g["taps_T"][pair][:, 2 * tt + k, :], bank[:], bias_rel[:, a, k : k + 1], by_vector)
+            else:
+                if a == 0:
+                    u = block_pool.tile([P, REF, FEATURES], F32)
+                    g["u_pix"].append(u)
+                dst = g["u_pix"][k][:, 2 * a : 2 * a + 2, :]
                 if by_vector:
-                    nc.vector.tensor_scalar_mul(out=mean, in0=bank[:, PASSES_PER_TICK, :], scalar1=1.0 / TAPS)
+                    nc.vector.tensor_copy(out=dst, in_=bank[:])
                 else:
-                    nc.scalar.mul(out=mean, in_=bank[:, PASSES_PER_TICK, :], mul=1.0 / TAPS)
+                    nc.scalar.copy(out=dst, in_=bank[:])
 
-        with tc.psum_pool(name="early", bufs=EARLY_BANKS) as early:
-            for tick in range(AHEAD + EARLY_BANKS):
-                if tick >= EARLY_BANKS:
-                    collect(tick - EARLY_BANKS, by_vector=(tick % 2 == 1))
-                if tick < AHEAD:
-                    issue(tick, early)
-        issue(AHEAD, transit)
-
-        pri_pool = ctx.enter_context(tc.psum_pool(name="pri", bufs=1))
-        tap8 = pri_pool.tile([P, 2, HALVES, P], F32, name="tap8", tag="tap8")
-        last_tap = {}
-        loaded = {}
-        routes = {}
+        items = {}
 
         def item(n):
-            group, rest = divmod(n, GROUP_ITEMS)
-            it, rest = divmod(rest, LIVE * HALVES)
-            member, half = divmod(rest, HALVES)
-            block = LIVE * group + member
-            if n < 0 or block >= N_BLOCKS:
+            if n < 0 or n >= N_ITEMS:
                 return None
-            return block, it, half
+            group, rest = divmod(n, GROUP_ITEMS)
+            it, j = divmod(rest, LIVE)
+            return group, it, j
 
-        def load_priors(n):
-            who = item(n)
-            if who is None:
-                return
-            block, it, half = who
-            pri_a = blocks[block][0]
-            slot = n % SLOTS
-            quad0 = pri_pool.tile([P, QUAD, P], F32, name="quad0_%d" % slot, tag="quad0_%d" % slot)
-            quad1 = pri_pool.tile([P, QUAD, P], F32, name="quad1_%d" % slot, tag="quad1_%d" % slot)
-            if half == HALVES - 1:
-                place = (n // HALVES) % 2
-                for g in range(HALVES):
-                    nc.tensor.transpose(tap8[:, place, g, :], pri_a[:, HALVES * 2 * QUAD + g, :], ident[:])
-                last_tap[n - 1] = tap8[:, place, :, :]
-            pieces = [(quad0[:], 0, QUAD), (quad1[:], QUAD, QUAD)]
-            for pri, tap0, n_taps in pieces:
-                for u in range(n_taps):
-                    nc.tensor.transpose(pri[:, u, :], pri_a[:, HALVES * (tap0 + u) + half, :], ident[:])
-            loaded[n] = pieces
-
-        def start_iteration(block, it):
-            if it == 0:
-                work = work_pool.tile([P, TAPS, FEATURES], F32)
-                pri_last = work_pool.tile([P, FEATURES], F32)
-                routes[block] = {"work": work, "o": blocks[block][1][:], "pri_last": pri_last}
-            dist = item_pool.tile([P, TAPS, HALVES * HALF_CAPS], F32)
-            cw = item_pool.tile([P, TAPS, HALVES * HALF_CAPS], F32)
-            cw_sum = item_pool.tile([P, HALVES * HALF_CAPS], F32)
-            routes[block]["dist"] = dist
-            routes[block]["cw"] = cw
-            routes[block]["cw_sum"] = cw_sum
-
-        def subtract(rt, half, pieces):
-            feats = slice(half * P, (half + 1) * P)
-            for pri, tap0, n_taps in pieces:
-                nc.vector.tensor_tensor(
-                    out=rt["work"][:, tap0 : tap0 + n_taps, feats],
-                    in0=pri,
-                    in1=rt["o"][:, feats].unsqueeze(1).to_broadcast([P, n_taps, P]),
-                    op=ALU.subtract,
-                )
-
-        def subtract_last(rt, pri):
-            nc.vector.tensor_tensor(
-                out=rt["work"][:, TAPS - 1, :], in0=pri.rearrange("p g f -> p (g f)"), in1=rt["o"], op=ALU.subtract
-            )
-
-        def keep_last(rt, pri):
-            nc.scalar.copy(out=rt["pri_last"][:].rearrange("p (g f) -> p g f", g=HALVES), in_=pri)
-
-        def multiply_last(rt, pri, half):
-            nc.vector.tensor_tensor(
-                out=rt["work"][:, TAPS - 1, half * P : (half + 1) * P].rearrange("p (c k) -> p c k", k=CAP_CH),
-                in0=pri[:, half, :].rearrange("p (c k) -> p c k", k=CAP_CH),
-                in1=rt["cw"][:, TAPS - 1, half * HALF_CAPS : (half + 1) * HALF_CAPS]
-                .unsqueeze(2)
-                .to_broadcast([P, HALF_CAPS, CAP_CH]),
-                op=ALU.mult,
-            )
-
-        def square(rt, half, tap0, n_taps):
-            diff = rt["work"][:, tap0 : tap0 + n_taps, half * P : (half + 1) * P]
-            nc.scalar.activation(out=diff, in_=diff, func=ACT.Square)
-
-        def sum_channels(rt, half, tap0, n_taps):
-            nc.vector.tensor_reduce(
-                out=rt["dist"][:, tap0 : tap0 + n_taps, half * HALF_CAPS : (half + 1) * HALF_CAPS],
-                in_=rt["work"][:, tap0 : tap0 + n_taps, half * P : (half + 1) * P].rearrange("p t (c k) -> p t c k", k=CAP_CH),
-                axis=AXIS_X,
-                op=ALU.add,
-            )
-
-        def inverse_root(rt, half):
-            for cap in range(half * HALF_CAPS, (half + 1) * HALF_CAPS):
-                nc.scalar.activation(
-                    out=rt["cw"][:, :, cap],
-                    in_=rt["dist"][:, :, cap],
-                    func=ACT.Abs_reciprocal_sqrt,
-                    bias=EPS,
-                    accum_out=rt["cw_sum"][:, cap : cap + 1],
-                )
-
-        def multiply(rt, half, pieces):
-            for pri, tap0, n_taps in pieces:
-                nc.vector.tensor_tensor(
-                    out=rt["work"][:, tap0 : tap0 + n_taps, half * P : (half + 1) * P].rearrange("p t (c k) -> p t c k", k=CAP_CH),
-                    in0=pri.rearrange("p t (c k) -> p t c k", k=CAP_CH),
-                    in1=rt["cw"][:, tap0 : tap0 + n_taps, half * HALF_CAPS : (half + 1) * HALF_CAPS]
-                    .unsqueeze(3)
-                    .to_broadcast([P, n_taps, HALF_CAPS, CAP_CH]),
-                    op=ALU.mult,
-                )
-
-        def invert_sum(rt):
-            cw_inv = item_pool.tile([P, HALVES * HALF_CAPS], F32)
-            nc.scalar.activation(out=cw_inv[:], in_=rt["cw_sum"][:], func=ACT.Abs_reciprocal_sqrt)
-            nc.scalar.activation(out=cw_inv[:], in_=cw_inv[:], func=ACT.Square)
-            rt["cw_inv"] = cw_inv
-
-        def sum_taps(rt, goes_on):
-            work = rt["work"]
-            nc.gpsimd.tensor_tensor(out=work[:, 0:4, :], in0=work[:, 0:4, :], in1=work[:, 4:8, :], op=ALU.add)
-            nc.gpsimd.tensor_tensor(out=work[:, 0:2, :], in0=work[:, 0:2, :], in1=work[:, 2:4, :], op=ALU.add)
-            nc.gpsimd.tensor_tensor(out=work[:, 0, :], in0=work[:, 0, :], in1=work[:, 1, :], op=ALU.add)
-            nc.gpsimd.tensor_tensor(out=work[:, 0, :], in0=work[:, 0, :], in1=work[:, 8, :], op=ALU.add)
-            o_next = item_pool.tile([P, FEATURES], F32)
-            nc.gpsimd.tensor_tensor(
-                out=o_next[:].rearrange("p (c k) -> p c k", k=CAP_CH),
-                in0=work[:, 0, :].rearrange("p (c k) -> p c k", k=CAP_CH),
-                in1=rt["cw_inv"][:].unsqueeze(2).to_broadcast([P, HALVES * HALF_CAPS, CAP_CH]),
-                op=ALU.mult,
-            )
-            rt["o"] = o_next[:]
-            if goes_on:
-                nc.gpsimd.tensor_tensor(out=work[:, TAPS - 1, :], in0=rt["pri_last"][:], in1=o_next[:], op=ALU.subtract)
-
-        def sum_taps_at_the_end(rt):
-            summed = item_pool.tile([P, FEATURES], F32)
-            nc.vector.tensor_reduce(out=summed[:], in_=rt["work"][:].rearrange("p t f -> p f t"), axis=AXIS_X, op=ALU.add)
-            o_last = item_pool.tile([P, FEATURES], F32)
-            nc.vector.tensor_tensor(
-                out=o_last[:].rearrange("p (c k) -> p c k", k=CAP_CH),
-                in0=summed[:].rearrange("p (c k) -> p c k", k=CAP_CH),
-                in1=rt["cw_inv"][:].unsqueeze(2).to_broadcast([P, HALVES * HALF_CAPS, CAP_CH]),
-                op=ALU.mult,
-            )
-            rt["o"] = o_last[:]
-
-        def prepare_input(tick):
-            b, pos = divmod(tick, TICKS_PER_IMAGE)
-            first = TICKS_PER_IMAGE - SLICES
-            if b + 1 >= IMAGES or pos < first - 1:
-                return
-            if pos == first - 1:
-                raws[b + 1] = load_image(b + 1)
-                return
-            j, part = divmod(pos - first, ROWS // REGROUP_ROWS)
-            dst, src = regroup_views(raws[b + 1], j, REGROUP_ROWS * part, REGROUP_ROWS)
-            nc.scalar.copy(out=dst, in_=src)
-
-        raws = {}
-        N_TICKS = N_BLOCKS * TICKS_PER_BLOCK
-        LEAVE_AFTER = 5
-
-        load_priors(0)
-        load_priors(1)
-
-        for n in range(N_ITEMS + LEAVE_AFTER + 1):
-            measure = item(n)
-            weigh = item(n - 1)
-            ends = item(n - 2)
-            left = item(n - LEAVE_AFTER)
-            tick = n + AHEAD
-
-            if measure:
-                block, it, half = measure
-                if half == 0:
-                    start_iteration(block, it)
-                subtract(routes[block], half, loaded[n])
-                if half == 0 and it == 0:
-                    subtract_last(routes[block], last_tap[n])
-                square(routes[block], half, 0, QUAD)
-                square(routes[block], half, QUAD, TAPS - QUAD)
-            block_done = ends and ends[2] == HALVES - 1
-            if ends:
-                multiply_last(routes[ends[0]], last_tap[n - 2 - ends[2]], ends[2])
-            if weigh:
-                multiply(routes[weigh[0]], weigh[2], loaded[n - 1])
-            if tick < N_TICKS:
-                collect(tick)
-            if measure and half == 0 and it == 0:
-                keep_last(routes[block], last_tap[n])
-            out_ps = None
-            if left and left[1] == ITERATIONS - 1 and left[2] == HALVES - 1:
-                out_ps = transit.tile([P, HALVES, P], F32, tag="bank")
-                for g in range(HALVES):
-                    nc.tensor.transpose(out_ps[:, g, :], routes[left[0]]["o"][:, g * P : (g + 1) * P], ident[:])
-            load_priors(n + SLOTS - 1)
-            if weigh and weigh[2] == HALVES - 1:
-                invert_sum(routes[weigh[0]])
-            if out_ps is not None:
-                b, blk = divmod(left[0], BLOCKS_PER_IMAGE)
-                out_sb = item_pool.tile([P, HALVES, P], F32)
-                for g in range(HALVES):
-                    nc.scalar.activation(
-                        out=out_sb[:, g, :], in_=out_ps[:, g, :], func=ACT.Identity, bias=bias_mean[:, g : g + 1]
+        def sum_taps(n):
+            total = psum.tile([P, HALVES, P], F32, tag="total", bufs=1)
+            wp = items[n]["weighted"]
+            for h in range(HALVES):
+                for t in range(REF):
+                    nc.tensor.matmul(
+                        total[:, h, :],
+                        lhsT=wp[:, t, h * P : (h + 1) * P],
+                        rhs=ident[:],
+                        is_transpose=True,
+                        start=(t == 0),
+                        stop=(t == REF - 1),
                     )
-                nc.sync.dma_start(
-                    out=out[b].rearrange("(g f) h w -> f g (h w)", g=HALVES)[:, :, blk * P : (blk + 1) * P], in_=out_sb[:]
-                )
-            if tick < N_TICKS:
-                prepare_input(tick)
-            if measure:
-                sum_channels(routes[block], half, 0, QUAD)
-                sum_channels(routes[block], half, QUAD, TAPS - QUAD)
-                inverse_root(routes[block], half)
-            if block_done:
-                if ends[0] == N_BLOCKS - 1 and ends[1] == ITERATIONS - 1:
-                    sum_taps_at_the_end(routes[ends[0]])
-                else:
-                    sum_taps(routes[ends[0]], goes_on=ends[1] < ITERATIONS - 1)
+            items[n]["total"] = total
 
-            if tick + 1 < N_TICKS:
-                if (tick + 1) % TICKS_PER_IMAGE == 0:
-                    quantise_image()
-                issue(tick + 1, transit)
+        def keep_total(n):
+            total_T = item_pool.tile([P, HALVES, P], F32)
+            nc.scalar.copy(out=total_T[:], in_=items[n]["total"][:])
+            items[n]["total_T"] = total_T
+
+        def leave(n):
+            group, it, j = item(n)
+            out_sb = item_pool.tile([P, HALVES, P], F32)
+            nc.vector.tensor_tensor(
+                out=out_sb[:], in0=items[n]["total"][:], in1=groups[group]["ref_T"][:, :, j * P : (j + 1) * P], op=ALU.add
+            )
+            b, part = divmod(group, GROUPS_PER_IMAGE)
+            first = GROUP_PIXELS * part + j * P
+            nc.sync.dma_start(
+                out=out[b].rearrange("(g f) h w -> f g (h w)", g=HALVES)[:, :, first : first + P], in_=out_sb[:]
+            )
+
+        def turn_output(n):
+            group, it, j = item(n)
+            o = psum.tile([P, FEATURES], F32, tag="o")
+            for h in range(HALVES):
+                if it == 0:
+                    src = groups[group]["start_T"][:, h, j * P : (j + 1) * P]
+                else:
+                    src = items[n - LIVE]["total_T"][:, h, :]
+                nc.tensor.transpose(o[:, h * P : (h + 1) * P], src, ident[:])
+            items[n] = {"o": o}
+
+        def subtract(n):
+            group, it, j = item(n)
+            d = work_pool.tile([P, TAPS, FEATURES], F32)
+            items[n]["d"] = d
+            nc.vector.tensor_tensor(
+                out=d[:, 0:REF, :],
+                in0=groups[group]["u_pix"][j][:],
+                in1=items[n]["o"][:].unsqueeze(1).to_broadcast([P, REF, FEATURES]),
+                op=ALU.subtract,
+            )
+
+        def square(n):
+            d = items[n]["d"]
+            nc.scalar.activation(out=d[:, REF, :], in_=items[n]["o"][:], func=ACT.Square)
+            nc.scalar.activation(out=d[:, 0:REF, :], in_=d[:, 0:REF, :], func=ACT.Square)
+
+        def sum_channels(n):
+            dist = item_pool.tile([P, TAPS, CAPS], F32)
+            items[n]["dist"] = dist
+            nc.vector.tensor_reduce(
+                out=dist[:], in_=items[n]["d"][:].rearrange("p t (c k) -> p t c k", k=CAP_CH), axis=AXIS_X, op=ALU.add
+            )
+
+        def inverse_root(n):
+            cw = item_pool.tile([P, TAPS, CAPS], F32)
+            items[n]["cw"] = cw
+            nc.scalar.activation(out=cw[:], in_=items[n]["dist"][:], func=ACT.Abs_reciprocal_sqrt, bias=EPS)
+
+        def sum_weights(n):
+            cw_sum = item_pool.tile([P, CAPS], F32)
+            items[n]["cw_sum"] = cw_sum
+            nc.vector.tensor_reduce(out=cw_sum[:], in_=items[n]["cw"][:].rearrange("p t c -> p c t"), axis=AXIS_X, op=ALU.add)
+
+        def invert_sum(n):
+            cw_inv = item_pool.tile([P, CAPS], F32)
+            items[n]["cw_inv"] = cw_inv
+            nc.vector.reciprocal(out=cw_inv[:], in_=items[n]["cw_sum"][:])
+
+        def normalise(n):
+            share = item_pool.tile([P, REF, CAPS], F32)
+            items[n]["share"] = share
+            nc.gpsimd.tensor_tensor(
+                out=share[:],
+                in0=items[n]["cw"][:, 0:REF, :],
+                in1=items[n]["cw_inv"][:].unsqueeze(1).to_broadcast([P, REF, CAPS]),
+                op=ALU.mult,
+            )
+
+        def multiply(engine, n, tap0, n_taps):
+            group, it, j = item(n)
+            engine.tensor_tensor(
+                out=items[n]["weighted"][:, tap0 : tap0 + n_taps, :].rearrange("p t (c k) -> p t c k", k=CAP_CH),
+                in0=groups[group]["u_pix"][j][:, tap0 : tap0 + n_taps, :].rearrange("p t (c k) -> p t c k", k=CAP_CH),
+                in1=items[n]["share"][:, tap0 : tap0 + n_taps, :].unsqueeze(3).to_broadcast([P, n_taps, CAPS, CAP_CH]),
+                op=ALU.mult,
+            )
+
+        def begin_weighted(n):
+            weighted = work_pool.tile([P, REF, FEATURES], F32)
+            items[n]["weighted"] = weighted
+
+        IMAGE_STEPS = GROUP_ITEMS * GROUPS_PER_IMAGE
+        slices_at = {}
+        works_at = {}
+        for b in range(1, IMAGES):
+            work0 = IMAGE_STEPS * (b - 1) + GROUP_ITEMS - 2 - INPUT_WORKS
+            for number in range(INPUT_WORKS):
+                works_at[work0 + number] = (b, number)
+            for number in range(SLICES):
+                at = work0 - 1 - number if b > 1 else work0 - 1 - number // 2
+                slices_at.setdefault(at, []).append((b, SLICES - 1 - number))
+
+        row = [([(0,) + unit], k % 2 == 1) for k, unit in enumerate(TAP_UNITS + MEAN_UNITS + TURN_UNITS[0:PAIRS])]
+        head_slots = len(row)
+        row += [([(0,) + u], k % 2 == 1) for k, u in enumerate(TURN_UNITS[PAIRS:])]
+        fill_slots = len(row)
+        row_end = [0]
+        for group in range(1, N_GROUPS):
+            units = [[u] for u in TAP_UNITS + REF_UNITS] + [[m, u] for m, u in zip(MEAN_UNITS, TURN_UNITS)]
+            if group == 1:
+                row += [([(0,) + u], False) for u in REF_UNITS]
+            row += [([(group,) + u for u in slot], False) for slot in units]
+            row_end.append(len(row))
+        begun = [0]
+
+        def next_slot(pool, depth):
+            at = begun[0]
+            begun[0] += 1
+            if at < len(row):
+                for unit in row[at][0]:
+                    if unit[0] not in groups:
+                        begin_group(unit[0])
+                    issue(pool, depth, *unit)
+            if at > 0 and at != head_slots:
+                for unit in row[at - 1][0]:
+                    collect(*unit, by_vector=row[at - 1][1])
+
+        def slots_in(s):
+            if s == 0:
+                return fill_slots - head_slots
+            ready = row_end[min((s + 1) // GROUP_ITEMS + 1, N_GROUPS - 1)]
+            if ready == len(row):
+                ready += 1
+            return min(SLOTS_PER_STEP + (1 if s < GROUP_ITEMS else 0), ready - begun[0])
+
+        with tc.psum_pool(name="early", bufs=2) as early:
+            for k in range(head_slots):
+                next_slot(early, EARLY_DEPTH)
+            for unit in row[head_slots - 1][0]:
+                collect(*unit, by_vector=row[head_slots - 1][1])
+        psum = ctx.enter_context(tc.psum_pool(name="psum", bufs=2))
+        turn_output(0)
+
+        def slots(n):
+            for k in range(n):
+                next_slot(psum, DEPTH)
+
+        for s in range(N_ITEMS + 3):
+            ends = item(s - 3)
+            if ends:
+                sum_taps(s - 3)
+            n_slots = slots_in(s)
+            slots(n_slots // 3)
+            if ends and ends[1] < ITERATIONS - 1:
+                keep_total(s - 3)
+            if item(s + 1):
+                turn_output(s + 1)
+            slots(n_slots // 3)
+            if item(s):
+                subtract(s)
+            if ends and ends[1] == ITERATIONS - 1:
+                leave(s - 3)
+            if item(s):
+                square(s)
+            if item(s - 1):
+                sum_channels(s - 1)
+                inverse_root(s - 1)
+            if item(s - 2):
+                begin_weighted(s - 2)
+                for tap0 in range(0, G_TAPS, 2):
+                    multiply(nc.gpsimd, s - 2, tap0, 2)
+                multiply(nc.vector, s - 2, G_TAPS, REF - G_TAPS)
+            slots(n_slots - 2 * (n_slots // 3))
+            if s in works_at:
+                input_work(*works_at[s])
+            if item(s - 1):
+                sum_weights(s - 1)
+                invert_sum(s - 1)
+                normalise(s - 1)
+            for b, number in slices_at.get(s, []):
+                dst, src = regroup_views(raws[b], REGROUP_ROWS * number, REGROUP_ROWS)
+                nc.scalar.copy(out=dst, in_=src)
+                if number == SLICES - 1 and b + 1 < IMAGES:
+                    raws[b + 1] = load_image(b + 1)

@@ -35,13 +35,18 @@ GROUPS_PER_IMAGE = PIXELS // GROUP_PIXELS
 N_GROUPS = IMAGES * GROUPS_PER_IMAGE
 GROUP_ITEMS = LIVE * ITERATIONS
 N_ITEMS = N_GROUPS * GROUP_ITEMS
+IMAGE_STEPS = GROUP_ITEMS * GROUPS_PER_IMAGE
 NEG_REF = TAPS
+NEG_REF8 = TAPS + 1
+W_PLACES = TAPS + 2
 PAIRS = REF // 2
-EARLY_DEPTH = {"made": 4, "turned": 2, "sum": 2}
-DEPTH = {"made": 2, "turned": 2, "sum": 1}
+G_TAPS = 5
+BURST = 3
 SLOTS_PER_STEP = 3
+EARLY_BANKS = {"made": 6, "sum": 2}
+BANKS = {"made": 3, "sum": 1}
+MEAN_FROM = 14
 INPUT_WORKS = 4
-G_TAPS = 6
 REGROUP_ROWS = 4
 SLICES = ROWS // REGROUP_ROWS
 
@@ -53,10 +58,7 @@ def tile_capsulelayer_t_kernel(tc, image, weight, bias, out):
     with ExitStack() as ctx:
         ctx.enter_context(tc.manual_schedule())
         consts = ctx.enter_context(tc.tile_pool(name="consts", bufs=1))
-        images = ctx.enter_context(tc.tile_pool(name="images", bufs=2))
-
-        ident = consts.tile([P, P], F32)
-        make_identity(nc, ident[:])
+        images = ctx.enter_context(tc.tile_pool(name="images", bufs=1))
 
         x_grouped = consts.tile([P, ROWS, COLS, PACK], BF16, align_bytes=64)
         x_sets = []
@@ -65,20 +67,23 @@ def tile_capsulelayer_t_kernel(tc, image, weight, bias, out):
             centre = [consts.tile([P, PIXELS], U8, name="x_centre%d_%d" % (s, j), align_bytes=64) for j in range(KS)]
             offset = [consts.tile([P, COLS + PIXELS + COLS], U8, name="x_offset%d_%d" % (s, j), align_bytes=64) for j in range(KS)]
             for j in range(KS):
-                nc.gpsimd.memset(codes[j][:].bitcast(F32), 0.0)
                 nc.gpsimd.memset(centre[j][:].bitcast(F32), 0.0)
+                nc.gpsimd.memset(codes[j][:].bitcast(F32), 0.0)
                 nc.gpsimd.memset(offset[j][:].bitcast(F32), 0.0)
             x_sets.append((codes, centre, offset))
+        ident = consts.tile([P, P], F32)
+        make_identity(nc, ident[:])
 
         def load_image(b):
             x_raw = images.tile([P, PACK, ROWS, COLS], BF16)
             nc.sync.dma_start(out=x_raw[:], in_=image[b].rearrange("(p r) h w -> p r h w", r=PACK))
             return x_raw
 
-        def regroup_views(x_raw, row0, n_rows):
-            dst = x_grouped[:, row0 : row0 + n_rows, :, :]
-            src = x_raw[:, :, row0 : row0 + n_rows, :].rearrange("p r h w -> p h w r")
-            return dst, src
+        def regroup_image(copy, x_raw, row0, n_rows):
+            copy(
+                out=x_grouped[:, row0 : row0 + n_rows, :, :],
+                in_=x_raw[:, :, row0 : row0 + n_rows, :].rearrange("p r h w -> p h w r"),
+            )
 
         def columns(ap, lo, hi):
             return ap.rearrange("p (h w) -> p h w", w=COLS)[:, :, lo:hi]
@@ -117,23 +122,21 @@ def tile_capsulelayer_t_kernel(tc, image, weight, bias, out):
             return words, scales
 
         raws = {0: load_image(0)}
-        w_codes = consts.tile([P, TAPS + 1, FEATURES], U32, align_bytes=64)
-        w_scales = consts.tile([P, TAPS + 1, FEATURES], U8, align_bytes=64)
+        w_codes = consts.tile([P, W_PLACES, FEATURES], U32, align_bytes=64)
+        w_scales = consts.tile([P, W_PLACES, FEATURES], U8, align_bytes=64)
         bias_bf = consts.tile([P, TAPS * HALVES], BF16)
         w_rows = weight.rearrange("a b c i j (p r) n -> p (a b c i j) r n", r=PACK)
         with tc.tile_pool(name="head", bufs=1) as head:
-            w_raws = []
-            for i in range(KS):
+            w_raws = {}
+            for i in (KS - 1, 0, 1):
                 w_raw = head.tile([P, KS, PACK, FEATURES], BF16, bufs=KS)
                 nc.sync.dma_start(out=w_raw[:], in_=w_rows[:, KS * i : KS * (i + 1), :, :])
-                w_raws.append(w_raw)
+                w_raws[i] = w_raw
             with nc.allow_non_contiguous_dma(reason="2304 bias values, one to a partition, once"):
                 nc.sync.dma_start(out=bias_bf[:], in_=bias.rearrange("a b c i j o (g f) -> f (a b c i j o g)", g=HALVES))
-            dst, src = regroup_views(raws[0], 0, ROWS)
-            nc.vector.tensor_copy(out=dst, in_=src)
             w_groupeds = []
-            for t in range(TAPS):
-                w_grouped = head.tile([P, FEATURES, PACK], BF16, align_bytes=64, bufs=TAPS)
+            for t in range(W_PLACES):
+                w_grouped = head.tile([P, FEATURES, PACK], BF16, align_bytes=64, bufs=W_PLACES)
                 w_groupeds.append(w_grouped)
 
             def regroup_weights(t, copy):
@@ -146,27 +149,30 @@ def tile_capsulelayer_t_kernel(tc, image, weight, bias, out):
                     in_=w_groupeds[t][:].rearrange("p n r -> p (n r)"),
                 )
 
-            for t in (0, 1, 3, 5, 7):
+            for t in (REF, 0, 2, 4, 6):
                 regroup_weights(t, nc.scalar.copy)
-            for number in range(INPUT_WORKS):
-                input_work(0, number)
-            for t in (REF, 2, 4, 6):
+            regroup_image(nc.vector.tensor_copy, raws[0], 0, ROWS)
+            raws[1] = load_image(1)
+            input_work(0, 0)
+            nc.vector.tensor_scalar_mul(out=w_groupeds[NEG_REF][:], in0=w_groupeds[REF][:], scalar1=-1.0)
+            input_work(0, 1)
+            quantise_weights(NEG_REF)
+            input_work(0, 2)
+            quantise_weights(0)
+            input_work(0, 3)
+            for t in (1, 3, 5, 7):
                 regroup_weights(t, nc.vector.tensor_copy)
-            for t in range(TAPS):
                 quantise_weights(t)
-            w_negated = head.tile([P, FEATURES, PACK], BF16, align_bytes=64)
-            nc.vector.tensor_scalar_mul(out=w_negated[:], in0=w_groupeds[REF][:], scalar1=-1.0)
-            nc.vector.quantize_mx(
-                out=w_codes[:, NEG_REF, :].bitcast(FP8X4),
-                scales=w_scales[:, NEG_REF, :],
-                in_=w_negated[:].rearrange("p n r -> p (n r)"),
-            )
-        raws[1] = load_image(1)
+                if t < 7:
+                    quantise_weights(t + 1)
+            nc.vector.tensor_scalar_mul(out=w_groupeds[NEG_REF8][:], in0=w_groupeds[REF][:], scalar1=-8.0)
+            quantise_weights(NEG_REF8)
+            quantise_weights(REF)
 
         bias_cols = consts.tile([P, TAPS, HALVES], F32)
-        nc.vector.tensor_copy(out=bias_cols[:].rearrange("p t g -> p (t g)"), in_=bias_bf[:])
+        nc.gpsimd.tensor_copy(out=bias_cols[:].rearrange("p t g -> p (t g)"), in_=bias_bf[:])
         bias_rel = consts.tile([P, REF, HALVES], F32)
-        nc.vector.tensor_tensor(
+        nc.gpsimd.tensor_tensor(
             out=bias_rel[:],
             in0=bias_cols[:, 0:REF, :],
             in1=bias_cols[:, REF : REF + 1, :].to_broadcast([P, REF, HALVES]),
@@ -181,7 +187,7 @@ def tile_capsulelayer_t_kernel(tc, image, weight, bias, out):
         work_pool = ctx.enter_context(tc.tile_pool(name="work", bufs=2))
         item_pool = ctx.enter_context(tc.tile_pool(name="item", bufs=4))
         groups = {}
-        banks = {}
+        made = {}
 
         def begin_group(group):
             ref_T = group_pool.tile([P, HALVES, GROUP_PIXELS], F32)
@@ -201,56 +207,52 @@ def tile_capsulelayer_t_kernel(tc, image, weight, bias, out):
                 stop=stop,
             )
 
+        MEAN_TERMS = [(t, t) for t in range(REF)] + [(REF, NEG_REF8)]
+
+        def issue(pool, banks, group, kind, a, k, spare=0):
+            g = groups[group]
+            if kind == "mean":
+                if a == 0:
+                    sum_bank = pool.tile([P, GROUP_PIXELS], F32, tag="sum", bufs=banks["sum"])
+                    made[group, kind, k] = sum_bank
+                product(group, made[group, kind, k][:], *MEAN_TERMS[a], k, a == 0, a == len(MEAN_TERMS) - 1)
+                return
+            bank = pool.tile([P, GROUP_PIXELS], F32, tag="made", bufs=banks["made"])
+            made[group, kind, a, k] = bank
+            for n in range(spare):
+                product(group, bank[:], a, a, 0, True, True)
+            if kind == "turn":
+                for tt in range(2):
+                    for h in range(HALVES):
+                        to = (HALVES * tt + h) * P
+                        nc.tensor.transpose(
+                            bank[:, to : to + P], g["taps_T"][a][:, HALVES * tt + h, k * P : (k + 1) * P], ident[:]
+                        )
+            elif kind == "ref":
+                product(group, bank[:], REF, REF, k, True, True)
+            elif kind == "tap":
+                product(group, bank[:], a, a, k, True, False)
+                product(group, bank[:], REF, NEG_REF, k, False, True)
+
         def empty(dst, src, bias_col, by_vector):
             if by_vector:
                 nc.vector.tensor_scalar_add(out=dst, in0=src, scalar1=bias_col)
             else:
                 nc.scalar.activation(out=dst, in_=src, func=ACT.Identity, bias=bias_col)
 
-        TAP_UNITS = [("tap", t, h) for t in range(REF) for h in range(HALVES)]
-        REF_UNITS = [("ref", 0, h) for h in range(HALVES)]
-        MEAN_UNITS = [("mean", t, h) for h in range(HALVES) for t in range(REF)]
-        TURN_UNITS = [("turn", pair, j) for j in range(LIVE) for pair in range(PAIRS)]
-
-        def issue(pool, depth, group, kind, a, k):
-            g = groups[group]
-            if kind == "mean":
-                if a == 0:
-                    sum_bank = pool.tile([P, GROUP_PIXELS], F32, tag="sum", bufs=depth["sum"])
-                    banks[group, kind, k] = sum_bank
-                bank = banks[group, kind, k]
-                product(group, bank[:], a, a, k, a == 0, False)
-                product(group, bank[:], REF, NEG_REF, k, False, a == REF - 1)
-                return
-            if kind == "turn":
-                bank = pool.tile([P, 2, FEATURES], F32, tag="turned", bufs=depth["turned"])
-                for tt in range(2):
-                    for h in range(HALVES):
-                        nc.tensor.transpose(
-                            bank[:, tt, h * P : (h + 1) * P], g["taps_T"][a][:, 2 * tt + h, k * P : (k + 1) * P], ident[:]
-                        )
-            else:
-                bank = pool.tile([P, GROUP_PIXELS], F32, tag="made", bufs=depth["made"])
-                if kind == "ref":
-                    product(group, bank[:], REF, REF, k, True, True)
-                else:
-                    product(group, bank[:], a, a, k, True, False)
-                    product(group, bank[:], REF, NEG_REF, k, False, True)
-            banks[group, kind, a, k] = bank
-
         def collect(group, kind, a, k, by_vector=False):
             g = groups[group]
             if kind == "mean":
-                if a == REF - 1:
+                if a == len(MEAN_TERMS) - 1:
                     nc.scalar.activation(
                         out=g["start_T"][:, k, :],
-                        in_=banks[group, kind, k][:],
+                        in_=made[group, kind, k][:],
                         func=ACT.Identity,
                         bias=bias_start[:, k : k + 1],
                         scale=1.0 / TAPS,
                     )
                 return
-            bank = banks[group, kind, a, k]
+            bank = made[group, kind, a, k]
             if kind == "ref":
                 empty(g["ref_T"][:, k, :], bank[:], bias_cols[:, REF, k : k + 1], by_vector)
             elif kind == "tap":
@@ -258,12 +260,12 @@ def tile_capsulelayer_t_kernel(tc, image, weight, bias, out):
                 if tt == 0 and k == 0:
                     taps_T = group_pool.tile([P, 2 * HALVES, GROUP_PIXELS], F32, bufs=PAIRS)
                     g["taps_T"][pair] = taps_T
-                empty(g["taps_T"][pair][:, 2 * tt + k, :], bank[:], bias_rel[:, a, k : k + 1], by_vector)
+                empty(g["taps_T"][pair][:, HALVES * tt + k, :], bank[:], bias_rel[:, a, k : k + 1], by_vector)
             else:
                 if a == 0:
                     u = block_pool.tile([P, REF, FEATURES], F32)
                     g["u_pix"].append(u)
-                dst = g["u_pix"][k][:, 2 * a : 2 * a + 2, :]
+                dst = g["u_pix"][k][:, 2 * a : 2 * a + 2, :].rearrange("p t f -> p (t f)")
                 if by_vector:
                     nc.vector.tensor_copy(out=dst, in_=bank[:])
                 else:
@@ -278,32 +280,37 @@ def tile_capsulelayer_t_kernel(tc, image, weight, bias, out):
             it, j = divmod(rest, LIVE)
             return group, it, j
 
-        def sum_taps(n):
-            total = psum.tile([P, HALVES, P], F32, tag="total", bufs=1)
+        def sum_taps(n, tap0, n_taps, first, last):
+            if first:
+                items[n]["total"] = []
+                for h in range(HALVES):
+                    total = psum.tile([P, P], F32, name="total%d" % h, tag="total%d" % h, bufs=1)
+                    items[n]["total"].append(total)
             wp = items[n]["weighted"]
             for h in range(HALVES):
-                for t in range(REF):
+                for t in range(tap0, tap0 + n_taps):
                     nc.tensor.matmul(
-                        total[:, h, :],
+                        items[n]["total"][h][:],
                         lhsT=wp[:, t, h * P : (h + 1) * P],
                         rhs=ident[:],
                         is_transpose=True,
-                        start=(t == 0),
-                        stop=(t == REF - 1),
+                        start=(first and t == tap0),
+                        stop=(last and t == tap0 + n_taps - 1),
                     )
-            items[n]["total"] = total
 
         def keep_total(n):
-            total_T = item_pool.tile([P, HALVES, P], F32)
-            nc.scalar.copy(out=total_T[:], in_=items[n]["total"][:])
+            total_T = item_pool.tile([P, HALVES, P], F32, bufs=2)
+            for h in range(HALVES):
+                nc.scalar.copy(out=total_T[:, h, :], in_=items[n]["total"][h][:])
             items[n]["total_T"] = total_T
 
         def leave(n):
             group, it, j = item(n)
-            out_sb = item_pool.tile([P, HALVES, P], F32)
-            nc.vector.tensor_tensor(
-                out=out_sb[:], in0=items[n]["total"][:], in1=groups[group]["ref_T"][:, :, j * P : (j + 1) * P], op=ALU.add
-            )
+            out_sb = item_pool.tile([P, HALVES, P], F32, bufs=2)
+            for h in range(HALVES):
+                nc.vector.tensor_tensor(
+                    out=out_sb[:, h, :], in0=items[n]["total"][h][:], in1=groups[group]["ref_T"][:, h, j * P : (j + 1) * P], op=ALU.add
+                )
             b, part = divmod(group, GROUPS_PER_IMAGE)
             first = GROUP_PIXELS * part + j * P
             nc.sync.dma_start(
@@ -312,7 +319,7 @@ def tile_capsulelayer_t_kernel(tc, image, weight, bias, out):
 
         def turn_output(n):
             group, it, j = item(n)
-            o = psum.tile([P, FEATURES], F32, tag="o")
+            o = psum.tile([P, FEATURES], F32, tag="o", bufs=1)
             for h in range(HALVES):
                 if it == 0:
                     src = groups[group]["start_T"][:, h, j * P : (j + 1) * P]
@@ -351,13 +358,10 @@ def tile_capsulelayer_t_kernel(tc, image, weight, bias, out):
 
         def sum_weights(n):
             cw_sum = item_pool.tile([P, CAPS], F32)
-            items[n]["cw_sum"] = cw_sum
             nc.vector.tensor_reduce(out=cw_sum[:], in_=items[n]["cw"][:].rearrange("p t c -> p c t"), axis=AXIS_X, op=ALU.add)
-
-        def invert_sum(n):
             cw_inv = item_pool.tile([P, CAPS], F32)
             items[n]["cw_inv"] = cw_inv
-            nc.vector.reciprocal(out=cw_inv[:], in_=items[n]["cw_sum"][:])
+            nc.vector.reciprocal(out=cw_inv[:], in_=cw_sum[:])
 
         def normalise(n):
             share = item_pool.tile([P, REF, CAPS], F32)
@@ -378,100 +382,121 @@ def tile_capsulelayer_t_kernel(tc, image, weight, bias, out):
                 op=ALU.mult,
             )
 
-        def begin_weighted(n):
-            weighted = work_pool.tile([P, REF, FEATURES], F32)
-            items[n]["weighted"] = weighted
+        TAP_UNITS = [("tap", t, h) for t in range(REF) for h in range(HALVES)]
+        MEAN_UNITS = [("mean", a, h) for h in range(HALVES) for a in range(len(MEAN_TERMS))]
+        TURN_UNITS = [("turn", pair, j) for j in range(LIVE) for pair in range(PAIRS)]
+        REF_UNITS = [("ref", 0, h) for h in range(HALVES)]
+        MAKE_UP = ("make up", 0, 0)
 
-        IMAGE_STEPS = GROUP_ITEMS * GROUPS_PER_IMAGE
+        begin_group(0)
+        head_units = TAP_UNITS + MEAN_UNITS + TURN_UNITS + REF_UNITS
+        with tc.psum_pool(name="early", bufs=1) as early:
+            for k, unit in enumerate(head_units):
+                issue(early, EARLY_BANKS, 0, *unit)
+                if k > 0:
+                    collect(0, *head_units[k - 1], by_vector=(k % 2 == 1))
+            collect(0, *head_units[-1])
+        psum = ctx.enter_context(tc.psum_pool(name="psum", bufs=1))
+
+        row = []
+        for group in range(1, N_GROUPS):
+            slots = [[u] for u in TAP_UNITS + REF_UNITS + TURN_UNITS]
+            for k, unit in enumerate(MEAN_UNITS):
+                slots[MEAN_FROM + k] = [unit] + slots[MEAN_FROM + k]
+            if group > 1:
+                slots += [[MAKE_UP], [MAKE_UP]]
+            row += [(group, units) for units in slots]
+        issued = [0]
+        collected = [0]
+
+        def issue_slot():
+            at = issued[0]
+            if at >= len(row):
+                return
+            issued[0] += 1
+            group, units = row[at]
+            if group not in groups:
+                begin_group(group)
+            passes = 0
+            for unit in units:
+                if unit[0] == "tap":
+                    passes += 2
+                elif unit[0] in ("mean", "ref"):
+                    passes += 1
+            for unit in units:
+                issue(psum, BANKS, group, *unit, spare=(BURST - passes if unit == units[-1] else 0))
+
+        def collect_slot():
+            at = collected[0]
+            if at >= len(row):
+                return
+            collected[0] += 1
+            group, units = row[at]
+            for unit in units:
+                if unit[0] != "make up":
+                    collect(group, *unit)
+
         slices_at = {}
         works_at = {}
         for b in range(1, IMAGES):
             work0 = IMAGE_STEPS * (b - 1) + GROUP_ITEMS - 2 - INPUT_WORKS
             for number in range(INPUT_WORKS):
                 works_at[work0 + number] = (b, number)
-            for number in range(SLICES):
-                at = work0 - 1 - number if b > 1 else work0 - 1 - number // 2
-                slices_at.setdefault(at, []).append((b, SLICES - 1 - number))
+            if b > 1:
+                for number in range(SLICES):
+                    slices_at[work0 - 1 - SLICES + number] = (b, number)
 
-        row = [([(0,) + unit], k % 2 == 1) for k, unit in enumerate(TAP_UNITS + MEAN_UNITS + TURN_UNITS[0:PAIRS])]
-        head_slots = len(row)
-        row += [([(0,) + u], k % 2 == 1) for k, u in enumerate(TURN_UNITS[PAIRS:])]
-        fill_slots = len(row)
-        row_end = [0]
-        for group in range(1, N_GROUPS):
-            units = [[u] for u in TAP_UNITS + REF_UNITS] + [[m, u] for m, u in zip(MEAN_UNITS, TURN_UNITS)]
-            if group == 1:
-                row += [([(0,) + u], False) for u in REF_UNITS]
-            row += [([(group,) + u for u in slot], False) for slot in units]
-            row_end.append(len(row))
-        begun = [0]
-
-        def next_slot(pool, depth):
-            at = begun[0]
-            begun[0] += 1
-            if at < len(row):
-                for unit in row[at][0]:
-                    if unit[0] not in groups:
-                        begin_group(unit[0])
-                    issue(pool, depth, *unit)
-            if at > 0 and at != head_slots:
-                for unit in row[at - 1][0]:
-                    collect(*unit, by_vector=row[at - 1][1])
-
-        def slots_in(s):
-            if s == 0:
-                return fill_slots - head_slots
-            ready = row_end[min((s + 1) // GROUP_ITEMS + 1, N_GROUPS - 1)]
-            if ready == len(row):
-                ready += 1
-            return min(SLOTS_PER_STEP + (1 if s < GROUP_ITEMS else 0), ready - begun[0])
-
-        with tc.psum_pool(name="early", bufs=2) as early:
-            for k in range(head_slots):
-                next_slot(early, EARLY_DEPTH)
-            for unit in row[head_slots - 1][0]:
-                collect(*unit, by_vector=row[head_slots - 1][1])
-        psum = ctx.enter_context(tc.psum_pool(name="psum", bufs=2))
-        turn_output(0)
-
-        def slots(n):
-            for k in range(n):
-                next_slot(psum, DEPTH)
-
-        for s in range(N_ITEMS + 3):
-            ends = item(s - 3)
-            if ends:
-                sum_taps(s - 3)
-            n_slots = slots_in(s)
-            slots(n_slots // 3)
-            if ends and ends[1] < ITERATIONS - 1:
-                keep_total(s - 3)
+        def turn_next(s):
             if item(s + 1):
                 turn_output(s + 1)
-            slots(n_slots // 3)
+
+        turn_output(0)
+        for s in range(N_ITEMS + 3):
+            ends = item(s - 3)
+            if s > 0:
+                collect_slot()
+            if ends and ends[1] < ITERATIONS - 1:
+                keep_total(s - 3)
+            issue_slot()
+            collect_slot()
             if item(s):
                 subtract(s)
             if ends and ends[1] == ITERATIONS - 1:
                 leave(s - 3)
             if item(s):
                 square(s)
+            if item(s - 2):
+                weighted = work_pool.tile([P, REF, FEATURES], F32)
+                items[s - 2]["weighted"] = weighted
+                for tap0 in range(0, G_TAPS, 2):
+                    n_taps = min(2, G_TAPS - tap0)
+                    multiply(nc.gpsimd, s - 2, tap0, n_taps)
+                    sum_taps(s - 2, tap0, n_taps, tap0 == 0, False)
+                    if tap0 < 4:
+                        issue_slot()
+                    if tap0 == 0:
+                        turn_next(s)
+            else:
+                issue_slot()
+                issue_slot()
+                turn_next(s)
             if item(s - 1):
                 sum_channels(s - 1)
                 inverse_root(s - 1)
+            collect_slot()
             if item(s - 2):
-                begin_weighted(s - 2)
-                for tap0 in range(0, G_TAPS, 2):
-                    multiply(nc.gpsimd, s - 2, tap0, 2)
                 multiply(nc.vector, s - 2, G_TAPS, REF - G_TAPS)
-            slots(n_slots - 2 * (n_slots // 3))
+                sum_taps(s - 2, G_TAPS, REF - G_TAPS, False, True)
             if s in works_at:
                 input_work(*works_at[s])
             if item(s - 1):
                 sum_weights(s - 1)
-                invert_sum(s - 1)
                 normalise(s - 1)
-            for b, number in slices_at.get(s, []):
-                dst, src = regroup_views(raws[b], REGROUP_ROWS * number, REGROUP_ROWS)
-                nc.scalar.copy(out=dst, in_=src)
+            if s in slices_at:
+                b, number = slices_at[s]
+                regroup_image(nc.scalar.copy, raws[b], REGROUP_ROWS * number, REGROUP_ROWS)
                 if number == SLICES - 1 and b + 1 < IMAGES:
                     raws[b + 1] = load_image(b + 1)
+            if s == 0:
+                regroup_image(nc.vector.tensor_copy, raws[1], 0, ROWS)
+                raws[2] = load_image(2)

@@ -33,16 +33,18 @@ GROUP_PIXELS = LIVE * P
 GROUP_ROWS = GROUP_PIXELS // COLS
 GROUPS_PER_IMAGE = PIXELS // GROUP_PIXELS
 N_GROUPS = IMAGES * GROUPS_PER_IMAGE
-GROUP_ITEMS = LIVE * ITERATIONS
+TURN = LIVE * HALVES
+GROUP_ITEMS = TURN * ITERATIONS
 N_ITEMS = N_GROUPS * GROUP_ITEMS
 IMAGE_STEPS = GROUP_ITEMS * GROUPS_PER_IMAGE
+HALF_CAPS = CAPS // HALVES
 NEG_REF = TAPS
 NEG_REF8 = TAPS + 1
 W_PLACES = TAPS + 2
 PAIRS = REF // 2
-G_TAPS = 5
+G_TAPS = 6
 BURST = 3
-SLOTS_PER_STEP = 3
+SLOTS_PER_TWO_STEPS = 3
 EARLY_BANKS = {"made": 6, "sum": 2}
 BANKS = {"made": 3, "sum": 1}
 MEAN_FROM = 14
@@ -184,7 +186,7 @@ def tile_capsulelayer_t_kernel(tc, image, weight, bias, out):
 
         group_pool = ctx.enter_context(tc.tile_pool(name="group", bufs=2))
         block_pool = ctx.enter_context(tc.tile_pool(name="block", bufs=2 * LIVE))
-        work_pool = ctx.enter_context(tc.tile_pool(name="work", bufs=2))
+        work_pool = ctx.enter_context(tc.tile_pool(name="work", bufs=4))
         item_pool = ctx.enter_context(tc.tile_pool(name="item", bufs=4))
         groups = {}
         made = {}
@@ -277,108 +279,100 @@ def tile_capsulelayer_t_kernel(tc, image, weight, bias, out):
             if n < 0 or n >= N_ITEMS:
                 return None
             group, rest = divmod(n, GROUP_ITEMS)
-            it, j = divmod(rest, LIVE)
-            return group, it, j
+            it, rest = divmod(rest, TURN)
+            j, half = divmod(rest, HALVES)
+            return group, it, j, slice(half * P, (half + 1) * P), half
 
-        def sum_taps(n, tap0, n_taps, first, last):
-            if first:
-                items[n]["total"] = []
-                for h in range(HALVES):
-                    total = psum.tile([P, P], F32, name="total%d" % h, tag="total%d" % h, bufs=1)
-                    items[n]["total"].append(total)
+        def sum_taps(n):
+            total = psum.tile([P, P], F32, tag="total", bufs=2)
+            items[n]["total"] = total
             wp = items[n]["weighted"]
-            for h in range(HALVES):
-                for t in range(tap0, tap0 + n_taps):
-                    nc.tensor.matmul(
-                        items[n]["total"][h][:],
-                        lhsT=wp[:, t, h * P : (h + 1) * P],
-                        rhs=ident[:],
-                        is_transpose=True,
-                        start=(first and t == tap0),
-                        stop=(last and t == tap0 + n_taps - 1),
-                    )
+            for t in range(REF):
+                nc.tensor.matmul(
+                    total[:], lhsT=wp[:, t, :], rhs=ident[:], is_transpose=True, start=(t == 0), stop=(t == REF - 1)
+                )
 
         def keep_total(n):
-            total_T = item_pool.tile([P, HALVES, P], F32, bufs=2)
-            for h in range(HALVES):
-                nc.scalar.copy(out=total_T[:, h, :], in_=items[n]["total"][h][:])
+            total_T = item_pool.tile([P, P], F32)
+            nc.scalar.copy(out=total_T[:], in_=items[n]["total"][:])
             items[n]["total_T"] = total_T
 
         def leave(n):
-            group, it, j = item(n)
-            out_sb = item_pool.tile([P, HALVES, P], F32, bufs=2)
-            for h in range(HALVES):
-                nc.vector.tensor_tensor(
-                    out=out_sb[:, h, :], in0=items[n]["total"][h][:], in1=groups[group]["ref_T"][:, h, j * P : (j + 1) * P], op=ALU.add
-                )
+            group, it, j, feats, half = item(n)
+            out_sb = item_pool.tile([P, P], F32)
+            nc.vector.tensor_tensor(
+                out=out_sb[:], in0=items[n]["total"][:], in1=groups[group]["ref_T"][:, half, j * P : (j + 1) * P], op=ALU.add
+            )
             b, part = divmod(group, GROUPS_PER_IMAGE)
             first = GROUP_PIXELS * part + j * P
             nc.sync.dma_start(
-                out=out[b].rearrange("(g f) h w -> f g (h w)", g=HALVES)[:, :, first : first + P], in_=out_sb[:]
+                out=out[b].rearrange("(g f) h w -> g f (h w)", g=HALVES)[half, :, first : first + P], in_=out_sb[:]
             )
 
         def turn_output(n):
-            group, it, j = item(n)
-            o = psum.tile([P, FEATURES], F32, tag="o", bufs=1)
-            for h in range(HALVES):
-                if it == 0:
-                    src = groups[group]["start_T"][:, h, j * P : (j + 1) * P]
-                else:
-                    src = items[n - LIVE]["total_T"][:, h, :]
-                nc.tensor.transpose(o[:, h * P : (h + 1) * P], src, ident[:])
+            group, it, j, feats, half = item(n)
+            o = psum.tile([P, P], F32, tag="o", bufs=2)
+            if it == 0:
+                src = groups[group]["start_T"][:, half, j * P : (j + 1) * P]
+            else:
+                src = items[n - TURN]["total_T"][:]
+            nc.tensor.transpose(o[:], src, ident[:])
             items[n] = {"o": o}
 
         def subtract(n):
-            group, it, j = item(n)
-            d = work_pool.tile([P, TAPS, FEATURES], F32)
+            group, it, j, feats, half = item(n)
+            d = work_pool.tile([P, TAPS, P], F32)
             items[n]["d"] = d
             nc.vector.tensor_tensor(
                 out=d[:, 0:REF, :],
-                in0=groups[group]["u_pix"][j][:],
-                in1=items[n]["o"][:].unsqueeze(1).to_broadcast([P, REF, FEATURES]),
+                in0=groups[group]["u_pix"][j][:, :, feats],
+                in1=items[n]["o"][:].unsqueeze(1).to_broadcast([P, REF, P]),
                 op=ALU.subtract,
             )
 
+        def square_output(n):
+            nc.scalar.activation(out=items[n]["d"][:, REF, :], in_=items[n]["o"][:], func=ACT.Square)
+
         def square(n):
             d = items[n]["d"]
-            nc.scalar.activation(out=d[:, REF, :], in_=items[n]["o"][:], func=ACT.Square)
             nc.scalar.activation(out=d[:, 0:REF, :], in_=d[:, 0:REF, :], func=ACT.Square)
 
         def sum_channels(n):
-            dist = item_pool.tile([P, TAPS, CAPS], F32)
+            dist = item_pool.tile([P, TAPS, HALF_CAPS], F32)
             items[n]["dist"] = dist
             nc.vector.tensor_reduce(
                 out=dist[:], in_=items[n]["d"][:].rearrange("p t (c k) -> p t c k", k=CAP_CH), axis=AXIS_X, op=ALU.add
             )
 
         def inverse_root(n):
-            cw = item_pool.tile([P, TAPS, CAPS], F32)
+            cw = item_pool.tile([P, TAPS, HALF_CAPS], F32)
             items[n]["cw"] = cw
             nc.scalar.activation(out=cw[:], in_=items[n]["dist"][:], func=ACT.Abs_reciprocal_sqrt, bias=EPS)
 
         def sum_weights(n):
-            cw_sum = item_pool.tile([P, CAPS], F32)
+            cw_sum = item_pool.tile([P, HALF_CAPS], F32)
             nc.vector.tensor_reduce(out=cw_sum[:], in_=items[n]["cw"][:].rearrange("p t c -> p c t"), axis=AXIS_X, op=ALU.add)
-            cw_inv = item_pool.tile([P, CAPS], F32)
+            cw_inv = item_pool.tile([P, HALF_CAPS], F32)
             items[n]["cw_inv"] = cw_inv
             nc.vector.reciprocal(out=cw_inv[:], in_=cw_sum[:])
 
         def normalise(n):
-            share = item_pool.tile([P, REF, CAPS], F32)
+            share = item_pool.tile([P, REF, HALF_CAPS], F32)
             items[n]["share"] = share
             nc.gpsimd.tensor_tensor(
                 out=share[:],
                 in0=items[n]["cw"][:, 0:REF, :],
-                in1=items[n]["cw_inv"][:].unsqueeze(1).to_broadcast([P, REF, CAPS]),
+                in1=items[n]["cw_inv"][:].unsqueeze(1).to_broadcast([P, REF, HALF_CAPS]),
                 op=ALU.mult,
             )
 
         def multiply(engine, n, tap0, n_taps):
-            group, it, j = item(n)
+            group, it, j, feats, half = item(n)
+            taps = slice(tap0, tap0 + n_taps)
             engine.tensor_tensor(
-                out=items[n]["weighted"][:, tap0 : tap0 + n_taps, :].rearrange("p t (c k) -> p t c k", k=CAP_CH),
-                in0=groups[group]["u_pix"][j][:, tap0 : tap0 + n_taps, :].rearrange("p t (c k) -> p t c k", k=CAP_CH),
-                in1=items[n]["share"][:, tap0 : tap0 + n_taps, :].unsqueeze(3).to_broadcast([P, n_taps, CAPS, CAP_CH]),
+                out=items[n]["weighted"][:, taps, :].rearrange("p t (c k) -> p t c k", k=CAP_CH),
+                in0=groups[group]["u_pix"][j][:, taps, feats].rearrange("p t (c k) -> p t c k", k=CAP_CH),
+                in1=items[n]["share"][:, taps, :].unsqueeze(3).to_broadcast([P, n_taps, HALF_CAPS, CAP_CH]),
                 op=ALU.mult,
             )
 
@@ -439,64 +433,55 @@ def tile_capsulelayer_t_kernel(tc, image, weight, bias, out):
         slices_at = {}
         works_at = {}
         for b in range(1, IMAGES):
-            work0 = IMAGE_STEPS * (b - 1) + GROUP_ITEMS - 2 - INPUT_WORKS
+            work0 = IMAGE_STEPS * (b - 1) + GROUP_ITEMS // 2
             for number in range(INPUT_WORKS):
-                works_at[work0 + number] = (b, number)
+                works_at[work0 + 2 * number] = (b, number)
             if b > 1:
                 for number in range(SLICES):
-                    slices_at[work0 - 1 - SLICES + number] = (b, number)
-
-        def turn_next(s):
-            if item(s + 1):
-                turn_output(s + 1)
+                    slices_at[work0 - 2 * (SLICES - number)] = (b, number)
 
         turn_output(0)
-        for s in range(N_ITEMS + 3):
-            ends = item(s - 3)
-            if s > 0:
-                collect_slot()
+        for s in range(N_ITEMS + 7):
+            if item(s - 5):
+                multiply(nc.vector, s - 5, G_TAPS, REF - G_TAPS)
+            ends = item(s - 6)
             if ends and ends[1] < ITERATIONS - 1:
-                keep_total(s - 3)
+                keep_total(s - 6)
+            elif ends:
+                leave(s - 6)
+            if issued[0] > collected[0]:
+                collect_slot()
             issue_slot()
-            collect_slot()
+            if item(s + 1):
+                turn_output(s + 1)
+            if item(s - 5):
+                sum_taps(s - 5)
+            if s % 2 == 1:
+                issue_slot()
             if item(s):
                 subtract(s)
-            if ends and ends[1] == ITERATIONS - 1:
-                leave(s - 3)
-            if item(s):
-                square(s)
-            if item(s - 2):
-                weighted = work_pool.tile([P, REF, FEATURES], F32)
-                items[s - 2]["weighted"] = weighted
-                for tap0 in range(0, G_TAPS, 2):
-                    n_taps = min(2, G_TAPS - tap0)
-                    multiply(nc.gpsimd, s - 2, tap0, n_taps)
-                    sum_taps(s - 2, tap0, n_taps, tap0 == 0, False)
-                    if tap0 < 4:
-                        issue_slot()
-                    if tap0 == 0:
-                        turn_next(s)
-            else:
-                issue_slot()
-                issue_slot()
-                turn_next(s)
+            if item(s - 3):
+                inverse_root(s - 3)
             if item(s - 1):
-                sum_channels(s - 1)
-                inverse_root(s - 1)
-            collect_slot()
+                square(s - 1)
             if item(s - 2):
-                multiply(nc.vector, s - 2, G_TAPS, REF - G_TAPS)
-                sum_taps(s - 2, G_TAPS, REF - G_TAPS, False, True)
+                sum_channels(s - 2)
+            collect_slot()
             if s in works_at:
                 input_work(*works_at[s])
-            if item(s - 1):
-                sum_weights(s - 1)
-                normalise(s - 1)
+            if item(s - 3):
+                sum_weights(s - 3)
+                normalise(s - 3)
+                weighted = work_pool.tile([P, REF, P], F32)
+                items[s - 3]["weighted"] = weighted
+                multiply(nc.gpsimd, s - 3, 0, G_TAPS)
+            if item(s):
+                square_output(s)
             if s in slices_at:
                 b, number = slices_at[s]
                 regroup_image(nc.scalar.copy, raws[b], REGROUP_ROWS * number, REGROUP_ROWS)
                 if number == SLICES - 1 and b + 1 < IMAGES:
                     raws[b + 1] = load_image(b + 1)
-            if s == 0:
+            if s == 1:
                 regroup_image(nc.vector.tensor_copy, raws[1], 0, ROWS)
                 raws[2] = load_image(2)

@@ -42,8 +42,10 @@ NEG_REF = TAPS
 NEG_REF8 = TAPS + 1
 W_PLACES = TAPS + 2
 PAIRS = REF // 2
+V_SUBS = REF - 1
+T_PAIR = PAIRS - 1
 G_TAPS = 6
-BURST = 3
+BURST = 4
 SLOTS_PER_TWO_STEPS = 3
 EARLY_BANKS = {"made": 6, "sum": 2}
 BANKS = {"made": 3, "sum": 1}
@@ -182,7 +184,7 @@ def tile_capsulelayer_t_kernel(tc, image, weight, bias, out):
         )
         bias_start = consts.tile([P, HALVES], F32)
         nc.vector.tensor_reduce(out=bias_start[:], in_=bias_rel[:].rearrange("p t g -> p g t"), axis=AXIS_X, op=ALU.add)
-        nc.vector.tensor_scalar_mul(out=bias_start[:], in0=bias_start[:], scalar1=1.0 / TAPS)
+        nc.vector.tensor_scalar_mul(out=bias_start[:], in0=bias_start[:], scalar1=-1.0 / TAPS)
 
         group_pool = ctx.enter_context(tc.tile_pool(name="group", bufs=2))
         block_pool = ctx.enter_context(tc.tile_pool(name="block", bufs=2 * LIVE))
@@ -194,7 +196,7 @@ def tile_capsulelayer_t_kernel(tc, image, weight, bias, out):
         def begin_group(group):
             ref_T = group_pool.tile([P, HALVES, GROUP_PIXELS], F32)
             start_T = group_pool.tile([P, HALVES, GROUP_PIXELS], F32)
-            groups[group] = {"ref_T": ref_T, "start_T": start_T, "u_pix": [], "taps_T": {}}
+            groups[group] = {"ref_T": ref_T, "start_T": start_T, "u_pix": {}, "taps_T": {}}
 
         def product(group, bank, t_x, w_place, half, start, stop):
             feats = slice(half * P, (half + 1) * P)
@@ -211,8 +213,7 @@ def tile_capsulelayer_t_kernel(tc, image, weight, bias, out):
 
         MEAN_TERMS = [(t, t) for t in range(REF)] + [(REF, NEG_REF8)]
 
-        def issue(pool, banks, group, kind, a, k, spare=0):
-            g = groups[group]
+        def issue(pool, banks, group, kind, a, k):
             if kind == "mean":
                 if a == 0:
                     sum_bank = pool.tile([P, GROUP_PIXELS], F32, tag="sum", bufs=banks["sum"])
@@ -221,10 +222,13 @@ def tile_capsulelayer_t_kernel(tc, image, weight, bias, out):
                 return
             bank = pool.tile([P, GROUP_PIXELS], F32, tag="made", bufs=banks["made"])
             made[group, kind, a, k] = bank
-            for n in range(spare):
-                product(group, bank[:], a, a, 0, True, True)
+            fill(group, kind, a, k)
+
+        def fill(group, kind, a, k):
+            g = groups[group]
+            bank = made[group, kind, a, k]
             if kind == "turn":
-                for tt in range(2):
+                for tt in range(1 if a == T_PAIR else 2):
                     for h in range(HALVES):
                         to = (HALVES * tt + h) * P
                         nc.tensor.transpose(
@@ -232,7 +236,7 @@ def tile_capsulelayer_t_kernel(tc, image, weight, bias, out):
                         )
             elif kind == "ref":
                 product(group, bank[:], REF, REF, k, True, True)
-            elif kind == "tap":
+            else:
                 product(group, bank[:], a, a, k, True, False)
                 product(group, bank[:], REF, NEG_REF, k, False, True)
 
@@ -251,7 +255,7 @@ def tile_capsulelayer_t_kernel(tc, image, weight, bias, out):
                         in_=made[group, kind, k][:],
                         func=ACT.Identity,
                         bias=bias_start[:, k : k + 1],
-                        scale=1.0 / TAPS,
+                        scale=-1.0 / TAPS,
                     )
                 return
             bank = made[group, kind, a, k]
@@ -260,20 +264,27 @@ def tile_capsulelayer_t_kernel(tc, image, weight, bias, out):
             elif kind == "tap":
                 pair, tt = divmod(a, 2)
                 if tt == 0 and k == 0:
-                    taps_T = group_pool.tile([P, 2 * HALVES, GROUP_PIXELS], F32, bufs=PAIRS)
-                    g["taps_T"][pair] = taps_T
+                    if pair == T_PAIR:
+                        kept_T = group_pool.tile([P, 2 * HALVES, GROUP_PIXELS], F32)
+                        g["taps_T"][pair] = kept_T
+                    else:
+                        taps_T = group_pool.tile([P, 2 * HALVES, GROUP_PIXELS], F32, bufs=PAIRS - 1)
+                        g["taps_T"][pair] = taps_T
                 empty(g["taps_T"][pair][:, HALVES * tt + k, :], bank[:], bias_rel[:, a, k : k + 1], by_vector)
             else:
-                if a == 0:
-                    u = block_pool.tile([P, REF, FEATURES], F32)
-                    g["u_pix"].append(u)
-                dst = g["u_pix"][k][:, 2 * a : 2 * a + 2, :].rearrange("p t f -> p (t f)")
+                if k not in g["u_pix"]:
+                    u = block_pool.tile([P, V_SUBS, FEATURES], F32)
+                    g["u_pix"][k] = u
+                n_taps = 1 if a == T_PAIR else 2
+                dst = g["u_pix"][k][:, 2 * a : 2 * a + n_taps, :].rearrange("p t f -> p (t f)")
+                src = bank[:, 0 : n_taps * FEATURES]
                 if by_vector:
-                    nc.vector.tensor_copy(out=dst, in_=bank[:])
+                    nc.vector.tensor_copy(out=dst, in_=src)
                 else:
-                    nc.scalar.copy(out=dst, in_=bank[:])
+                    nc.scalar.copy(out=dst, in_=src)
 
         items = {}
+        turned_at = {}
 
         def item(n):
             if n < 0 or n >= N_ITEMS:
@@ -294,7 +305,7 @@ def tile_capsulelayer_t_kernel(tc, image, weight, bias, out):
 
         def keep_total(n):
             total_T = item_pool.tile([P, P], F32)
-            nc.scalar.copy(out=total_T[:], in_=items[n]["total"][:])
+            nc.scalar.mul(out=total_T[:], in_=items[n]["total"][:], mul=-1.0)
             items[n]["total_T"] = total_T
 
         def leave(n):
@@ -309,33 +320,44 @@ def tile_capsulelayer_t_kernel(tc, image, weight, bias, out):
                 out=out[b].rearrange("(g f) h w -> g f (h w)", g=HALVES)[half, :, first : first + P], in_=out_sb[:]
             )
 
-        def turn_output(n):
-            group, it, j, feats, half = item(n)
-            o = psum.tile([P, P], F32, tag="o", bufs=2)
-            if it == 0:
-                src = groups[group]["start_T"][:, half, j * P : (j + 1) * P]
-            else:
-                src = items[n - TURN]["total_T"][:]
-            nc.tensor.transpose(o[:], src, ident[:])
-            items[n] = {"o": o}
+        def turn(s):
+            turned = psum.tile([P, 2 + REF - G_TAPS, P], F32, tag="turned", bufs=2)
+            turned_at[s] = turned
+            if item(s):
+                group, it, j, feats, half = item(s)
+                pixels = slice(j * P, (j + 1) * P)
+                if it == 0:
+                    minus_o = groups[group]["start_T"][:, half, pixels]
+                else:
+                    minus_o = items[s - TURN]["total_T"][:]
+                u_T = groups[group]["taps_T"][T_PAIR][:, HALVES + half, pixels]
+                nc.tensor.matmul(turned[:, 0, :], lhsT=u_T, rhs=ident[:], is_transpose=True, start=True, stop=False)
+                nc.tensor.matmul(turned[:, 0, :], lhsT=minus_o, rhs=ident[:], is_transpose=True, start=False, stop=True)
+                nc.tensor.transpose(turned[:, 1, :], minus_o, ident[:])
+                items[s] = {}
+            if item(s - 5):
+                group, it, j, feats, half = item(s - 5)
+                for tt in range(REF - G_TAPS):
+                    u_T = groups[group]["taps_T"][T_PAIR][:, HALVES * tt + half, j * P : (j + 1) * P]
+                    nc.tensor.transpose(turned[:, 2 + tt, :], u_T, ident[:])
 
         def subtract(n):
             group, it, j, feats, half = item(n)
             d = work_pool.tile([P, TAPS, P], F32)
             items[n]["d"] = d
             nc.vector.tensor_tensor(
-                out=d[:, 0:REF, :],
+                out=d[:, 0:V_SUBS, :],
                 in0=groups[group]["u_pix"][j][:, :, feats],
-                in1=items[n]["o"][:].unsqueeze(1).to_broadcast([P, REF, P]),
-                op=ALU.subtract,
+                in1=turned_at[n][:, 1, :].unsqueeze(1).to_broadcast([P, V_SUBS, P]),
+                op=ALU.add,
             )
 
         def square_output(n):
-            nc.scalar.activation(out=items[n]["d"][:, REF, :], in_=items[n]["o"][:], func=ACT.Square)
+            nc.scalar.activation(out=items[n]["d"][:, V_SUBS:TAPS, :], in_=turned_at[n][:, 0:2, :], func=ACT.Square)
 
         def square(n):
             d = items[n]["d"]
-            nc.scalar.activation(out=d[:, 0:REF, :], in_=d[:, 0:REF, :], func=ACT.Square)
+            nc.scalar.activation(out=d[:, 0:V_SUBS, :], in_=d[:, 0:V_SUBS, :], func=ACT.Square)
 
         def sum_channels(n):
             dist = item_pool.tile([P, TAPS, HALF_CAPS], F32)
@@ -366,12 +388,11 @@ def tile_capsulelayer_t_kernel(tc, image, weight, bias, out):
                 op=ALU.mult,
             )
 
-        def multiply(engine, n, tap0, n_taps):
-            group, it, j, feats, half = item(n)
+        def multiply(engine, n, tap0, n_taps, priors):
             taps = slice(tap0, tap0 + n_taps)
             engine.tensor_tensor(
                 out=items[n]["weighted"][:, taps, :].rearrange("p t (c k) -> p t c k", k=CAP_CH),
-                in0=groups[group]["u_pix"][j][:, taps, feats].rearrange("p t (c k) -> p t c k", k=CAP_CH),
+                in0=priors.rearrange("p t (c k) -> p t c k", k=CAP_CH),
                 in1=items[n]["share"][:, taps, :].unsqueeze(3).to_broadcast([P, n_taps, HALF_CAPS, CAP_CH]),
                 op=ALU.mult,
             )
@@ -380,7 +401,8 @@ def tile_capsulelayer_t_kernel(tc, image, weight, bias, out):
         MEAN_UNITS = [("mean", a, h) for h in range(HALVES) for a in range(len(MEAN_TERMS))]
         TURN_UNITS = [("turn", pair, j) for j in range(LIVE) for pair in range(PAIRS)]
         REF_UNITS = [("ref", 0, h) for h in range(HALVES)]
-        MAKE_UP = ("make up", 0, 0)
+        TURN_BY_PAIR = [("turn", pair, j) for pair in range(PAIRS) for j in range(LIVE)]
+        PASSES = {"tap": 2, "ref": 1, "turn": 0}
 
         begin_group(0)
         head_units = TAP_UNITS + MEAN_UNITS + TURN_UNITS + REF_UNITS
@@ -392,43 +414,54 @@ def tile_capsulelayer_t_kernel(tc, image, weight, bias, out):
             collect(0, *head_units[-1])
         psum = ctx.enter_context(tc.psum_pool(name="psum", bufs=1))
 
-        row = []
-        for group in range(1, N_GROUPS):
-            slots = [[u] for u in TAP_UNITS + REF_UNITS + TURN_UNITS]
-            for k, unit in enumerate(MEAN_UNITS):
-                slots[MEAN_FROM + k] = [unit] + slots[MEAN_FROM + k]
-            if group > 1:
-                slots += [[MAKE_UP], [MAKE_UP]]
-            row += [(group, units) for units in slots]
-        issued = [0]
-        collected = [0]
+        units = list(TAP_UNITS[: 2 * PACK])
+        for k in range(2 * PACK, len(TAP_UNITS)):
+            units += [TURN_BY_PAIR[k - 2 * PACK], TAP_UNITS[k]]
+        units += REF_UNITS + TURN_BY_PAIR[2 * PACK :]
+        plan = []
+        means = list(MEAN_UNITS)
+        for s in range(GROUP_ITEMS):
+            mine = units[len(units) * s // GROUP_ITEMS : len(units) * (s + 1) // GROUP_ITEMS]
+            passes = sum([PASSES[unit[0]] for unit in mine])
+            n_means = min(max(BURST - passes, 0), len(means))
+            if plan and len(means) == len(MEAN_TERMS):
+                n_means = 0 if plan[-1][1] else n_means
+            n_means = min(n_means, len(means) - len(MEAN_TERMS)) if len(means) > len(MEAN_TERMS) else n_means
+            plan.append((mine, means[:n_means], max(BURST - passes - n_means, 0)))
+            means = means[n_means:]
+        waiting = []
 
-        def issue_slot():
-            at = issued[0]
-            if at >= len(row):
+        def issue_step(s):
+            group, rest = divmod(s, GROUP_ITEMS)
+            group += 1
+            if group >= N_GROUPS or s < 0:
                 return
-            issued[0] += 1
-            group, units = row[at]
-            if group not in groups:
+            if rest == 0:
                 begin_group(group)
-            passes = 0
-            for unit in units:
-                if unit[0] == "tap":
-                    passes += 2
-                elif unit[0] in ("mean", "ref"):
-                    passes += 1
-            for unit in units:
-                issue(psum, BANKS, group, *unit, spare=(BURST - passes if unit == units[-1] else 0))
+            mine, mean_passes, spare = plan[rest]
+            for unit in mine:
+                bank = psum.tile([P, GROUP_PIXELS], F32, tag="made", bufs=BANKS["made"])
+                made[(group,) + unit] = bank
+            for n in range(spare):
+                product(group, made[(group,) + mine[0]][:], 0, 0, 0, True, True)
+            for unit in mean_passes:
+                issue(psum, BANKS, group, *unit)
+            for unit in mine:
+                if unit[0] != "turn":
+                    fill(group, *unit)
+            for unit in mine:
+                if unit[0] == "turn":
+                    fill(group, *unit)
+            waiting.append((group, mine, [m for m in mean_passes if m[1] == len(MEAN_TERMS) - 1]))
 
-        def collect_slot():
-            at = collected[0]
-            if at >= len(row):
+        def collect_units(first):
+            if not waiting:
                 return
-            collected[0] += 1
-            group, units = row[at]
-            for unit in units:
-                if unit[0] != "make up":
-                    collect(group, *unit)
+            group, mine, mean_ends = waiting[0]
+            for unit in mean_ends + mine[0:1] if first else mine[1:]:
+                collect(group, *unit)
+            if not first:
+                waiting.remove(waiting[0])
 
         slices_at = {}
         works_at = {}
@@ -440,33 +473,29 @@ def tile_capsulelayer_t_kernel(tc, image, weight, bias, out):
                 for number in range(SLICES):
                     slices_at[work0 - 2 * (SLICES - number)] = (b, number)
 
-        turn_output(0)
+        turn(0)
         for s in range(N_ITEMS + 7):
-            if item(s - 5):
-                multiply(nc.vector, s - 5, G_TAPS, REF - G_TAPS)
             ends = item(s - 6)
             if ends and ends[1] < ITERATIONS - 1:
                 keep_total(s - 6)
-            elif ends:
-                leave(s - 6)
-            if issued[0] > collected[0]:
-                collect_slot()
-            issue_slot()
-            if item(s + 1):
-                turn_output(s + 1)
-            if item(s - 5):
-                sum_taps(s - 5)
-            if s % 2 == 1:
-                issue_slot()
-            if item(s):
-                subtract(s)
             if item(s - 3):
                 inverse_root(s - 3)
+            collect_units(True)
+            issue_step(s)
+            turn(s + 1)
+            if item(s):
+                subtract(s)
+            if item(s - 5):
+                multiply(nc.vector, s - 5, G_TAPS, REF - G_TAPS, turned_at[s][:, 2:, :])
+                sum_taps(s - 5)
             if item(s - 1):
                 square(s - 1)
             if item(s - 2):
                 sum_channels(s - 2)
-            collect_slot()
+            if ends and ends[1] == ITERATIONS - 1:
+                leave(s - 6)
+            if len(waiting) > (1 if s < N_ITEMS - GROUP_ITEMS else 0):
+                collect_units(False)
             if s in works_at:
                 input_work(*works_at[s])
             if item(s - 3):
@@ -474,7 +503,8 @@ def tile_capsulelayer_t_kernel(tc, image, weight, bias, out):
                 normalise(s - 3)
                 weighted = work_pool.tile([P, REF, P], F32)
                 items[s - 3]["weighted"] = weighted
-                multiply(nc.gpsimd, s - 3, 0, G_TAPS)
+                group, it, j, feats, half = item(s - 3)
+                multiply(nc.gpsimd, s - 3, 0, G_TAPS, groups[group]["u_pix"][j][:, 0:G_TAPS, feats])
             if item(s):
                 square_output(s)
             if s in slices_at:

@@ -16,16 +16,19 @@ AXIS_X = mybir.AxisListType.X
 P = 128
 PACK = 4
 IMAGES = 4
+CHANNELS = 512
 ROWS = 32
 COLS = 32
 PIXELS = ROWS * COLS
 KS = 3
 TAPS = KS * KS
-REF = TAPS - 1
+REF = 4
+OTHERS = (1, 7, 3, 0, 6, 5, 2, 8)
+N_OTHERS = TAPS - 1
 FEATURES = 256
 CAP_CH = 16
-CAPS = FEATURES // CAP_CH
 HALVES = FEATURES // P
+HALF_CAPS = P // CAP_CH
 ITERATIONS = 3
 EPS = 1e-4
 LIVE = 4
@@ -34,27 +37,23 @@ GROUP_ROWS = GROUP_PIXELS // COLS
 GROUPS_PER_IMAGE = PIXELS // GROUP_PIXELS
 N_GROUPS = IMAGES * GROUPS_PER_IMAGE
 TURN = LIVE * HALVES
-GROUP_ITEMS = TURN * ITERATIONS
-N_ITEMS = N_GROUPS * GROUP_ITEMS
-IMAGE_STEPS = GROUP_ITEMS * GROUPS_PER_IMAGE
-HALF_CAPS = CAPS // HALVES
+GROUP_STEPS = TURN * ITERATIONS
+N_ITEMS = N_GROUPS * GROUP_STEPS
 NEG_REF = TAPS
 NEG_REF8 = TAPS + 1
 W_PLACES = TAPS + 2
-PAIRS = REF // 2
-V_SUBS = REF - 1
+PAIRS = N_OTHERS // 2
 T_PAIR = PAIRS - 1
-G_TAPS = 6
-BURST = 4
-SLOTS_PER_TWO_STEPS = 3
+G_TAPS = N_OTHERS - 2
+T_SUBS = 1
+V_SUBS = N_OTHERS - T_SUBS
+BURST = 3
 EARLY_BANKS = {"made": 6, "sum": 2}
 BANKS = {"made": 3, "sum": 1}
-MEAN_FROM = 14
-INPUT_WORKS = 4
 REGROUP_ROWS = 4
 SLICES = ROWS // REGROUP_ROWS
 
-FLOPS = 2 * IMAGES * PIXELS * 512 * TAPS * FEATURES
+FLOPS = 2 * IMAGES * PIXELS * CHANNELS * TAPS * FEATURES
 
 
 def tile_capsulelayer_t_kernel(tc, image, weight, bias, out):
@@ -66,15 +65,20 @@ def tile_capsulelayer_t_kernel(tc, image, weight, bias, out):
 
         x_grouped = consts.tile([P, ROWS, COLS, PACK], BF16, align_bytes=64)
         x_sets = []
-        for s in range(2):
-            codes = [consts.tile([P, COLS + PIXELS + COLS], U32, name="x_codes%d_%d" % (s, j), align_bytes=64) for j in range(KS)]
-            centre = [consts.tile([P, PIXELS], U8, name="x_centre%d_%d" % (s, j), align_bytes=64) for j in range(KS)]
-            offset = [consts.tile([P, COLS + PIXELS + COLS], U8, name="x_offset%d_%d" % (s, j), align_bytes=64) for j in range(KS)]
-            for j in range(KS):
+        for number in range(2):
+            codes = [consts.tile([P, COLS + PIXELS + COLS], U32, name="x_codes%d_%d" % (number, j), align_bytes=64) for j in range(KS)]
+            centre = [consts.tile([P, PIXELS], U8, name="x_centre%d_%d" % (number, j), align_bytes=64) for j in range(KS)]
+            offset = [consts.tile([P, COLS + PIXELS + COLS], U8, name="x_offset%d_%d" % (number, j), align_bytes=64) for j in range(KS)]
+            x_sets.append((codes, centre, offset))
+
+        def clear_planes(number):
+            codes, centre, offset = x_sets[number]
+            for j in (1, 0, 2):
                 nc.gpsimd.memset(centre[j][:].bitcast(F32), 0.0)
                 nc.gpsimd.memset(codes[j][:].bitcast(F32), 0.0)
                 nc.gpsimd.memset(offset[j][:].bitcast(F32), 0.0)
-            x_sets.append((codes, centre, offset))
+
+        clear_planes(0)
         ident = consts.tile([P, P], F32)
         make_identity(nc, ident[:])
 
@@ -89,29 +93,27 @@ def tile_capsulelayer_t_kernel(tc, image, weight, bias, out):
                 in_=x_raw[:, :, row0 : row0 + n_rows, :].rearrange("p r h w -> p h w r"),
             )
 
+        def quantise_image(b):
+            codes, centre, offset = x_sets[b % 2]
+            nc.vector.quantize_mx(
+                out=codes[1][:, COLS : COLS + PIXELS].bitcast(FP8X4),
+                scales=centre[1][:],
+                in_=x_grouped[:].rearrange("p h w r -> p (h w r)"),
+            )
+
         def columns(ap, lo, hi):
             return ap.rearrange("p (h w) -> p h w", w=COLS)[:, :, lo:hi]
 
-        def input_work(b, number):
+        def shift_columns(b, j):
             codes, centre, offset = x_sets[b % 2]
-            words = [codes[j][:, COLS : COLS + PIXELS].bitcast(I32) for j in range(KS)]
-            if number == 0:
-                nc.vector.quantize_mx(
-                    out=codes[1][:, COLS : COLS + PIXELS].bitcast(FP8X4),
-                    scales=centre[1][:],
-                    in_=x_grouped[:].rearrange("p h w r -> p (h w r)"),
-                )
-            elif number == 1:
-                nc.vector.tensor_copy(out=columns(words[0], 1, COLS), in_=columns(words[1], 0, COLS - 1))
-                nc.vector.tensor_copy(out=columns(words[2], 0, COLS - 1), in_=columns(words[1], 1, COLS))
-            elif number == 2:
-                nc.vector.tensor_copy(out=columns(centre[0][:], 1, COLS), in_=columns(centre[1][:], 0, COLS - 1))
-                nc.vector.tensor_copy(out=columns(centre[2][:], 0, COLS - 1), in_=columns(centre[1][:], 1, COLS))
-            else:
-                for j in range(KS):
-                    nc.vector.tensor_copy(
-                        out=offset[j][:, COLS : COLS + PIXELS].bitcast(I32), in_=centre[j][:].bitcast(I32)
-                    )
+            shift = j - 1
+            to_lo, to_hi = max(0, -shift), COLS - max(0, shift)
+            for plane in ([c[:, COLS : COLS + PIXELS].bitcast(I32) for c in codes], [c[:] for c in centre]):
+                nc.vector.tensor_copy(out=columns(plane[j], to_lo, to_hi), in_=columns(plane[1], to_lo + shift, to_hi + shift))
+
+        def offset_rows(b, j):
+            codes, centre, offset = x_sets[b % 2]
+            nc.vector.tensor_copy(out=offset[j][:, COLS : COLS + PIXELS].bitcast(I32), in_=centre[j][:].bitcast(I32))
 
         def x_window(group, t):
             i, j = divmod(t, KS)
@@ -125,26 +127,29 @@ def tile_capsulelayer_t_kernel(tc, image, weight, bias, out):
                 scales = offset[j][:, start : start + GROUP_PIXELS]
             return words, scales
 
-        raws = {0: load_image(0)}
         w_codes = consts.tile([P, W_PLACES, FEATURES], U32, align_bytes=64)
         w_scales = consts.tile([P, W_PLACES, FEATURES], U8, align_bytes=64)
         bias_bf = consts.tile([P, TAPS * HALVES], BF16)
         w_rows = weight.rearrange("a b c i j (p r) n -> p (a b c i j) r n", r=PACK)
-        with tc.tile_pool(name="head", bufs=1) as head:
+        raws = {}
+        with tc.tile_pool(name="stage", bufs=1) as stage:
             w_raws = {}
-            for i in (KS - 1, 0, 1):
-                w_raw = head.tile([P, KS, PACK, FEATURES], BF16, bufs=KS)
-                nc.sync.dma_start(out=w_raw[:], in_=w_rows[:, KS * i : KS * (i + 1), :, :])
-                w_raws[i] = w_raw
-            with nc.allow_non_contiguous_dma(reason="2304 bias values, one to a partition, once"):
-                nc.sync.dma_start(out=bias_bf[:], in_=bias.rearrange("a b c i j o (g f) -> f (a b c i j o g)", g=HALVES))
+            for t in (REF,) + OTHERS:
+                w_raw = stage.tile([P, PACK, FEATURES], BF16, bufs=TAPS)
+                nc.sync.dma_start(out=w_raw[:], in_=w_rows[:, t, :, :])
+                w_raws[t] = w_raw
+                if t == REF:
+                    raws[0] = load_image(0)
+                if t == OTHERS[0]:
+                    with nc.allow_non_contiguous_dma(reason="2304 bias values, one to a partition, once"):
+                        nc.sync.dma_start(out=bias_bf[:], in_=bias.rearrange("a b c i j o (g f) -> f (a b c i j o g)", g=HALVES))
             w_groupeds = []
             for t in range(W_PLACES):
-                w_grouped = head.tile([P, FEATURES, PACK], BF16, align_bytes=64, bufs=W_PLACES)
+                w_grouped = stage.tile([P, FEATURES, PACK], BF16, align_bytes=64, bufs=W_PLACES)
                 w_groupeds.append(w_grouped)
 
-            def regroup_weights(t, copy):
-                copy(out=w_groupeds[t][:], in_=w_raws[t // KS][:, t % KS, :, :].rearrange("p r n -> p n r"))
+            def regroup_weights(copy, t):
+                copy(out=w_groupeds[t][:], in_=w_raws[t][:].rearrange("p r n -> p n r"))
 
             def quantise_weights(t):
                 nc.vector.quantize_mx(
@@ -153,41 +158,47 @@ def tile_capsulelayer_t_kernel(tc, image, weight, bias, out):
                     in_=w_groupeds[t][:].rearrange("p n r -> p (n r)"),
                 )
 
-            for t in (REF, 0, 2, 4, 6):
-                regroup_weights(t, nc.scalar.copy)
+            regroup_weights(nc.vector.tensor_copy, REF)
+            nc.vector.tensor_scalar_mul(out=w_groupeds[NEG_REF][:], in0=w_groupeds[REF][:], scalar1=-1.0)
+            quantise_weights(NEG_REF)
+            for k in (0, 1, 3, 5):
+                regroup_weights(nc.scalar.copy, OTHERS[k])
             regroup_image(nc.vector.tensor_copy, raws[0], 0, ROWS)
             raws[1] = load_image(1)
-            input_work(0, 0)
-            nc.vector.tensor_scalar_mul(out=w_groupeds[NEG_REF][:], in0=w_groupeds[REF][:], scalar1=-1.0)
-            input_work(0, 1)
-            quantise_weights(NEG_REF)
-            input_work(0, 2)
-            quantise_weights(0)
-            input_work(0, 3)
-            for t in (1, 3, 5, 7):
-                regroup_weights(t, nc.vector.tensor_copy)
-                quantise_weights(t)
-                if t < 7:
-                    quantise_weights(t + 1)
-            nc.vector.tensor_scalar_mul(out=w_groupeds[NEG_REF8][:], in0=w_groupeds[REF][:], scalar1=-8.0)
+            quantise_image(0)
+            offset_rows(0, 1)
+            quantise_weights(OTHERS[0])
+            quantise_weights(OTHERS[1])
+            shift_columns(0, 0)
+            regroup_weights(nc.vector.tensor_copy, OTHERS[2])
+            quantise_weights(OTHERS[2])
+            offset_rows(0, 0)
+            quantise_weights(OTHERS[3])
+            regroup_weights(nc.vector.tensor_copy, OTHERS[4])
+            quantise_weights(OTHERS[4])
+            shift_columns(0, 2)
+            quantise_weights(OTHERS[5])
+            offset_rows(0, 2)
+            for k in (6, 7):
+                regroup_weights(nc.vector.tensor_copy, OTHERS[k])
+                quantise_weights(OTHERS[k])
+            nc.vector.tensor_scalar_mul(out=w_groupeds[NEG_REF8][:], in0=w_groupeds[REF][:], scalar1=1.0 - TAPS)
             quantise_weights(NEG_REF8)
             quantise_weights(REF)
 
         bias_cols = consts.tile([P, TAPS, HALVES], F32)
         nc.gpsimd.tensor_copy(out=bias_cols[:].rearrange("p t g -> p (t g)"), in_=bias_bf[:])
-        bias_rel = consts.tile([P, REF, HALVES], F32)
+        bias_rel = consts.tile([P, TAPS, HALVES], F32)
         nc.gpsimd.tensor_tensor(
-            out=bias_rel[:],
-            in0=bias_cols[:, 0:REF, :],
-            in1=bias_cols[:, REF : REF + 1, :].to_broadcast([P, REF, HALVES]),
-            op=ALU.subtract,
+            out=bias_rel[:], in0=bias_cols[:], in1=bias_cols[:, REF : REF + 1, :].to_broadcast([P, TAPS, HALVES]), op=ALU.subtract
         )
+        clear_planes(1)
         bias_start = consts.tile([P, HALVES], F32)
         nc.vector.tensor_reduce(out=bias_start[:], in_=bias_rel[:].rearrange("p t g -> p g t"), axis=AXIS_X, op=ALU.add)
         nc.vector.tensor_scalar_mul(out=bias_start[:], in0=bias_start[:], scalar1=-1.0 / TAPS)
 
-        group_pool = ctx.enter_context(tc.tile_pool(name="group", bufs=2))
         block_pool = ctx.enter_context(tc.tile_pool(name="block", bufs=2 * LIVE))
+        group_pool = ctx.enter_context(tc.tile_pool(name="group", bufs=2))
         work_pool = ctx.enter_context(tc.tile_pool(name="work", bufs=4))
         item_pool = ctx.enter_context(tc.tile_pool(name="item", bufs=4))
         groups = {}
@@ -198,9 +209,9 @@ def tile_capsulelayer_t_kernel(tc, image, weight, bias, out):
             start_T = group_pool.tile([P, HALVES, GROUP_PIXELS], F32)
             groups[group] = {"ref_T": ref_T, "start_T": start_T, "u_pix": {}, "taps_T": {}}
 
-        def product(group, bank, t_x, w_place, half, start, stop):
+        def product(group, bank, t, w_place, half, start, stop):
             feats = slice(half * P, (half + 1) * P)
-            words, scales = x_window(group, t_x)
+            words, scales = x_window(group, t)
             nc.tensor.matmul_mx(
                 out=bank,
                 lhsT=w_codes[:, w_place, feats].bitcast(FP8X4),
@@ -211,36 +222,43 @@ def tile_capsulelayer_t_kernel(tc, image, weight, bias, out):
                 stop=stop,
             )
 
-        MEAN_TERMS = [(t, t) for t in range(REF)] + [(REF, NEG_REF8)]
+        MEAN_TERMS = [(t, t) for t in OTHERS] + [(REF, NEG_REF8)]
 
-        def issue(pool, banks, group, kind, a, k):
-            if kind == "mean":
-                if a == 0:
-                    sum_bank = pool.tile([P, GROUP_PIXELS], F32, tag="sum", bufs=banks["sum"])
-                    made[group, kind, k] = sum_bank
-                product(group, made[group, kind, k][:], *MEAN_TERMS[a], k, a == 0, a == len(MEAN_TERMS) - 1)
-                return
+        def add_to_mean(pool, banks, group, a, half):
+            if a == 0:
+                sum_bank = pool.tile([P, GROUP_PIXELS], F32, tag="sum", bufs=banks["sum"])
+                made[group, "mean", half] = sum_bank
+            product(group, made[group, "mean", half][:], *MEAN_TERMS[a], half, a == 0, a == len(MEAN_TERMS) - 1)
+
+        def end_mean(group, half):
+            nc.scalar.activation(
+                out=groups[group]["start_T"][:, half, :],
+                in_=made[group, "mean", half][:],
+                func=ACT.Identity,
+                bias=bias_start[:, half : half + 1],
+                scale=-1.0 / TAPS,
+            )
+
+        def new_bank(pool, banks, unit):
             bank = pool.tile([P, GROUP_PIXELS], F32, tag="made", bufs=banks["made"])
-            made[group, kind, a, k] = bank
-            fill(group, kind, a, k)
+            made[unit] = bank
 
-        def fill(group, kind, a, k):
-            g = groups[group]
+        def make(group, kind, a, k):
             bank = made[group, kind, a, k]
             if kind == "turn":
-                for tt in range(1 if a == T_PAIR else 2):
+                for tt in range(N_OTHERS - G_TAPS - T_SUBS if a == T_PAIR else 2):
                     for h in range(HALVES):
-                        to = (HALVES * tt + h) * P
+                        at = HALVES * tt + h
                         nc.tensor.transpose(
-                            bank[:, to : to + P], g["taps_T"][a][:, HALVES * tt + h, k * P : (k + 1) * P], ident[:]
+                            bank[:, at * P : (at + 1) * P], groups[group]["taps_T"][a][:, at, k * P : (k + 1) * P], ident[:]
                         )
             elif kind == "ref":
                 product(group, bank[:], REF, REF, k, True, True)
             else:
-                product(group, bank[:], a, a, k, True, False)
-                product(group, bank[:], REF, NEG_REF, k, False, True)
+                product(group, bank[:], REF, NEG_REF, k, True, False)
+                product(group, bank[:], OTHERS[a], OTHERS[a], k, False, True)
 
-        def empty(dst, src, bias_col, by_vector):
+        def empty(by_vector, dst, src, bias_col):
             if by_vector:
                 nc.vector.tensor_scalar_add(out=dst, in0=src, scalar1=bias_col)
             else:
@@ -248,40 +266,71 @@ def tile_capsulelayer_t_kernel(tc, image, weight, bias, out):
 
         def collect(group, kind, a, k, by_vector=False):
             g = groups[group]
-            if kind == "mean":
-                if a == len(MEAN_TERMS) - 1:
-                    nc.scalar.activation(
-                        out=g["start_T"][:, k, :],
-                        in_=made[group, kind, k][:],
-                        func=ACT.Identity,
-                        bias=bias_start[:, k : k + 1],
-                        scale=-1.0 / TAPS,
-                    )
-                return
             bank = made[group, kind, a, k]
             if kind == "ref":
-                empty(g["ref_T"][:, k, :], bank[:], bias_cols[:, REF, k : k + 1], by_vector)
+                empty(by_vector, g["ref_T"][:, k, :], bank[:], bias_cols[:, REF, k : k + 1])
             elif kind == "tap":
                 pair, tt = divmod(a, 2)
-                if tt == 0 and k == 0:
+                if pair not in g["taps_T"]:
                     if pair == T_PAIR:
                         kept_T = group_pool.tile([P, 2 * HALVES, GROUP_PIXELS], F32)
                         g["taps_T"][pair] = kept_T
                     else:
                         taps_T = group_pool.tile([P, 2 * HALVES, GROUP_PIXELS], F32, bufs=PAIRS - 1)
                         g["taps_T"][pair] = taps_T
-                empty(g["taps_T"][pair][:, HALVES * tt + k, :], bank[:], bias_rel[:, a, k : k + 1], by_vector)
+                t = OTHERS[a]
+                empty(by_vector, g["taps_T"][pair][:, HALVES * tt + k, :], bank[:], bias_rel[:, t, k : k + 1])
             else:
                 if k not in g["u_pix"]:
                     u = block_pool.tile([P, V_SUBS, FEATURES], F32)
                     g["u_pix"][k] = u
-                n_taps = 1 if a == T_PAIR else 2
+                n_taps = N_OTHERS - G_TAPS - T_SUBS if a == T_PAIR else 2
                 dst = g["u_pix"][k][:, 2 * a : 2 * a + n_taps, :].rearrange("p t f -> p (t f)")
-                src = bank[:, 0 : n_taps * FEATURES]
                 if by_vector:
-                    nc.vector.tensor_copy(out=dst, in_=src)
+                    nc.vector.tensor_copy(out=dst, in_=bank[:, 0 : n_taps * FEATURES])
                 else:
-                    nc.scalar.copy(out=dst, in_=src)
+                    nc.scalar.copy(out=dst, in_=bank[:, 0 : n_taps * FEATURES])
+
+        TURN_PAIRS = [pair for pair in range(PAIRS) if pair != T_PAIR or T_SUBS < N_OTHERS - G_TAPS]
+        TAP_UNITS = [("tap", a, h) for a in range(N_OTHERS) for h in range(HALVES)]
+        TURN_UNITS = [("turn", pair, j) for pair in TURN_PAIRS for j in range(LIVE)]
+        REF_UNITS = [("ref", 0, h) for h in range(HALVES)]
+
+        begin_group(0)
+        HEAD_BLOCKS = 4
+        order = []
+        for a in range(N_OTHERS):
+            order += [(0, "tap", a, h) for h in range(HALVES)]
+            if a >= 2 and a % 2 == 0:
+                order += [(0, "turn", (a - 2) // 2, j) for j in range(HEAD_BLOCKS)]
+        LAG = 2
+
+        with tc.psum_pool(name="early", bufs=1) as early:
+            for k, unit in enumerate(order):
+                new_bank(early, EARLY_BANKS, unit)
+                make(*unit)
+                if unit[1] == "tap":
+                    add_to_mean(early, EARLY_BANKS, 0, unit[2], unit[3])
+                if k >= LAG:
+                    collect(*order[k - LAG], by_vector=(k > 6 and k % 2 == 1))
+            for h in range(HALVES):
+                add_to_mean(early, EARLY_BANKS, 0, N_OTHERS, h)
+            for k in range(LAG):
+                collect(*order[k - LAG], by_vector=(k == 0))
+            last = [(0, "turn", T_PAIR, j) for j in range(HEAD_BLOCKS) if T_PAIR in TURN_PAIRS]
+            for unit in last:
+                new_bank(early, EARLY_BANKS, unit)
+                make(*unit)
+            for h in range(HALVES):
+                end_mean(0, h)
+            for unit in last:
+                collect(*unit, by_vector=True)
+            for h in range(HALVES):
+                unit = (0, "ref", 0, h)
+                new_bank(early, EARLY_BANKS, unit)
+                make(*unit)
+                collect(*unit)
+        psum = ctx.enter_context(tc.psum_pool(name="psum", bufs=1))
 
         items = {}
         turned_at = {}
@@ -289,71 +338,47 @@ def tile_capsulelayer_t_kernel(tc, image, weight, bias, out):
         def item(n):
             if n < 0 or n >= N_ITEMS:
                 return None
-            group, rest = divmod(n, GROUP_ITEMS)
+            group, rest = divmod(n, GROUP_STEPS)
             it, rest = divmod(rest, TURN)
             j, half = divmod(rest, HALVES)
-            return group, it, j, slice(half * P, (half + 1) * P), half
-
-        def sum_taps(n):
-            total = psum.tile([P, P], F32, tag="total", bufs=2)
-            items[n]["total"] = total
-            wp = items[n]["weighted"]
-            for t in range(REF):
-                nc.tensor.matmul(
-                    total[:], lhsT=wp[:, t, :], rhs=ident[:], is_transpose=True, start=(t == 0), stop=(t == REF - 1)
-                )
-
-        def keep_total(n):
-            total_T = item_pool.tile([P, P], F32)
-            nc.scalar.mul(out=total_T[:], in_=items[n]["total"][:], mul=-1.0)
-            items[n]["total_T"] = total_T
-
-        def leave(n):
-            group, it, j, feats, half = item(n)
-            out_sb = item_pool.tile([P, P], F32)
-            nc.vector.tensor_tensor(
-                out=out_sb[:], in0=items[n]["total"][:], in1=groups[group]["ref_T"][:, half, j * P : (j + 1) * P], op=ALU.add
-            )
-            b, part = divmod(group, GROUPS_PER_IMAGE)
-            first = GROUP_PIXELS * part + j * P
-            nc.sync.dma_start(
-                out=out[b].rearrange("(g f) h w -> g f (h w)", g=HALVES)[half, :, first : first + P], in_=out_sb[:]
-            )
+            return group, it, j, half, slice(half * P, (half + 1) * P), slice(j * P, (j + 1) * P)
 
         def turn(s):
-            turned = psum.tile([P, 2 + REF - G_TAPS, P], F32, tag="turned", bufs=2)
+            turned = psum.tile([P, T_SUBS + 1 + N_OTHERS - G_TAPS, P], F32, tag="turned", bufs=2)
             turned_at[s] = turned
             if item(s):
-                group, it, j, feats, half = item(s)
-                pixels = slice(j * P, (j + 1) * P)
+                group, it, j, half, feats, pixels = item(s)
                 if it == 0:
                     minus_o = groups[group]["start_T"][:, half, pixels]
                 else:
                     minus_o = items[s - TURN]["total_T"][:]
-                u_T = groups[group]["taps_T"][T_PAIR][:, HALVES + half, pixels]
-                nc.tensor.matmul(turned[:, 0, :], lhsT=u_T, rhs=ident[:], is_transpose=True, start=True, stop=False)
-                nc.tensor.matmul(turned[:, 0, :], lhsT=minus_o, rhs=ident[:], is_transpose=True, start=False, stop=True)
-                nc.tensor.transpose(turned[:, 1, :], minus_o, ident[:])
+                for k in range(T_SUBS):
+                    u_T = groups[group]["taps_T"][T_PAIR][:, HALVES * (2 - T_SUBS + k) + half, pixels]
+                    nc.tensor.matmul(turned[:, k, :], lhsT=u_T, rhs=ident[:], is_transpose=True, start=True, stop=False)
+                    nc.tensor.matmul(turned[:, k, :], lhsT=minus_o, rhs=ident[:], is_transpose=True, start=False, stop=True)
+                nc.tensor.transpose(turned[:, T_SUBS, :], minus_o, ident[:])
                 items[s] = {}
             if item(s - 5):
-                group, it, j, feats, half = item(s - 5)
-                for tt in range(REF - G_TAPS):
-                    u_T = groups[group]["taps_T"][T_PAIR][:, HALVES * tt + half, j * P : (j + 1) * P]
-                    nc.tensor.transpose(turned[:, 2 + tt, :], u_T, ident[:])
+                group, it, j, half, feats, pixels = item(s - 5)
+                for k in range(N_OTHERS - G_TAPS):
+                    u_T = groups[group]["taps_T"][T_PAIR][:, HALVES * k + half, pixels]
+                    nc.tensor.transpose(turned[:, T_SUBS + 1 + k, :], u_T, ident[:])
 
         def subtract(n):
-            group, it, j, feats, half = item(n)
+            group, it, j, half, feats, pixels = item(n)
             d = work_pool.tile([P, TAPS, P], F32)
             items[n]["d"] = d
             nc.vector.tensor_tensor(
                 out=d[:, 0:V_SUBS, :],
                 in0=groups[group]["u_pix"][j][:, :, feats],
-                in1=turned_at[n][:, 1, :].unsqueeze(1).to_broadcast([P, V_SUBS, P]),
+                in1=turned_at[n][:, T_SUBS, :].unsqueeze(1).to_broadcast([P, V_SUBS, P]),
                 op=ALU.add,
             )
 
-        def square_output(n):
-            nc.scalar.activation(out=items[n]["d"][:, V_SUBS:TAPS, :], in_=turned_at[n][:, 0:2, :], func=ACT.Square)
+        def square_turned(n):
+            nc.scalar.activation(
+                out=items[n]["d"][:, V_SUBS:TAPS, :], in_=turned_at[n][:, 0 : T_SUBS + 1, :], func=ACT.Square
+            )
 
         def square(n):
             d = items[n]["d"]
@@ -379,17 +404,18 @@ def tile_capsulelayer_t_kernel(tc, image, weight, bias, out):
             nc.vector.reciprocal(out=cw_inv[:], in_=cw_sum[:])
 
         def normalise(n):
-            share = item_pool.tile([P, REF, HALF_CAPS], F32)
+            share = item_pool.tile([P, N_OTHERS, HALF_CAPS], F32)
             items[n]["share"] = share
             nc.gpsimd.tensor_tensor(
                 out=share[:],
-                in0=items[n]["cw"][:, 0:REF, :],
-                in1=items[n]["cw_inv"][:].unsqueeze(1).to_broadcast([P, REF, HALF_CAPS]),
+                in0=items[n]["cw"][:, 0:N_OTHERS, :],
+                in1=items[n]["cw_inv"][:].unsqueeze(1).to_broadcast([P, N_OTHERS, HALF_CAPS]),
                 op=ALU.mult,
             )
+            weighted = work_pool.tile([P, N_OTHERS, P], F32)
+            items[n]["weighted"] = weighted
 
-        def multiply(engine, n, tap0, n_taps, priors):
-            taps = slice(tap0, tap0 + n_taps)
+        def multiply(engine, n, taps, n_taps, priors):
             engine.tensor_tensor(
                 out=items[n]["weighted"][:, taps, :].rearrange("p t (c k) -> p t c k", k=CAP_CH),
                 in0=priors.rearrange("p t (c k) -> p t c k", k=CAP_CH),
@@ -397,116 +423,153 @@ def tile_capsulelayer_t_kernel(tc, image, weight, bias, out):
                 op=ALU.mult,
             )
 
-        TAP_UNITS = [("tap", t, h) for t in range(REF) for h in range(HALVES)]
-        MEAN_UNITS = [("mean", a, h) for h in range(HALVES) for a in range(len(MEAN_TERMS))]
-        TURN_UNITS = [("turn", pair, j) for j in range(LIVE) for pair in range(PAIRS)]
-        REF_UNITS = [("ref", 0, h) for h in range(HALVES)]
-        TURN_BY_PAIR = [("turn", pair, j) for pair in range(PAIRS) for j in range(LIVE)]
+        def sum_taps(n):
+            total = psum.tile([P, P], F32, tag="total", bufs=2)
+            items[n]["total"] = total
+            for k in range(N_OTHERS):
+                nc.tensor.matmul(
+                    total[:],
+                    lhsT=items[n]["weighted"][:, k, :],
+                    rhs=ident[:],
+                    is_transpose=True,
+                    start=(k == 0),
+                    stop=(k == N_OTHERS - 1),
+                )
+
+        def keep_total(n):
+            total_T = item_pool.tile([P, P], F32)
+            nc.scalar.mul(out=total_T[:], in_=items[n]["total"][:], mul=-1.0)
+            items[n]["total_T"] = total_T
+
+        def leave(n):
+            group, it, j, half, feats, pixels = item(n)
+            out_sb = item_pool.tile([P, P], F32)
+            nc.vector.tensor_tensor(
+                out=out_sb[:], in0=items[n]["total"][:], in1=groups[group]["ref_T"][:, half, pixels], op=ALU.add
+            )
+            b, part = divmod(group, GROUPS_PER_IMAGE)
+            first = GROUP_PIXELS * part + j * P
+            nc.sync.dma_start(
+                out=out[b].rearrange("(g f) h w -> f g (h w)", g=HALVES)[:, half, first : first + P], in_=out_sb[:]
+            )
+
+        plan = {}
+        mean_plan = {}
         PASSES = {"tap": 2, "ref": 1, "turn": 0}
 
-        begin_group(0)
-        head_units = TAP_UNITS + MEAN_UNITS + TURN_UNITS + REF_UNITS
-        with tc.psum_pool(name="early", bufs=1) as early:
-            for k, unit in enumerate(head_units):
-                issue(early, EARLY_BANKS, 0, *unit)
-                if k > 0:
-                    collect(0, *head_units[k - 1], by_vector=(k % 2 == 1))
-            collect(0, *head_units[-1])
-        psum = ctx.enter_context(tc.psum_pool(name="psum", bufs=1))
+        def put(s, unit, by_vector=False):
+            plan.setdefault(s, []).append((unit, by_vector))
 
-        units = list(TAP_UNITS[: 2 * PACK])
-        for k in range(2 * PACK, len(TAP_UNITS)):
-            units += [TURN_BY_PAIR[k - 2 * PACK], TAP_UNITS[k]]
-        units += REF_UNITS + TURN_BY_PAIR[2 * PACK :]
-        plan = []
-        means = list(MEAN_UNITS)
-        for s in range(GROUP_ITEMS):
-            mine = units[len(units) * s // GROUP_ITEMS : len(units) * (s + 1) // GROUP_ITEMS]
-            passes = sum([PASSES[unit[0]] for unit in mine])
-            n_means = min(max(BURST - passes, 0), len(means))
-            if plan and len(means) == len(MEAN_TERMS):
-                n_means = 0 if plan[-1][1] else n_means
-            n_means = min(n_means, len(means) - len(MEAN_TERMS)) if len(means) > len(MEAN_TERMS) else n_means
-            plan.append((mine, means[:n_means], max(BURST - passes - n_means, 0)))
-            means = means[n_means:]
-        waiting = []
+        late_units = [(0, "turn", pair, j) for j in range(HEAD_BLOCKS, LIVE) for pair in TURN_PAIRS]
+        for k, unit in enumerate(late_units):
+            put(k // 2, unit, by_vector=(k % 2 == 0))
+        units = TAP_UNITS[: 4 * HALVES]
+        for k in range(4 * HALVES, len(TAP_UNITS)):
+            units = units + [TURN_UNITS[k - 4 * HALVES], TAP_UNITS[k]]
+        units = units + REF_UNITS + TURN_UNITS[len(TAP_UNITS) - 4 * HALVES :]
+        for group in range(1, N_GROUPS):
+            start = GROUP_STEPS * (group - 1)
+            first = 0 if group == 1 else 0
+            for k, unit in enumerate(units):
+                put(start + first + (GROUP_STEPS - first) * k // len(units), (group,) + unit)
+            s = start + first
+            for half in range(HALVES):
+                terms = list(range(len(MEAN_TERMS)))
+                while terms:
+                    passes = sum([PASSES[unit[1]] for unit, by_vector in plan.get(s, [])])
+                    n_terms = min(max(BURST - passes, 0), len(terms))
+                    mean_plan[s] = [(group, a, half) for a in terms[:n_terms]]
+                    terms = terms[n_terms:]
+                    s += 1
+                s += 1
 
-        def issue_step(s):
-            group, rest = divmod(s, GROUP_ITEMS)
-            group += 1
-            if group >= N_GROUPS or s < 0:
-                return
-            if rest == 0:
-                begin_group(group)
-            mine, mean_passes, spare = plan[rest]
+        def prepare(s):
+            mine = [unit for unit, by_vector in plan.get(s, [])]
+            terms = mean_plan.get(s, [])
             for unit in mine:
-                bank = psum.tile([P, GROUP_PIXELS], F32, tag="made", bufs=BANKS["made"])
-                made[(group,) + unit] = bank
-            for n in range(spare):
-                product(group, made[(group,) + mine[0]][:], 0, 0, 0, True, True)
-            for unit in mean_passes:
-                issue(psum, BANKS, group, *unit)
+                if unit[0] not in groups:
+                    begin_group(unit[0])
+                new_bank(psum, BANKS, unit)
+            spare = BURST - len(terms) - sum([PASSES[unit[1]] for unit in mine])
+            if mine and s < N_ITEMS - GROUP_STEPS:
+                for n in range(spare):
+                    product(mine[0][0], made[mine[0]][:], REF, REF, 0, True, True)
+            for term in terms:
+                add_to_mean(psum, BANKS, *term)
             for unit in mine:
-                if unit[0] != "turn":
-                    fill(group, *unit)
+                if unit[1] != "turn":
+                    make(*unit)
             for unit in mine:
-                if unit[0] == "turn":
-                    fill(group, *unit)
-            waiting.append((group, mine, [m for m in mean_passes if m[1] == len(MEAN_TERMS) - 1]))
+                if unit[1] == "turn":
+                    make(*unit)
 
-        def collect_units(first):
-            if not waiting:
-                return
-            group, mine, mean_ends = waiting[0]
-            for unit in mean_ends + mine[0:1] if first else mine[1:]:
-                collect(group, *unit)
-            if not first:
-                waiting.remove(waiting[0])
+        def collect_made(s, number):
+            if number == 0:
+                for group, a, half in mean_plan.get(s, []):
+                    if a == len(MEAN_TERMS) - 1:
+                        end_mean(group, half)
+            for unit, by_vector in plan.get(s, [])[:1] if number == 0 else plan.get(s, [])[1:]:
+                if not by_vector:
+                    collect(*unit)
+
+        def collect_by_vector(s):
+            for unit, by_vector in plan.get(s, []):
+                if by_vector:
+                    collect(*unit, by_vector=True)
 
         slices_at = {}
-        works_at = {}
+        image_work = {}
         for b in range(1, IMAGES):
-            work0 = IMAGE_STEPS * (b - 1) + GROUP_ITEMS // 2
-            for number in range(INPUT_WORKS):
-                works_at[work0 + 2 * number] = (b, number)
-            if b > 1:
-                for number in range(SLICES):
-                    slices_at[work0 - 2 * (SLICES - number)] = (b, number)
+            ready = GROUP_STEPS * GROUPS_PER_IMAGE * (b - 1) + GROUP_STEPS // 2
+            for number in range(2 * KS):
+                image_work[ready + 2 * number - 2] = (b, number)
+            for number in range(SLICES):
+                if b > 1:
+                    slices_at[ready - 4 - 2 * (SLICES - 1 - number)] = (b, number)
+
+        def work_on_image(b, number):
+            if number == 0:
+                quantise_image(b)
+            elif number == 1:
+                offset_rows(b, 1)
+            elif number % 2 == 0:
+                shift_columns(b, number - 2)
+            else:
+                offset_rows(b, number - 3)
 
         turn(0)
-        for s in range(N_ITEMS + 7):
-            ends = item(s - 6)
-            if ends and ends[1] < ITERATIONS - 1:
-                keep_total(s - 6)
+        for s in range(N_ITEMS + 6):
+            if item(s - 6):
+                sum_taps(s - 6)
             if item(s - 3):
                 inverse_root(s - 3)
-            collect_units(True)
-            issue_step(s)
+            collect_made(s - 1, 0)
+            prepare(s)
             turn(s + 1)
             if item(s):
                 subtract(s)
             if item(s - 5):
-                multiply(nc.vector, s - 5, G_TAPS, REF - G_TAPS, turned_at[s][:, 2:, :])
-                sum_taps(s - 5)
+                multiply(nc.vector, s - 5, slice(G_TAPS, N_OTHERS), N_OTHERS - G_TAPS, turned_at[s][:, T_SUBS + 1 :, :])
             if item(s - 1):
                 square(s - 1)
             if item(s - 2):
                 sum_channels(s - 2)
-            if ends and ends[1] == ITERATIONS - 1:
+            collect_by_vector(s - 1)
+            ends = item(s - 6)
+            if ends and ends[1] < ITERATIONS - 1:
+                keep_total(s - 6)
+            elif ends:
                 leave(s - 6)
-            if len(waiting) > (1 if s < N_ITEMS - GROUP_ITEMS else 0):
-                collect_units(False)
-            if s in works_at:
-                input_work(*works_at[s])
+            collect_made(s - 1, 1)
+            if s in image_work:
+                work_on_image(*image_work[s])
             if item(s - 3):
                 sum_weights(s - 3)
                 normalise(s - 3)
-                weighted = work_pool.tile([P, REF, P], F32)
-                items[s - 3]["weighted"] = weighted
-                group, it, j, feats, half = item(s - 3)
-                multiply(nc.gpsimd, s - 3, 0, G_TAPS, groups[group]["u_pix"][j][:, 0:G_TAPS, feats])
+                group, it, j, half, feats, pixels = item(s - 3)
+                multiply(nc.gpsimd, s - 3, slice(0, G_TAPS), G_TAPS, groups[group]["u_pix"][j][:, 0:G_TAPS, feats])
             if item(s):
-                square_output(s)
+                square_turned(s)
             if s in slices_at:
                 b, number = slices_at[s]
                 regroup_image(nc.scalar.copy, raws[b], REGROUP_ROWS * number, REGROUP_ROWS)

@@ -398,10 +398,13 @@ def tile_capsulelayer_t_kernel(tc, image, weight, bias, out):
 
         def sum_weights(n):
             cw_sum = item_pool.tile([P, HALF_CAPS], F32)
+            items[n]["cw_sum"] = cw_sum
             nc.vector.tensor_reduce(out=cw_sum[:], in_=items[n]["cw"][:].rearrange("p t c -> p c t"), axis=AXIS_X, op=ALU.add)
+
+        def invert_sum(n):
             cw_inv = item_pool.tile([P, HALF_CAPS], F32)
             items[n]["cw_inv"] = cw_inv
-            nc.vector.reciprocal(out=cw_inv[:], in_=cw_sum[:])
+            nc.vector.reciprocal(out=cw_inv[:], in_=items[n]["cw_sum"][:])
 
         def normalise(n):
             share = item_pool.tile([P, N_OTHERS, HALF_CAPS], F32)
@@ -543,17 +546,25 @@ def tile_capsulelayer_t_kernel(tc, image, weight, bias, out):
                 sum_taps(s - 6)
             if item(s - 3):
                 inverse_root(s - 3)
+            if item(s - 2):
+                sum_channels(s - 2)
+            if item(s - 1):
+                square_turned(s - 1)
+                square(s - 1)
             collect_made(s - 1, 0)
             prepare(s)
             turn(s + 1)
+            if item(s - 3):
+                sum_weights(s - 3)
             if item(s):
                 subtract(s)
+            if item(s - 3):
+                invert_sum(s - 3)
+                normalise(s - 3)
+                group, it, j, half, feats, pixels = item(s - 3)
+                multiply(nc.gpsimd, s - 3, slice(0, G_TAPS), G_TAPS, groups[group]["u_pix"][j][:, 0:G_TAPS, feats])
             if item(s - 5):
                 multiply(nc.vector, s - 5, slice(G_TAPS, N_OTHERS), N_OTHERS - G_TAPS, turned_at[s][:, T_SUBS + 1 :, :])
-            if item(s - 1):
-                square(s - 1)
-            if item(s - 2):
-                sum_channels(s - 2)
             collect_by_vector(s - 1)
             ends = item(s - 6)
             if ends and ends[1] < ITERATIONS - 1:
@@ -563,13 +574,6 @@ def tile_capsulelayer_t_kernel(tc, image, weight, bias, out):
             collect_made(s - 1, 1)
             if s in image_work:
                 work_on_image(*image_work[s])
-            if item(s - 3):
-                sum_weights(s - 3)
-                normalise(s - 3)
-                group, it, j, half, feats, pixels = item(s - 3)
-                multiply(nc.gpsimd, s - 3, slice(0, G_TAPS), G_TAPS, groups[group]["u_pix"][j][:, 0:G_TAPS, feats])
-            if item(s):
-                square_turned(s)
             if s in slices_at:
                 b, number = slices_at[s]
                 regroup_image(nc.scalar.copy, raws[b], REGROUP_ROWS * number, REGROUP_ROWS)

@@ -44,9 +44,10 @@ NEG_REF8 = TAPS + 1
 W_PLACES = TAPS + 2
 PAIRS = N_OTHERS // 2
 T_PAIR = PAIRS - 1
-G_TAPS = N_OTHERS - 2
-T_SUBS = 1
-V_SUBS = N_OTHERS - T_SUBS
+G_TAPS = (7, 6)
+T_SUBS = (1, 2)
+TURNED_PLACES = max([1 + T_SUBS[h] + N_OTHERS - G_TAPS[1 - h] for h in range(HALVES)])
+U_TAPS = tuple([max(G_TAPS[h], N_OTHERS - T_SUBS[h]) for h in range(HALVES)])
 BURST = 3
 EARLY_BANKS = {"made": 6, "sum": 2}
 BANKS = {"made": 3, "sum": 1}
@@ -246,12 +247,13 @@ def tile_capsulelayer_t_kernel(tc, image, weight, bias, out):
         def make(group, kind, a, k):
             bank = made[group, kind, a, k]
             if kind == "turn":
-                for tt in range(N_OTHERS - G_TAPS - T_SUBS if a == T_PAIR else 2):
+                for tt in range(2):
                     for h in range(HALVES):
                         at = HALVES * tt + h
-                        nc.tensor.transpose(
-                            bank[:, at * P : (at + 1) * P], groups[group]["taps_T"][a][:, at, k * P : (k + 1) * P], ident[:]
-                        )
+                        if 2 * a + tt < U_TAPS[h]:
+                            nc.tensor.transpose(
+                                bank[:, at * P : (at + 1) * P], groups[group]["taps_T"][a][:, at, k * P : (k + 1) * P], ident[:]
+                            )
             elif kind == "ref":
                 product(group, bank[:], REF, REF, k, True, True)
             else:
@@ -282,16 +284,16 @@ def tile_capsulelayer_t_kernel(tc, image, weight, bias, out):
                 empty(by_vector, g["taps_T"][pair][:, HALVES * tt + k, :], bank[:], bias_rel[:, t, k : k + 1])
             else:
                 if k not in g["u_pix"]:
-                    u = block_pool.tile([P, V_SUBS, FEATURES], F32)
+                    u = block_pool.tile([P, max(U_TAPS), FEATURES], F32)
                     g["u_pix"][k] = u
-                n_taps = N_OTHERS - G_TAPS - T_SUBS if a == T_PAIR else 2
-                dst = g["u_pix"][k][:, 2 * a : 2 * a + n_taps, :].rearrange("p t f -> p (t f)")
+                n_columns = sum([P for tt in range(2) for h in range(HALVES) if 2 * a + tt < U_TAPS[h]])
+                dst = g["u_pix"][k][:].rearrange("p t f -> p (t f)")[:, 2 * a * FEATURES : 2 * a * FEATURES + n_columns]
                 if by_vector:
-                    nc.vector.tensor_copy(out=dst, in_=bank[:, 0 : n_taps * FEATURES])
+                    nc.vector.tensor_copy(out=dst, in_=bank[:, 0:n_columns])
                 else:
-                    nc.scalar.copy(out=dst, in_=bank[:, 0 : n_taps * FEATURES])
+                    nc.scalar.copy(out=dst, in_=bank[:, 0:n_columns])
 
-        TURN_PAIRS = [pair for pair in range(PAIRS) if pair != T_PAIR or T_SUBS < N_OTHERS - G_TAPS]
+        TURN_PAIRS = [pair for pair in range(PAIRS) if 2 * pair < max(U_TAPS)]
         TAP_UNITS = [("tap", a, h) for a in range(N_OTHERS) for h in range(HALVES)]
         TURN_UNITS = [("turn", pair, j) for pair in TURN_PAIRS for j in range(LIVE)]
         REF_UNITS = [("ref", 0, h) for h in range(HALVES)]
@@ -343,46 +345,55 @@ def tile_capsulelayer_t_kernel(tc, image, weight, bias, out):
             j, half = divmod(rest, HALVES)
             return group, it, j, half, slice(half * P, (half + 1) * P), slice(j * P, (j + 1) * P)
 
+        def first_multiplied(s):
+            return 1 + T_SUBS[s % HALVES]
+
         def turn(s):
-            turned = psum.tile([P, T_SUBS + 1 + N_OTHERS - G_TAPS, P], F32, tag="turned", bufs=2)
+            turned = psum.tile([P, TURNED_PLACES, P], F32, tag="turned", bufs=2)
             turned_at[s] = turned
+            at_multiplied = first_multiplied(s)
             if item(s):
                 group, it, j, half, feats, pixels = item(s)
                 if it == 0:
                     minus_o = groups[group]["start_T"][:, half, pixels]
                 else:
                     minus_o = items[s - TURN]["total_T"][:]
-                for k in range(T_SUBS):
-                    u_T = groups[group]["taps_T"][T_PAIR][:, HALVES * (2 - T_SUBS + k) + half, pixels]
+                n_subs = T_SUBS[half]
+                for k in range(n_subs):
+                    u_T = groups[group]["taps_T"][T_PAIR][:, HALVES * (2 - n_subs + k) + half, pixels]
                     nc.tensor.matmul(turned[:, k, :], lhsT=u_T, rhs=ident[:], is_transpose=True, start=True, stop=False)
                     nc.tensor.matmul(turned[:, k, :], lhsT=minus_o, rhs=ident[:], is_transpose=True, start=False, stop=True)
-                nc.tensor.transpose(turned[:, T_SUBS, :], minus_o, ident[:])
+                nc.tensor.transpose(turned[:, n_subs, :], minus_o, ident[:])
                 items[s] = {}
             if item(s - 5):
                 group, it, j, half, feats, pixels = item(s - 5)
-                for k in range(N_OTHERS - G_TAPS):
-                    u_T = groups[group]["taps_T"][T_PAIR][:, HALVES * k + half, pixels]
-                    nc.tensor.transpose(turned[:, T_SUBS + 1 + k, :], u_T, ident[:])
+                for k in range(G_TAPS[half], N_OTHERS):
+                    u_T = groups[group]["taps_T"][T_PAIR][:, HALVES * (k - 2 * T_PAIR) + half, pixels]
+                    nc.tensor.transpose(turned[:, at_multiplied + k - G_TAPS[half], :], u_T, ident[:])
 
         def subtract(n):
             group, it, j, half, feats, pixels = item(n)
             d = work_pool.tile([P, TAPS, P], F32)
             items[n]["d"] = d
+            v_subs = N_OTHERS - T_SUBS[half]
             nc.vector.tensor_tensor(
-                out=d[:, 0:V_SUBS, :],
-                in0=groups[group]["u_pix"][j][:, :, feats],
-                in1=turned_at[n][:, T_SUBS, :].unsqueeze(1).to_broadcast([P, V_SUBS, P]),
+                out=d[:, 0:v_subs, :],
+                in0=groups[group]["u_pix"][j][:, 0:v_subs, feats],
+                in1=turned_at[n][:, T_SUBS[half], :].unsqueeze(1).to_broadcast([P, v_subs, P]),
                 op=ALU.add,
             )
 
         def square_turned(n):
+            group, it, j, half, feats, pixels = item(n)
+            n_turned = T_SUBS[half] + 1
             nc.scalar.activation(
-                out=items[n]["d"][:, V_SUBS:TAPS, :], in_=turned_at[n][:, 0 : T_SUBS + 1, :], func=ACT.Square
+                out=items[n]["d"][:, TAPS - n_turned : TAPS, :], in_=turned_at[n][:, 0:n_turned, :], func=ACT.Square
             )
 
         def square(n):
-            d = items[n]["d"]
-            nc.scalar.activation(out=d[:, 0:V_SUBS, :], in_=d[:, 0:V_SUBS, :], func=ACT.Square)
+            group, it, j, half, feats, pixels = item(n)
+            diff = items[n]["d"][:, 0 : N_OTHERS - T_SUBS[half], :]
+            nc.scalar.activation(out=diff, in_=diff, func=ACT.Square)
 
         def sum_channels(n):
             dist = item_pool.tile([P, TAPS, HALF_CAPS], F32)
@@ -546,14 +557,20 @@ def tile_capsulelayer_t_kernel(tc, image, weight, bias, out):
                 sum_taps(s - 6)
             if item(s - 3):
                 inverse_root(s - 3)
-            if item(s - 2):
-                sum_channels(s - 2)
             if item(s - 1):
                 square_turned(s - 1)
                 square(s - 1)
             collect_made(s - 1, 0)
             prepare(s)
             turn(s + 1)
+            if item(s - 2):
+                sum_channels(s - 2)
+            if item(s - 5):
+                group, it, j, half, feats, pixels = item(s - 5)
+                n_taps = N_OTHERS - G_TAPS[half]
+                at = first_multiplied(s)
+                priors = turned_at[s][:, at : at + n_taps, :]
+                multiply(nc.vector, s - 5, slice(G_TAPS[half], N_OTHERS), n_taps, priors)
             if item(s - 3):
                 sum_weights(s - 3)
             if item(s):
@@ -562,9 +579,8 @@ def tile_capsulelayer_t_kernel(tc, image, weight, bias, out):
                 invert_sum(s - 3)
                 normalise(s - 3)
                 group, it, j, half, feats, pixels = item(s - 3)
-                multiply(nc.gpsimd, s - 3, slice(0, G_TAPS), G_TAPS, groups[group]["u_pix"][j][:, 0:G_TAPS, feats])
-            if item(s - 5):
-                multiply(nc.vector, s - 5, slice(G_TAPS, N_OTHERS), N_OTHERS - G_TAPS, turned_at[s][:, T_SUBS + 1 :, :])
+                n_taps = G_TAPS[half]
+                multiply(nc.gpsimd, s - 3, slice(0, n_taps), n_taps, groups[group]["u_pix"][j][:, 0:n_taps, feats])
             collect_by_vector(s - 1)
             ends = item(s - 6)
             if ends and ends[1] < ITERATIONS - 1:

@@ -51,6 +51,7 @@ U_TAPS = tuple([max(G_TAPS[h], N_OTHERS - T_SUBS[h]) for h in range(HALVES)])
 BURST = 3
 EARLY_BANKS = {"made": 6, "sum": 2}
 BANKS = {"made": 3, "sum": 1}
+LOAD_ROWS = 16
 REGROUP_ROWS = 4
 SLICES = ROWS // REGROUP_ROWS
 
@@ -62,7 +63,7 @@ def tile_capsulelayer_t_kernel(tc, image, weight, bias, out):
     with ExitStack() as ctx:
         ctx.enter_context(tc.manual_schedule())
         consts = ctx.enter_context(tc.tile_pool(name="consts", bufs=1))
-        images = ctx.enter_context(tc.tile_pool(name="images", bufs=1))
+        images = ctx.enter_context(tc.tile_pool(name="images", bufs=ROWS // LOAD_ROWS))
 
         x_grouped = consts.tile([P, ROWS, COLS, PACK], BF16, align_bytes=64)
         x_sets = []
@@ -83,15 +84,19 @@ def tile_capsulelayer_t_kernel(tc, image, weight, bias, out):
         ident = consts.tile([P, P], F32)
         make_identity(nc, ident[:])
 
-        def load_image(b):
-            x_raw = images.tile([P, PACK, ROWS, COLS], BF16)
-            nc.sync.dma_start(out=x_raw[:], in_=image[b].rearrange("(p r) h w -> p r h w", r=PACK))
-            return x_raw
+        raws = {}
 
-        def regroup_image(copy, x_raw, row0, n_rows):
+        def load_rows(b, part):
+            x_raw = images.tile([P, PACK, LOAD_ROWS, COLS], BF16)
+            raws[b, part] = x_raw
+            rows = slice(part * LOAD_ROWS, (part + 1) * LOAD_ROWS)
+            nc.sync.dma_start(out=x_raw[:], in_=image[b].rearrange("(p r) h w -> p r h w", r=PACK)[:, :, rows, :])
+
+        def regroup_rows(copy, b, row0, n_rows):
+            part, first = divmod(row0, LOAD_ROWS)
             copy(
                 out=x_grouped[:, row0 : row0 + n_rows, :, :],
-                in_=x_raw[:, :, row0 : row0 + n_rows, :].rearrange("p r h w -> p h w r"),
+                in_=raws[b, part][:, :, first : first + n_rows, :].rearrange("p r h w -> p h w r"),
             )
 
         def quantise_image(b):
@@ -132,7 +137,6 @@ def tile_capsulelayer_t_kernel(tc, image, weight, bias, out):
         w_scales = consts.tile([P, W_PLACES, FEATURES], U8, align_bytes=64)
         bias_bf = consts.tile([P, TAPS * HALVES], BF16)
         w_rows = weight.rearrange("a b c i j (p r) n -> p (a b c i j) r n", r=PACK)
-        raws = {}
         with tc.tile_pool(name="stage", bufs=1) as stage:
             w_raws = {}
             for t in (REF,) + OTHERS:
@@ -140,8 +144,9 @@ def tile_capsulelayer_t_kernel(tc, image, weight, bias, out):
                 nc.sync.dma_start(out=w_raw[:], in_=w_rows[:, t, :, :])
                 w_raws[t] = w_raw
                 if t == REF:
-                    raws[0] = load_image(0)
+                    load_rows(0, 0)
                 if t == OTHERS[0]:
+                    load_rows(0, 1)
                     with nc.allow_non_contiguous_dma(reason="2304 bias values, one to a partition, once"):
                         nc.sync.dma_start(out=bias_bf[:], in_=bias.rearrange("a b c i j o (g f) -> f (a b c i j o g)", g=HALVES))
             w_groupeds = []
@@ -161,14 +166,16 @@ def tile_capsulelayer_t_kernel(tc, image, weight, bias, out):
 
             regroup_weights(nc.vector.tensor_copy, REF)
             nc.vector.tensor_scalar_mul(out=w_groupeds[NEG_REF][:], in0=w_groupeds[REF][:], scalar1=-1.0)
-            quantise_weights(NEG_REF)
             for k in (0, 1, 3, 5):
                 regroup_weights(nc.scalar.copy, OTHERS[k])
-            regroup_image(nc.vector.tensor_copy, raws[0], 0, ROWS)
-            raws[1] = load_image(1)
+            regroup_rows(nc.vector.tensor_copy, 0, 0, LOAD_ROWS)
+            load_rows(1, 0)
+            quantise_weights(NEG_REF)
+            regroup_rows(nc.vector.tensor_copy, 0, LOAD_ROWS, LOAD_ROWS)
+            load_rows(1, 1)
             quantise_image(0)
-            offset_rows(0, 1)
             quantise_weights(OTHERS[0])
+            offset_rows(0, 1)
             quantise_weights(OTHERS[1])
             shift_columns(0, 0)
             regroup_weights(nc.vector.tensor_copy, OTHERS[2])
@@ -314,7 +321,7 @@ def tile_capsulelayer_t_kernel(tc, image, weight, bias, out):
                 if unit[1] == "tap":
                     add_to_mean(early, EARLY_BANKS, 0, unit[2], unit[3])
                 if k >= LAG:
-                    collect(*order[k - LAG], by_vector=(k > 6 and k % 2 == 1))
+                    collect(*order[k - LAG], by_vector=(k > 8 and k % 2 == 1))
             for h in range(HALVES):
                 add_to_mean(early, EARLY_BANKS, 0, N_OTHERS, h)
             for k in range(LAG):
@@ -592,9 +599,11 @@ def tile_capsulelayer_t_kernel(tc, image, weight, bias, out):
                 work_on_image(*image_work[s])
             if s in slices_at:
                 b, number = slices_at[s]
-                regroup_image(nc.scalar.copy, raws[b], REGROUP_ROWS * number, REGROUP_ROWS)
+                regroup_rows(nc.scalar.copy, b, REGROUP_ROWS * number, REGROUP_ROWS)
                 if number == SLICES - 1 and b + 1 < IMAGES:
-                    raws[b + 1] = load_image(b + 1)
+                    load_rows(b + 1, 0)
+                    load_rows(b + 1, 1)
             if s == 1:
-                regroup_image(nc.vector.tensor_copy, raws[1], 0, ROWS)
-                raws[2] = load_image(2)
+                for part in range(ROWS // LOAD_ROWS):
+                    regroup_rows(nc.vector.tensor_copy, 1, part * LOAD_ROWS, LOAD_ROWS)
+                    load_rows(2, part)

@@ -114,12 +114,23 @@ def tile_capsulelayer_t_kernel(tc, image, weight, bias, out):
             codes, centre, offset = x_sets[b % 2]
             shift = j - 1
             to_lo, to_hi = max(0, -shift), COLS - max(0, shift)
-            for plane in ([c[:, COLS : COLS + PIXELS].bitcast(I32) for c in codes], [c[:] for c in centre]):
-                nc.vector.tensor_copy(out=columns(plane[j], to_lo, to_hi), in_=columns(plane[1], to_lo + shift, to_hi + shift))
+            words = [c[:, COLS : COLS + PIXELS].bitcast(I32) for c in codes]
+            to, source = columns(words[j], to_lo, to_hi), columns(words[1], to_lo + shift, to_hi + shift)
+            if b == 0:
+                nc.vector.tensor_copy(out=to, in_=source)
+            else:
+                nc.sync.dma_start(out=to, in_=source)
+            nc.vector.tensor_copy(
+                out=columns(centre[j][:], to_lo, to_hi), in_=columns(centre[1][:], to_lo + shift, to_hi + shift)
+            )
 
         def offset_rows(b, j):
             codes, centre, offset = x_sets[b % 2]
-            nc.vector.tensor_copy(out=offset[j][:, COLS : COLS + PIXELS].bitcast(I32), in_=centre[j][:].bitcast(I32))
+            to, source = offset[j][:, COLS : COLS + PIXELS].bitcast(I32), centre[j][:].bitcast(I32)
+            if b == 0:
+                nc.vector.tensor_copy(out=to, in_=source)
+            else:
+                nc.sync.dma_start(out=to, in_=source)
 
         def x_window(group, t):
             i, j = divmod(t, KS)

from contextlib import ExitStack

import concourse.mybir as mybir
from concourse.masks import make_identity

F32 = mybir.dt.float32
BF16 = mybir.dt.bfloat16
U32 = mybir.dt.uint32
U8 = mybir.dt.uint8
I32 = mybir.dt.int32
FP8X4 = mybir.dt.float8_e4m3fn_x4
ALU = mybir.AluOpType
ACT = mybir.ActivationFunctionType
AXIS_X = mybir.AxisListType.X

P = 128
PACK = 4
IMAGES = 4
CHANNELS = 512
ROWS = 32
COLS = 32
PIXELS = ROWS * COLS
KS = 3
TAPS = KS * KS
REF = 4
OTHERS = (1, 7, 3, 0, 6, 5, 2, 8)
N_OTHERS = TAPS - 1
FEATURES = 256
CAP_CH = 16
HALVES = FEATURES // P
HALF_CAPS = P // CAP_CH
ITERATIONS = 3
EPS = 1e-4
LIVE = 4
GROUP_PIXELS = LIVE * P
GROUP_ROWS = GROUP_PIXELS // COLS
GROUPS_PER_IMAGE = PIXELS // GROUP_PIXELS
N_GROUPS = IMAGES * GROUPS_PER_IMAGE
TURN = LIVE * HALVES
GROUP_STEPS = TURN * ITERATIONS
N_ITEMS = N_GROUPS * GROUP_STEPS
NEG_REF = TAPS
NEG_REF8 = TAPS + 1
W_PLACES = TAPS + 2
PAIRS = N_OTHERS // 2
T_PAIR = PAIRS - 1
G_TAPS = (7, 6)
T_SUBS = (1, 2)
TURNED_PLACES = max([1 + T_SUBS[h] + N_OTHERS - G_TAPS[1 - h] for h in range(HALVES)])
U_TAPS = tuple([max(G_TAPS[h], N_OTHERS - T_SUBS[h]) for h in range(HALVES)])
BURST = 3
EARLY_BANKS = {"made": 6, "sum": 2}
BANKS = {"made": 3, "sum": 1}
LOAD_ROWS = 16
REGROUP_ROWS = 4
SLICES = ROWS // REGROUP_ROWS

FLOPS = 2 * IMAGES * PIXELS * CHANNELS * TAPS * FEATURES


def tile_capsulelayer_t_kernel(tc, image, weight, bias, out):
    nc = tc.nc
    with ExitStack() as ctx:
        ctx.enter_context(tc.manual_schedule())
        consts = ctx.enter_context(tc.tile_pool(name="consts", bufs=1))
        images = ctx.enter_context(tc.tile_pool(name="images", bufs=ROWS // LOAD_ROWS))

        x_grouped = consts.tile([P, ROWS, COLS, PACK], BF16, align_bytes=64)
        x_sets = []
        for number in range(2):
            codes = [consts.tile([P, COLS + PIXELS + COLS], U32, name="x_codes%d_%d" % (number, j), align_bytes=64) for j in range(KS)]
            centre = [consts.tile([P, PIXELS], U8, name="x_centre%d_%d" % (number, j), align_bytes=64) for j in range(KS)]
            offset = [consts.tile([P, COLS + PIXELS + COLS], U8, name="x_offset%d_%d" % (number, j), align_bytes=64) for j in range(KS)]
            x_sets.append((codes, centre, offset))

        def clear_planes(number):
            codes, centre, offset = x_sets[number]
            for j in (1, 0, 2):
                nc.gpsimd.memset(centre[j][:].bitcast(F32), 0.0)
                nc.gpsimd.memset(codes[j][:].bitcast(F32), 0.0)
                nc.gpsimd.memset(offset[j][:].bitcast(F32), 0.0)

        clear_planes(0)
        ident = consts.tile([P, P], F32)
        make_identity(nc, ident[:])

        raws = {}

        def load_rows(b, part):
            x_raw = images.tile([P, PACK, LOAD_ROWS, COLS], BF16)
            raws[b, part] = x_raw
            rows = slice(part * LOAD_ROWS, (part + 1) * LOAD_ROWS)
            nc.sync.dma_start(out=x_raw[:], in_=image[b].rearrange("(p r) h w -> p r h w", r=PACK)[:, :, rows, :])

        def regroup_rows(copy, b, row0, n_rows):
            part, first = divmod(row0, LOAD_ROWS)
            copy(
                out=x_grouped[:, row0 : row0 + n_rows, :, :],
                in_=raws[b, part][:, :, first : first + n_rows, :].rearrange("p r h w -> p h w r"),
            )

        def quantise_image(b):
            codes, centre, offset = x_sets[b % 2]
            nc.vector.quantize_mx(
                out=codes[1][:, COLS : COLS + PIXELS].bitcast(FP8X4),
                scales=centre[1][:],
                in_=x_grouped[:].rearrange("p h w r -> p (h w r)"),
            )

        def columns(ap, lo, hi):
            return ap.rearrange("p (h w) -> p h w", w=COLS)[:, :, lo:hi]

        def shift_columns(b, j):
            codes, centre, offset = x_sets[b % 2]
            shift = j - 1
            to_lo, to_hi = max(0, -shift), COLS - max(0, shift)
            words = [c[:, COLS : COLS + PIXELS].bitcast(I32) for c in codes]
            to, source = columns(words[j], to_lo, to_hi), columns(words[1], to_lo + shift, to_hi + shift)
            if b == 0:
                nc.vector.tensor_copy(out=to, in_=source)
            else:
                nc.sync.dma_start(out=to, in_=source)
            nc.vector.tensor_copy(
                out=columns(centre[j][:], to_lo, to_hi), in_=columns(centre[1][:], to_lo + shift, to_hi + shift)
            )

        def offset_rows(b, j):
            codes, centre, offset = x_sets[b % 2]
            to, source = offset[j][:, COLS : COLS + PIXELS].bitcast(I32), centre[j][:].bitcast(I32)
            if b == 0:
                nc.vector.tensor_copy(out=to, in_=source)
            else:
                nc.sync.dma_start(out=to, in_=source)

        def x_window(group, t):
            i, j = divmod(t, KS)
            b, part = divmod(group, GROUPS_PER_IMAGE)
            codes, centre, offset = x_sets[b % 2]
            start = COLS * (GROUP_ROWS * part + i)
            words = codes[j][:, start : start + GROUP_PIXELS].bitcast(FP8X4)
            if i == 1:
                scales = centre[j][:, start - COLS : start - COLS + GROUP_PIXELS]
            else:
                scales = offset[j][:, start : start + GROUP_PIXELS]
            return words, scales

        w_codes = consts.tile([P, W_PLACES, FEATURES], U32, align_bytes=64)
        w_scales = consts.tile([P, W_PLACES, FEATURES], U8, align_bytes=64)
        bias_bf = consts.tile([P, TAPS * HALVES], BF16)
        w_rows = weight.rearrange("a b c i j (p r) n -> p (a b c i j) r n", r=PACK)
        with tc.tile_pool(name="stage", bufs=1) as stage:
            w_raws = {}
            for t in (REF,) + OTHERS:
                w_raw = stage.tile([P, PACK, FEATURES], BF16, bufs=TAPS)
                nc.sync.dma_start(out=w_raw[:], in_=w_rows[:, t, :, :])
                w_raws[t] = w_raw
                if t == REF:
                    load_rows(0, 0)
                if t == OTHERS[0]:
                    load_rows(0, 1)
                    with nc.allow_non_contiguous_dma(reason="2304 bias values, one to a partition, once"):
                        nc.sync.dma_start(out=bias_bf[:], in_=bias.rearrange("a b c i j o (g f) -> f (a b c i j o g)", g=HALVES))
            w_groupeds = []
            for t in range(W_PLACES):
                w_grouped = stage.tile([P, FEATURES, PACK], BF16, align_bytes=64, bufs=W_PLACES)
                w_groupeds.append(w_grouped)

            def regroup_weights(copy, t):
                copy(out=w_groupeds[t][:], in_=w_raws[t][:].rearrange("p r n -> p n r"))

            def quantise_weights(t):
                nc.vector.quantize_mx(
                    out=w_codes[:, t, :].bitcast(FP8X4),
                    scales=w_scales[:, t, :],
                    in_=w_groupeds[t][:].rearrange("p n r -> p (n r)"),
                )

            regroup_weights(nc.vector.tensor_copy, REF)
            nc.vector.tensor_scalar_mul(out=w_groupeds[NEG_REF][:], in0=w_groupeds[REF][:], scalar1=-1.0)
            for k in (0, 1, 3, 5):
                regroup_weights(nc.scalar.copy, OTHERS[k])
            regroup_rows(nc.vector.tensor_copy, 0, 0, LOAD_ROWS)
            load_rows(1, 0)
            quantise_weights(NEG_REF)
            regroup_rows(nc.vector.tensor_copy, 0, LOAD_ROWS, LOAD_ROWS)
            load_rows(1, 1)
            quantise_image(0)
            quantise_weights(OTHERS[0])
            offset_rows(0, 1)
            quantise_weights(OTHERS[1])
            shift_columns(0, 0)
            regroup_weights(nc.vector.tensor_copy, OTHERS[2])
            quantise_weights(OTHERS[2])
            offset_rows(0, 0)
            quantise_weights(OTHERS[3])
            regroup_weights(nc.vector.tensor_copy, OTHERS[4])
            quantise_weights(OTHERS[4])
            shift_columns(0, 2)
            quantise_weights(OTHERS[5])
            offset_rows(0, 2)
            for k in (6, 7):
                regroup_weights(nc.vector.tensor_copy, OTHERS[k])
                quantise_weights(OTHERS[k])
            nc.vector.tensor_scalar_mul(out=w_groupeds[NEG_REF8][:], in0=w_groupeds[REF][:], scalar1=1.0 - TAPS)
            quantise_weights(NEG_REF8)
            quantise_weights(REF)

        bias_cols = consts.tile([P, TAPS, HALVES], F32)
        nc.gpsimd.tensor_copy(out=bias_cols[:].rearrange("p t g -> p (t g)"), in_=bias_bf[:])
        bias_rel = consts.tile([P, TAPS, HALVES], F32)
        nc.gpsimd.tensor_tensor(
            out=bias_rel[:], in0=bias_cols[:], in1=bias_cols[:, REF : REF + 1, :].to_broadcast([P, TAPS, HALVES]), op=ALU.subtract
        )
        clear_planes(1)
        bias_start = consts.tile([P, HALVES], F32)
        nc.vector.tensor_reduce(out=bias_start[:], in_=bias_rel[:].rearrange("p t g -> p g t"), axis=AXIS_X, op=ALU.add)
        nc.vector.tensor_scalar_mul(out=bias_start[:], in0=bias_start[:], scalar1=-1.0 / TAPS)

        block_pool = ctx.enter_context(tc.tile_pool(name="block", bufs=2 * LIVE))
        group_pool = ctx.enter_context(tc.tile_pool(name="group", bufs=2))
        work_pool = ctx.enter_context(tc.tile_pool(name="work", bufs=4))
        item_pool = ctx.enter_context(tc.tile_pool(name="item", bufs=4))
        groups = {}
        made = {}

        def begin_group(group):
            ref_T = group_pool.tile([P, HALVES, GROUP_PIXELS], F32)
            start_T = group_pool.tile([P, HALVES, GROUP_PIXELS], F32)
            groups[group] = {"ref_T": ref_T, "start_T": start_T, "u_pix": {}, "taps_T": {}}

        def product(group, bank, t, w_place, half, start, stop):
            feats = slice(half * P, (half + 1) * P)
            words, scales = x_window(group, t)
            nc.tensor.matmul_mx(
                out=bank,
                lhsT=w_codes[:, w_place, feats].bitcast(FP8X4),
                lhsT_scale=w_scales[:, w_place, feats],
                rhs=words,
                rhs_scale=scales,
                start=start,
                stop=stop,
            )

        MEAN_TERMS = [(t, t) for t in OTHERS] + [(REF, NEG_REF8)]

        def add_to_mean(pool, banks, group, a, half):
            if a == 0:
                sum_bank = pool.tile([P, GROUP_PIXELS], F32, tag="sum", bufs=banks["sum"])
                made[group, "mean", half] = sum_bank
            product(group, made[group, "mean", half][:], *MEAN_TERMS[a], half, a == 0, a == len(MEAN_TERMS) - 1)

        def end_mean(group, half):
            nc.scalar.activation(
                out=groups[group]["start_T"][:, half, :],
                in_=made[group, "mean", half][:],
                func=ACT.Identity,
                bias=bias_start[:, half : half + 1],
                scale=-1.0 / TAPS,
            )

        def new_bank(pool, banks, unit):
            bank = pool.tile([P, GROUP_PIXELS], F32, tag="made", bufs=banks["made"])
            made[unit] = bank

        def make(group, kind, a, k):
            bank = made[group, kind, a, k]
            if kind == "turn":
                for tt in range(2):
                    for h in range(HALVES):
                        at = HALVES * tt + h
                        if 2 * a + tt < U_TAPS[h]:
                            nc.tensor.transpose(
                                bank[:, at * P : (at + 1) * P], groups[group]["taps_T"][a][:, at, k * P : (k + 1) * P], ident[:]
                            )
            elif kind == "ref":
                product(group, bank[:], REF, REF, k, True, True)
            else:
                product(group, bank[:], REF, NEG_REF, k, True, False)
                product(group, bank[:], OTHERS[a], OTHERS[a], k, False, True)

        def empty(by_vector, dst, src, bias_col):
            if by_vector:
                nc.vector.tensor_scalar_add(out=dst, in0=src, scalar1=bias_col)
            else:
                nc.scalar.activation(out=dst, in_=src, func=ACT.Identity, bias=bias_col)

        def collect(group, kind, a, k, by_vector=False):
            g = groups[group]
            bank = made[group, kind, a, k]
            if kind == "ref":
                empty(by_vector, g["ref_T"][:, k, :], bank[:], bias_cols[:, REF, k : k + 1])
            elif kind == "tap":
                pair, tt = divmod(a, 2)
                if pair not in g["taps_T"]:
                    if pair == T_PAIR:
                        kept_T = group_pool.tile([P, 2 * HALVES, GROUP_PIXELS], F32)
                        g["taps_T"][pair] = kept_T
                    else:
                        taps_T = group_pool.tile([P, 2 * HALVES, GROUP_PIXELS], F32, bufs=PAIRS - 1)
                        g["taps_T"][pair] = taps_T
                t = OTHERS[a]
                empty(by_vector, g["taps_T"][pair][:, HALVES * tt + k, :], bank[:], bias_rel[:, t, k : k + 1])
            else:
                if k not in g["u_pix"]:
                    u = block_pool.tile([P, max(U_TAPS), FEATURES], F32)
                    g["u_pix"][k] = u
                n_columns = sum([P for tt in range(2) for h in range(HALVES) if 2 * a + tt < U_TAPS[h]])
                dst = g["u_pix"][k][:].rearrange("p t f -> p (t f)")[:, 2 * a * FEATURES : 2 * a * FEATURES + n_columns]
                if by_vector:
                    nc.vector.tensor_copy(out=dst, in_=bank[:, 0:n_columns])
                else:
                    nc.scalar.copy(out=dst, in_=bank[:, 0:n_columns])

        TURN_PAIRS = [pair for pair in range(PAIRS) if 2 * pair < max(U_TAPS)]
        TAP_UNITS = [("tap", a, h) for a in range(N_OTHERS) for h in range(HALVES)]
        TURN_UNITS = [("turn", pair, j) for pair in TURN_PAIRS for j in range(LIVE)]
        REF_UNITS = [("ref", 0, h) for h in range(HALVES)]

        begin_group(0)
        HEAD_BLOCKS = 4
        order = []
        for a in range(N_OTHERS):
            order += [(0, "tap", a, h) for h in range(HALVES)]
            if a >= 2 and a % 2 == 0:
                order += [(0, "turn", (a - 2) // 2, j) for j in range(HEAD_BLOCKS)]
        LAG = 2

        with tc.psum_pool(name="early", bufs=1) as early:
            for k, unit in enumerate(order):
                new_bank(early, EARLY_BANKS, unit)
                make(*unit)
                if unit[1] == "tap":
                    add_to_mean(early, EARLY_BANKS, 0, unit[2], unit[3])
                if k >= LAG:
                    collect(*order[k - LAG], by_vector=(k > 8 and k % 2 == 1))
            for h in range(HALVES):
                add_to_mean(early, EARLY_BANKS, 0, N_OTHERS, h)
            for k in range(LAG):
                collect(*order[k - LAG], by_vector=(k == 0))
            last = [(0, "turn", T_PAIR, j) for j in range(HEAD_BLOCKS) if T_PAIR in TURN_PAIRS]
            for unit in last:
                new_bank(early, EARLY_BANKS, unit)
                make(*unit)
            for h in range(HALVES):
                end_mean(0, h)
            for unit in last:
                collect(*unit, by_vector=True)
            for h in range(HALVES):
                unit = (0, "ref", 0, h)
                new_bank(early, EARLY_BANKS, unit)
                make(*unit)
                collect(*unit)
        psum = ctx.enter_context(tc.psum_pool(name="psum", bufs=1))

        items = {}
        turned_at = {}

        def item(n):
            if n < 0 or n >= N_ITEMS:
                return None
            group, rest = divmod(n, GROUP_STEPS)
            it, rest = divmod(rest, TURN)
            j, half = divmod(rest, HALVES)
            return group, it, j, half, slice(half * P, (half + 1) * P), slice(j * P, (j + 1) * P)

        def first_multiplied(s):
            return 1 + T_SUBS[s % HALVES]

        def turn(s):
            turned = psum.tile([P, TURNED_PLACES, P], F32, tag="turned", bufs=2)
            turned_at[s] = turned
            at_multiplied = first_multiplied(s)
            if item(s):
                group, it, j, half, feats, pixels = item(s)
                if it == 0:
                    minus_o = groups[group]["start_T"][:, half, pixels]
                else:
                    minus_o = items[s - TURN]["total_T"][:]
                n_subs = T_SUBS[half]
                for k in range(n_subs):
                    u_T = groups[group]["taps_T"][T_PAIR][:, HALVES * (2 - n_subs + k) + half, pixels]
                    nc.tensor.matmul(turned[:, k, :], lhsT=u_T, rhs=ident[:], is_transpose=True, start=True, stop=False)
                    nc.tensor.matmul(turned[:, k, :], lhsT=minus_o, rhs=ident[:], is_transpose=True, start=False, stop=True)
                nc.tensor.transpose(turned[:, n_subs, :], minus_o, ident[:])
                items[s] = {}
            if item(s - 5):
                group, it, j, half, feats, pixels = item(s - 5)
                for k in range(G_TAPS[half], N_OTHERS):
                    u_T = groups[group]["taps_T"][T_PAIR][:, HALVES * (k - 2 * T_PAIR) + half, pixels]
                    nc.tensor.transpose(turned[:, at_multiplied + k - G_TAPS[half], :], u_T, ident[:])

        def subtract(n):
            group, it, j, half, feats, pixels = item(n)
            d = work_pool.tile([P, TAPS, P], F32)
            items[n]["d"] = d
            v_subs = N_OTHERS - T_SUBS[half]
            nc.vector.tensor_tensor(
                out=d[:, 0:v_subs, :],
                in0=groups[group]["u_pix"][j][:, 0:v_subs, feats],
                in1=turned_at[n][:, T_SUBS[half], :].unsqueeze(1).to_broadcast([P, v_subs, P]),
                op=ALU.add,
            )

        def square_turned(n):
            group, it, j, half, feats, pixels = item(n)
            n_turned = T_SUBS[half] + 1
            nc.scalar.activation(
                out=items[n]["d"][:, TAPS - n_turned : TAPS, :], in_=turned_at[n][:, 0:n_turned, :], func=ACT.Square
            )

        def square(n):
            group, it, j, half, feats, pixels = item(n)
            diff = items[n]["d"][:, 0 : N_OTHERS - T_SUBS[half], :]
            nc.scalar.activation(out=diff, in_=diff, func=ACT.Square)

        def sum_channels(n):
            dist = item_pool.tile([P, TAPS, HALF_CAPS], F32)
            items[n]["dist"] = dist
            nc.vector.tensor_reduce(
                out=dist[:], in_=items[n]["d"][:].rearrange("p t (c k) -> p t c k", k=CAP_CH), axis=AXIS_X, op=ALU.add
            )

        def inverse_root(n):
            cw = item_pool.tile([P, TAPS, HALF_CAPS], F32)
            items[n]["cw"] = cw
            nc.scalar.activation(out=cw[:], in_=items[n]["dist"][:], func=ACT.Abs_reciprocal_sqrt, bias=EPS)

        def sum_weights(n):
            cw_sum = item_pool.tile([P, HALF_CAPS], F32)
            items[n]["cw_sum"] = cw_sum
            nc.vector.tensor_reduce(out=cw_sum[:], in_=items[n]["cw"][:].rearrange("p t c -> p c t"), axis=AXIS_X, op=ALU.add)

        def invert_sum(n):
            cw_inv = item_pool.tile([P, HALF_CAPS], F32)
            items[n]["cw_inv"] = cw_inv
            nc.vector.reciprocal(out=cw_inv[:], in_=items[n]["cw_sum"][:])

        def normalise(n):
            share = item_pool.tile([P, N_OTHERS, HALF_CAPS], F32)
            items[n]["share"] = share
            nc.gpsimd.tensor_tensor(
                out=share[:],
                in0=items[n]["cw"][:, 0:N_OTHERS, :],
                in1=items[n]["cw_inv"][:].unsqueeze(1).to_broadcast([P, N_OTHERS, HALF_CAPS]),
                op=ALU.mult,
            )
            weighted = work_pool.tile([P, N_OTHERS, P], F32)
            items[n]["weighted"] = weighted

        def multiply(engine, n, taps, n_taps, priors):
            engine.tensor_tensor(
                out=items[n]["weighted"][:, taps, :].rearrange("p t (c k) -> p t c k", k=CAP_CH),
                in0=priors.rearrange("p t (c k) -> p t c k", k=CAP_CH),
                in1=items[n]["share"][:, taps, :].unsqueeze(3).to_broadcast([P, n_taps, HALF_CAPS, CAP_CH]),
                op=ALU.mult,
            )

        def sum_taps(n):
            total = psum.tile([P, P], F32, tag="total", bufs=2)
            items[n]["total"] = total
            for k in range(N_OTHERS):
                nc.tensor.matmul(
                    total[:],
                    lhsT=items[n]["weighted"][:, k, :],
                    rhs=ident[:],
                    is_transpose=True,
                    start=(k == 0),
                    stop=(k == N_OTHERS - 1),
                )

        def keep_total(n):
            total_T = item_pool.tile([P, P], F32)
            nc.scalar.mul(out=total_T[:], in_=items[n]["total"][:], mul=-1.0)
            items[n]["total_T"] = total_T

        def leave(n):
            group, it, j, half, feats, pixels = item(n)
            out_sb = item_pool.tile([P, P], F32)
            nc.vector.tensor_tensor(
                out=out_sb[:], in0=items[n]["total"][:], in1=groups[group]["ref_T"][:, half, pixels], op=ALU.add
            )
            b, part = divmod(group, GROUPS_PER_IMAGE)
            first = GROUP_PIXELS * part + j * P
            nc.sync.dma_start(
                out=out[b].rearrange("(g f) h w -> f g (h w)", g=HALVES)[:, half, first : first + P], in_=out_sb[:]
            )

        plan = {}
        mean_plan = {}
        PASSES = {"tap": 2, "ref": 1, "turn": 0}

        def put(s, unit, by_vector=False):
            plan.setdefault(s, []).append((unit, by_vector))

        late_units = [(0, "turn", pair, j) for j in range(HEAD_BLOCKS, LIVE) for pair in TURN_PAIRS]
        for k, unit in enumerate(late_units):
            put(k // 2, unit, by_vector=(k % 2 == 0))
        units = TAP_UNITS[: 4 * HALVES]
        for k in range(4 * HALVES, len(TAP_UNITS)):
            units = units + [TURN_UNITS[k - 4 * HALVES], TAP_UNITS[k]]
        units = units + REF_UNITS + TURN_UNITS[len(TAP_UNITS) - 4 * HALVES :]
        for group in range(1, N_GROUPS):
            start = GROUP_STEPS * (group - 1)
            first = 0 if group == 1 else 0
            for k, unit in enumerate(units):
                put(start + first + (GROUP_STEPS - first) * k // len(units), (group,) + unit)
            s = start + first
            for half in range(HALVES):
                terms = list(range(len(MEAN_TERMS)))
                while terms:
                    passes = sum([PASSES[unit[1]] for unit, by_vector in plan.get(s, [])])
                    n_terms = min(max(BURST - passes, 0), len(terms))
                    mean_plan[s] = [(group, a, half) for a in terms[:n_terms]]
                    terms = terms[n_terms:]
                    s += 1
                s += 1

        def prepare(s):
            mine = [unit for unit, by_vector in plan.get(s, [])]
            terms = mean_plan.get(s, [])
            for unit in mine:
                if unit[0] not in groups:
                    begin_group(unit[0])
                new_bank(psum, BANKS, unit)
            spare = BURST - len(terms) - sum([PASSES[unit[1]] for unit in mine])
            if mine and s < N_ITEMS - GROUP_STEPS:
                for n in range(spare):
                    product(mine[0][0], made[mine[0]][:], REF, REF, 0, True, True)
            for term in terms:
                add_to_mean(psum, BANKS, *term)
            for unit in mine:
                if unit[1] != "turn":
                    make(*unit)
            for unit in mine:
                if unit[1] == "turn":
                    make(*unit)

        def collect_made(s, number):
            if number == 0:
                for group, a, half in mean_plan.get(s, []):
                    if a == len(MEAN_TERMS) - 1:
                        end_mean(group, half)
            for unit, by_vector in plan.get(s, [])[:1] if number == 0 else plan.get(s, [])[1:]:
                if not by_vector:
                    collect(*unit)

        def collect_by_vector(s):
            for unit, by_vector in plan.get(s, []):
                if by_vector:
                    collect(*unit, by_vector=True)

        slices_at = {}
        image_work = {}
        for b in range(1, IMAGES):
            ready = GROUP_STEPS * GROUPS_PER_IMAGE * (b - 1) + GROUP_STEPS // 2
            for number in range(2 * KS):
                image_work[ready + 2 * number - 2] = (b, number)
            for number in range(SLICES):
                if b > 1:
                    slices_at[ready - 4 - 2 * (SLICES - 1 - number)] = (b, number)

        def work_on_image(b, number):
            if number == 0:
                quantise_image(b)
            elif number == 1:
                offset_rows(b, 1)
            elif number % 2 == 0:
                shift_columns(b, number - 2)
            else:
                offset_rows(b, number - 3)

        turn(0)
        for s in range(N_ITEMS + 6):
            if item(s - 6):
                sum_taps(s - 6)
            if item(s - 3):
                inverse_root(s - 3)
            if item(s - 1):
                square_turned(s - 1)
                square(s - 1)
            collect_made(s - 1, 0)
            prepare(s)
            turn(s + 1)
            if item(s - 2):
                sum_channels(s - 2)
            if item(s - 5):
                group, it, j, half, feats, pixels = item(s - 5)
                n_taps = N_OTHERS - G_TAPS[half]
                at = first_multiplied(s)
                priors = turned_at[s][:, at : at + n_taps, :]
                multiply(nc.vector, s - 5, slice(G_TAPS[half], N_OTHERS), n_taps, priors)
            if item(s - 3):
                sum_weights(s - 3)
            if item(s):
                subtract(s)
            if item(s - 3):
                invert_sum(s - 3)
                normalise(s - 3)
                group, it, j, half, feats, pixels = item(s - 3)
                n_taps = G_TAPS[half]
                multiply(nc.gpsimd, s - 3, slice(0, n_taps), n_taps, groups[group]["u_pix"][j][:, 0:n_taps, feats])
            collect_by_vector(s - 1)
            ends = item(s - 6)
            if ends and ends[1] < ITERATIONS - 1:
                keep_total(s - 6)
            elif ends:
                leave(s - 6)
            collect_made(s - 1, 1)
            if s in image_work:
                work_on_image(*image_work[s])
            if s in slices_at:
                b, number = slices_at[s]
                regroup_rows(nc.scalar.copy, b, REGROUP_ROWS * number, REGROUP_ROWS)
                if number == SLICES - 1 and b + 1 < IMAGES:
                    load_rows(b + 1, 0)
                    load_rows(b + 1, 1)
            if s == 1:
                for part in range(ROWS // LOAD_ROWS):
                    regroup_rows(nc.vector.tensor_copy, 1, part * LOAD_ROWS, LOAD_ROWS)
                    load_rows(2, part)
